import numpy as np
import ml_dtypes


def mxq(x, axis, fmt="e4m3"):
    dtype, down = {"e4m3": (ml_dtypes.float8_e4m3fn, 7), "e5m2": (ml_dtypes.float8_e5m2, 14)}[fmt]
    v = np.moveaxis(np.asarray(x, np.float32).astype(ml_dtypes.bfloat16).astype(np.float64), axis, -1)
    blocks = v.reshape(v.shape[:-1] + (-1, 32))
    amax = np.abs(blocks).max(-1, keepdims=True)
    byte = np.maximum(np.where(amax > 0, np.frexp(amax)[1] - 1 + 127, 0) - down, 1)
    scale = np.exp2(byte - 127.0)
    codes = (blocks / scale).astype(np.float32).astype(dtype).astype(np.float64)
    return np.moveaxis((codes * scale).reshape(v.shape), -1, axis)


WIDE = False


def mx_kscale(k, group=512):
    if not WIDE:
        return np.ones(k)
    levels = np.array([20, -20, 10, -10, 0])
    if group != 512:
        return np.exp2(np.random.permutation(np.resize(levels, k // group))).repeat(group)
    a = np.random.permutation(np.resize(levels, k // 512 * 4)).reshape(k // 512, 4)
    idx = np.arange(k)
    return np.exp2(a[idx // 512, idx % 128 // 32])


BF16 = ml_dtypes.bfloat16


def bf(x):
    return np.asarray(x, np.float32).astype(BF16)


def f64(x):
    return np.asarray(x).astype(np.float64)


B, N, D, C, H, NS = 2, 1024, 1024, 1024, 16, 10
HD = C // H
T = B * N
D4 = (0.4829629131445341, 0.8365163037378079, 0.2241438680420134, -0.1294095225512604)


def scale_weights(scale_gain):
    g = np.exp(scale_gain - scale_gain.max(0, keepdims=True))
    return g / g.sum(0, keepdims=True)


def filter_adjoint(g_c, scale_gain):
    gains_exp = np.repeat(scale_weights(scale_gain), HD, axis=1)
    acc = np.zeros_like(g_c)
    for j in range(NS):
        d = 2 ** j
        gp = np.pad(g_c, ((0, 0), (0, 0), (0, 3 * d)))
        y = (D4[3] * gp[:, :, 0 * d:0 * d + N]
             + D4[2] * gp[:, :, 1 * d:1 * d + N]
             + D4[1] * gp[:, :, 2 * d:2 * d + N]
             + D4[0] * gp[:, :, 3 * d:3 * d + N])
        acc = acc + gains_exp[j][None, :, None] * y
    return acc


def setup_inputs():
    s = mx_kscale(T, group=N).reshape(B, N)[:, :1, None]
    x0 = bf(np.random.standard_normal((B, N, D)))
    k_w = bf(np.random.standard_normal((C, D)) / np.sqrt(D))
    k_b = bf(np.random.standard_normal(C) * 0.2)
    v_w = bf(np.random.standard_normal((C, D)) / np.sqrt(D))
    v_b = bf(np.random.standard_normal(C) * 0.2)
    scale_gain = bf(np.random.standard_normal((NS, H)) * 0.5)
    g = bf(np.random.standard_normal((B, C, N)) * np.exp2(np.random.randint(-12, 1, (B, 1, N))) * 0.25 / s)
    k = (f64(x0) @ f64(k_w).T + f64(k_b)).reshape(B, N, H, HD)
    k_mag = np.sqrt((k * k).sum(-1))
    return {"x": bf(f64(x0) * s), "k_w": k_w, "k_b": k_b, "v_w": v_w, "v_b": v_b, "scale_gain": scale_gain,
            "k_mag": np.asarray(k_mag, np.float32), "grad_out": g}


def reference(x, k_w, k_b, v_w, v_b, scale_gain, k_mag, grad_out):
    a = filter_adjoint(f64(grad_out), f64(scale_gain))
    m = np.repeat(f64(k_mag).transpose(0, 2, 1), HD, axis=1)
    dv = (a * m).transpose(1, 0, 2).reshape(C, T)
    x2 = f64(x).reshape(T, D)
    return mxq(dv, 1, "e5m2") @ mxq(x2, 0, "e4m3")

@@ -1,0 +1,181 @@
+from contextlib import ExitStack
+
+import concourse.mybir as mybir
+from concourse.masks import make_identity
+
+F32 = mybir.dt.float32
+BF16 = mybir.dt.bfloat16
+U32 = mybir.dt.uint32
+U8 = mybir.dt.uint8
+E4M3X4 = mybir.dt.float8_e4m3fn_x4
+E5M2X4 = mybir.dt.float8_e5m2_x4
+ALU = mybir.AluOpType
+ACT = mybir.ActivationFunctionType
+AXIS = mybir.AxisListType
+
+P = 128
+PACK = 4
+K_PASS = P * PACK
+BATCH, TOKENS, WIDTH, CHANNELS, HEADS, SCALES = 2, 1024, 1024, 1024, 16, 10
+HEAD_DIM = CHANNELS // HEADS
+PASSES = BATCH * TOKENS // K_PASS
+PASSES_PER_BATCH = TOKENS // K_PASS
+N_TILE = 512
+ZERO_PAD = 16
+TAP0, TAP1, TAP2, TAP3 = 0.4829629131445341, 0.8365163037378079, 0.2241438680420134, -0.1294095225512604
+
+FLOPS = 2 * CHANNELS * BATCH * TOKENS * WIDTH + 2 * 20 * CHANNELS * BATCH * TOKENS
+BYTES = 2 * 2 * BATCH * TOKENS * WIDTH + 4 * BATCH * TOKENS * HEADS + 2 * SCALES * HEADS + 4 * CHANNELS * WIDTH
+
+
+def tile_causalwaveletfieldattentionbyte_pa_v_kernel(
+    tc, x, k_w, k_b, v_w, v_b, scale_gain, k_mag, grad_out, out
+):
+    nc = tc.nc
+    with ExitStack() as ctx:
+        keep = ctx.enter_context(tc.tile_pool(name="keep", bufs=1))
+        sums = ctx.enter_context(tc.tile_pool(name="sums", bufs=4))
+        stage = ctx.enter_context(tc.tile_pool(name="stage", bufs=2))
+        psum_t = ctx.enter_context(tc.psum_pool(name="psum_t", bufs=4))
+        psum_o = ctx.enter_context(tc.psum_pool(name="psum_o", bufs=4))
+
+        logits_bf = keep.tile([P, SCALES * HEADS], BF16)
+        nc.sync.dma_start(out=logits_bf[:], in_=scale_gain.rearrange("j h -> (j h)").partition_broadcast(P))
+
+        grad = keep.tile([P, HEADS, TOKENS + ZERO_PAD], BF16)
+        nc.vector.memset(grad[:, :, TOKENS:], 0.0)
+
+        def load_head(h):
+            for b in range(BATCH):
+                nc.sync.dma_start(
+                    out=grad[b * HEAD_DIM : (b + 1) * HEAD_DIM, h, 0:TOKENS],
+                    in_=grad_out[b, h * HEAD_DIM : (h + 1) * HEAD_DIM, :],
+                )
+
+        load_head(0)
+        load_head(1)
+        kmag = keep.tile([P, PASSES * PACK, HEADS], F32)
+        nc.sync.dma_start(out=kmag[:], in_=k_mag.rearrange("b (i p) h -> p (b i) h", p=P))
+        x_raw = keep.tile([P, PASSES, PACK, WIDTH], BF16)
+        x_rows = x.rearrange("b (g t p) i -> (b g) p t i", t=PACK, p=P)
+        for s in range(PASSES):
+            nc.sync.dma_start(out=x_raw[:, s, :, :], in_=x_rows[s])
+        for h in range(2, HEADS):
+            load_head(h)
+
+        identity = keep.tile([P, P], F32)
+        make_identity(nc, identity[:])
+
+        logits = keep.tile([P, SCALES, HEADS], F32)
+        nc.vector.tensor_copy(out=logits[:].rearrange("p j h -> p (j h)"), in_=logits_bf[:])
+        top = keep.tile([P, HEADS], F32)
+        nc.vector.tensor_reduce(out=top[:], in_=logits[:].rearrange("p j h -> p h j"), axis=AXIS.X, op=ALU.max)
+        nc.vector.tensor_tensor(
+            out=logits[:], in0=logits[:], in1=top[:].unsqueeze(1).to_broadcast([P, SCALES, HEADS]), op=ALU.subtract
+        )
+        grown = keep.tile([P, SCALES, HEADS], F32)
+        nc.scalar.activation(out=grown[:], in_=logits[:], func=ACT.Exp)
+        total = keep.tile([P, HEADS], F32)
+        nc.vector.tensor_reduce(out=total[:], in_=grown[:].rearrange("p j h -> p h j"), axis=AXIS.X, op=ALU.add)
+        inverse = keep.tile([P, HEADS], F32)
+        nc.vector.reciprocal(out=inverse[:], in_=total[:])
+        gain = keep.tile([P, SCALES, HEADS], F32)
+        nc.vector.tensor_tensor(
+            out=gain[:], in0=grown[:], in1=inverse[:].unsqueeze(1).to_broadcast([P, SCALES, HEADS]), op=ALU.mult
+        )
+
+        w_pow = keep.tile([P, SCALES, HEADS], F32)
+        nc.vector.tensor_scalar_mul(out=w_pow[:], in0=gain[:], scalar1=TAP2)
+        nc.vector.scalar_tensor_tensor(
+            out=w_pow[:, 1:, :], in0=gain[:, : SCALES - 1, :], scalar=TAP1, in1=w_pow[:, 1:, :],
+            op0=ALU.mult, op1=ALU.add,
+        )
+        w_tri = keep.tile([P, SCALES, HEADS], F32)
+        nc.vector.tensor_scalar_mul(out=w_tri[:], in0=gain[:], scalar1=TAP0)
+
+        taps = [(2**m, w_pow, m) for m in range(1, SCALES)]
+        taps += [(3 * 2**j, w_tri, j) for j in range(SCALES) if 3 * 2**j < TOKENS]
+        taps = sorted(taps, key=lambda tap: tap[0])
+
+        x_codes = keep.tile([P, PASSES, WIDTH], U32, align_bytes=64)
+        x_scales = keep.tile([P, PASSES, WIDTH], U8, align_bytes=64)
+
+        def quantise_x(s):
+            x_grouped = stage.tile([P, WIDTH, PACK], BF16, align_bytes=64)
+            nc.scalar.copy(
+                out=x_grouped[:].rearrange("p (c i) t -> p c t i", i=4),
+                in_=x_raw[:, s, :, :].rearrange("p t (c i) -> p c t i", i=4),
+            )
+            nc.vector.quantize_mx(
+                out=x_codes[:, s, :].bitcast(E4M3X4),
+                scales=x_scales[:, s, :],
+                in_=x_grouped[:].rearrange("p c t -> p (c t)"),
+            )
+
+        def add_tap(acc, h, offset, weight):
+            count = TOKENS if offset <= ZERO_PAD else TOKENS - offset
+            nc.vector.scalar_tensor_tensor(
+                out=acc[:, 0:count], in0=grad[:, h, offset : offset + count], scalar=weight, in1=acc[:, 0:count],
+                op0=ALU.mult, op1=ALU.add,
+            )
+
+        for pair in range(HEADS // 2):
+            heads = (2 * pair, 2 * pair + 1)
+            accs = []
+            for h in heads:
+                acc = sums.tile([P, TOKENS], F32, name="acc")
+                nc.scalar.activation(
+                    out=acc[:], in_=grad[:, h, 1 : TOKENS + 1], func=ACT.Copy, scale=w_pow[:, 0, h : h + 1]
+                )
+                accs.append(acc)
+            for acc, h in zip(accs, heads):
+                add_tap(acc, h, 0, TAP3)
+            for offset, table, row in taps:
+                for acc, h in zip(accs, heads):
+                    add_tap(acc, h, offset, table[:, row, h : h + 1])
+
+            if pair == 0:
+                for s in range(PASSES):
+                    quantise_x(s)
+
+            dv_grouped = stage.tile([P, PASSES, P, PACK], BF16, align_bytes=64)
+            for side, (acc, h) in enumerate(zip(accs, heads)):
+                for g in range(PASSES_PER_BATCH):
+                    turned = psum_t.tile([P, PACK, P], F32)
+                    for t in range(PACK):
+                        first = g * K_PASS + t * P
+                        nc.tensor.transpose(turned[:, t, :], acc[:, first : first + P], identity[:])
+                    for b in range(BATCH):
+                        s = b * PASSES_PER_BATCH + g
+                        for t in range(PACK):
+                            nc.scalar.activation(
+                                out=dv_grouped[:, s, side * HEAD_DIM : (side + 1) * HEAD_DIM, t],
+                                in_=turned[:, t, b * HEAD_DIM : (b + 1) * HEAD_DIM],
+                                func=ACT.Copy,
+                                scale=kmag[:, s * PACK + t, h : h + 1],
+                            )
+
+            dv_codes = stage.tile([P, PASSES * P], U32, align_bytes=64)
+            dv_scales = stage.tile([P, PASSES * P], U8, align_bytes=64)
+            nc.vector.quantize_mx(
+                out=dv_codes[:].bitcast(E5M2X4),
+                scales=dv_scales[:],
+                in_=dv_grouped[:].rearrange("p s c t -> p (s c t)"),
+            )
+
+            result = stage.tile([P, WIDTH], F32)
+            for half in range(WIDTH // N_TILE):
+                cols = slice(half * N_TILE, (half + 1) * N_TILE)
+                product = psum_o.tile([P, N_TILE], F32)
+                for s in range(PASSES):
+                    nc.tensor.matmul_mx(
+                        out=product[:],
+                        lhsT=dv_codes[:, s * P : (s + 1) * P].bitcast(E5M2X4),
+                        lhsT_scale=dv_scales[:, s * P : (s + 1) * P],
+                        rhs=x_codes[:, s, cols].bitcast(E4M3X4),
+                        rhs_scale=x_scales[:, s, cols],
+                        start=(s == 0),
+                        stop=(s == PASSES - 1),
+                    )
+                nc.scalar.copy(out=result[:, cols], in_=product[:])
+            nc.sync.dma_start(out=out[pair * P : (pair + 1) * P, :], in_=result[:])

@@ -21,6 +21,12 @@ HEAD_DIM = CHANNELS // HEADS
 PASSES = BATCH * TOKENS // K_PASS
 PASSES_PER_BATCH = TOKENS // K_PASS
 N_TILE = 512
+STRIDE = 8
+CLASS_TOKENS = TOKENS // STRIDE
+BAND_COLS = 96
+BAND_TOKENS = STRIDE * BAND_COLS
+BANK_CLASSES = 4
+ROW = 224
 ZERO_PAD = 16
 TAP0, TAP1, TAP2, TAP3 = 0.4829629131445341, 0.8365163037378079, 0.2241438680420134, -0.1294095225512604
 
@@ -34,10 +40,12 @@ def tile_causalwaveletfieldattentionbyte_pa_v_kernel(
     nc = tc.nc
     with ExitStack() as ctx:
         keep = ctx.enter_context(tc.tile_pool(name="keep", bufs=1))
-        sums = ctx.enter_context(tc.tile_pool(name="sums", bufs=4))
+        sums = ctx.enter_context(tc.tile_pool(name="sums", bufs=6))
         stage = ctx.enter_context(tc.tile_pool(name="stage", bufs=2))
-        psum_t = ctx.enter_context(tc.psum_pool(name="psum_t", bufs=4))
-        psum_o = ctx.enter_context(tc.psum_pool(name="psum_o", bufs=4))
+        psum_c = ctx.enter_context(tc.psum_pool(name="psum_c", bufs=1))
+        psum_b = ctx.enter_context(tc.psum_pool(name="psum_b", bufs=4))
+        psum_t = ctx.enter_context(tc.psum_pool(name="psum_t", bufs=2))
+        psum_o = ctx.enter_context(tc.psum_pool(name="psum_o", bufs=1))
 
         logits_bf = keep.tile([P, SCALES * HEADS], BF16)
         nc.sync.dma_start(out=logits_bf[:], in_=scale_gain.rearrange("j h -> (j h)").partition_broadcast(P))
@@ -65,6 +73,10 @@ def tile_causalwaveletfieldattentionbyte_pa_v_kernel(
 
         identity = keep.tile([P, P], F32)
         make_identity(nc, identity[:])
+        identity_bf = keep.tile([P, P], BF16)
+        make_identity(nc, identity_bf[:])
+        rows = keep.tile([P, HEADS + 1, ROW], F32)
+        nc.vector.memset(rows[:], 0.0)
 
         logits = keep.tile([P, SCALES, HEADS], F32)
         nc.vector.tensor_copy(out=logits[:].rearrange("p j h -> p (j h)"), in_=logits_bf[:])
@@ -92,10 +104,29 @@ def tile_causalwaveletfieldattentionbyte_pa_v_kernel(
         )
         w_tri = keep.tile([P, SCALES, HEADS], F32)
         nc.vector.tensor_scalar_mul(out=w_tri[:], in0=gain[:], scalar1=TAP0)
+        w_zero = keep.tile([P, 1, HEADS], F32)
+        nc.vector.tensor_reduce(out=w_zero[:, 0, :], in_=gain[:].rearrange("p j h -> p h j"), axis=AXIS.X, op=ALU.add)
+        nc.vector.tensor_scalar_mul(out=w_zero[:], in0=w_zero[:], scalar1=TAP3)
 
-        taps = [(2**m, w_pow, m) for m in range(1, SCALES)]
+        taps = [(0, w_zero, 0)]
+        taps += [(2**m, w_pow, m) for m in range(SCALES)]
         taps += [(3 * 2**j, w_tri, j) for j in range(SCALES) if 3 * 2**j < TOKENS]
         taps = sorted(taps, key=lambda tap: tap[0])
+        fine_taps = [tap for tap in taps if tap[0] % STRIDE != 0]
+        band_taps = [tap for tap in taps if tap[0] % STRIDE == 0]
+
+        for offset, table, row in band_taps:
+            nc.vector.tensor_copy(out=rows[:, 0:HEADS, CLASS_TOKENS - 1 - offset // STRIDE], in_=table[:, row, :])
+        pitch = (HEADS + 1) * ROW
+        scratch = out.rearrange("c i -> (c i)")
+        nc.gpsimd.dma_start(
+            out=scratch[0 : P * pitch].rearrange("(p w) -> p w", w=pitch), in_=rows[:].rearrange("p h l -> p (h l)")
+        )
+        skewed = scratch[P - 1 : P - 1 + P * (pitch - 1)].rearrange("(p w) -> p w", w=pitch - 1)
+        band = keep.tile([P, HEADS, BAND_COLS], F32)
+        nc.gpsimd.dma_start(
+            out=band[:], in_=skewed[:, 0 : HEADS * ROW].rearrange("p (h l) -> p h l", l=ROW)[:, :, 0:BAND_COLS]
+        )
 
         x_codes = keep.tile([P, PASSES, WIDTH], U32, align_bytes=64)
         x_scales = keep.tile([P, PASSES, WIDTH], U8, align_bytes=64)
@@ -112,31 +143,65 @@ def tile_causalwaveletfieldattentionbyte_pa_v_kernel(
                 in_=x_grouped[:].rearrange("p c t -> p (c t)"),
             )
 
-        def add_tap(acc, h, offset, weight):
-            count = TOKENS if offset <= ZERO_PAD else TOKENS - offset
+        def add_tap(acc, h, offset, weight, first):
+            last = TOKENS if offset <= ZERO_PAD else TOKENS - offset
             nc.vector.scalar_tensor_tensor(
-                out=acc[:, 0:count], in0=grad[:, h, offset : offset + count], scalar=weight, in1=acc[:, 0:count],
-                op0=ALU.mult, op1=ALU.add,
+                out=acc[:, first:last], in0=grad[:, h, first + offset : last + offset], scalar=weight,
+                in1=acc[:, first:last], op0=ALU.mult, op1=ALU.add,
             )
+
+        def first_term(h):
+            offset, table, row = fine_taps[0]
+            acc = sums.tile([P, TOKENS], F32)
+            nc.scalar.activation(
+                out=acc[:], in_=grad[:, h, offset : offset + TOKENS], func=ACT.Copy, scale=table[:, row, h : h + 1]
+            )
+            return acc
+
+        def band_sums(h):
+            classes_ps = psum_c.tile([P, STRIDE, P], BF16)
+            for r in range(STRIDE):
+                nc.tensor.transpose(classes_ps[:, r, :], grad[:, h, r:TOKENS:STRIDE], identity_bf[:])
+            classes = stage.tile([P, STRIDE, P], F32)
+            nc.scalar.copy(out=classes[:], in_=classes_ps[:])
+            banks = []
+            for bank in range(STRIDE // BANK_CLASSES):
+                band_ps = psum_b.tile([P, BANK_CLASSES, BAND_COLS], F32)
+                for r in range(BANK_CLASSES):
+                    nc.tensor.matmul(
+                        out=band_ps[:, r, :], lhsT=classes[:, bank * BANK_CLASSES + r, :], rhs=band[:, h, :],
+                        start=True, stop=True,
+                    )
+                banks.append(band_ps)
+            return banks
+
+        def add_band_sums(acc, banks):
+            by_class = acc[:, 0:BAND_TOKENS].rearrange("p (q r) -> p q r", r=STRIDE)
+            for bank, band_ps in enumerate(banks):
+                part = by_class[:, :, bank * BANK_CLASSES : (bank + 1) * BANK_CLASSES]
+                nc.vector.tensor_tensor(out=part, in0=part, in1=band_ps[:].rearrange("p r q -> p q r"), op=ALU.add)
+
+        next_accs = [first_term(0), first_term(1)]
+        next_banks = [band_sums(0), band_sums(1)]
+        for s in range(PASSES):
+            quantise_x(s)
 
         for pair in range(HEADS // 2):
             heads = (2 * pair, 2 * pair + 1)
-            accs = []
-            for h in heads:
-                acc = sums.tile([P, TOKENS], F32, name="acc")
-                nc.scalar.activation(
-                    out=acc[:], in_=grad[:, h, 1 : TOKENS + 1], func=ACT.Copy, scale=w_pow[:, 0, h : h + 1]
-                )
-                accs.append(acc)
-            for acc, h in zip(accs, heads):
-                add_tap(acc, h, 0, TAP3)
-            for offset, table, row in taps:
+            accs, banks = next_accs, next_banks
+            if pair + 1 < HEADS // 2:
+                next_accs = [first_term(2 * pair + 2), first_term(2 * pair + 3)]
+            for offset, table, row in fine_taps[1:]:
                 for acc, h in zip(accs, heads):
-                    add_tap(acc, h, offset, table[:, row, h : h + 1])
-
-            if pair == 0:
-                for s in range(PASSES):
-                    quantise_x(s)
+                    add_tap(acc, h, offset, table[:, row, h : h + 1], 0)
+            for offset, table, row in band_taps:
+                if BAND_TOKENS + offset < TOKENS:
+                    for acc, h in zip(accs, heads):
+                        add_tap(acc, h, offset, table[:, row, h : h + 1], BAND_TOKENS)
+            for acc, head_banks in zip(accs, banks):
+                add_band_sums(acc, head_banks)
+            if pair + 1 < HEADS // 2:
+                next_banks = [band_sums(2 * pair + 2), band_sums(2 * pair + 3)]
 
             dv_grouped = stage.tile([P, PASSES, P, PACK], BF16, align_bytes=64)
             for side, (acc, h) in enumerate(zip(accs, heads)):

@@ -27,6 +27,7 @@ BAND_COLS = 96
 BAND_TOKENS = STRIDE * BAND_COLS
 BANK_CLASSES = 4
 ROW = 224
+PRODUCT_TAPS = 3
 ZERO_PAD = 16
 TAP0, TAP1, TAP2, TAP3 = 0.4829629131445341, 0.8365163037378079, 0.2241438680420134, -0.1294095225512604
 
@@ -75,8 +76,6 @@ def tile_causalwaveletfieldattentionbyte_pa_v_kernel(
         make_identity(nc, identity[:])
         identity_bf = keep.tile([P, P], BF16)
         make_identity(nc, identity_bf[:])
-        rows = keep.tile([P, HEADS + 1, ROW], F32)
-        nc.vector.memset(rows[:], 0.0)
 
         logits = keep.tile([P, SCALES, HEADS], F32)
         nc.vector.tensor_copy(out=logits[:].rearrange("p j h -> p (j h)"), in_=logits_bf[:])
@@ -115,13 +114,17 @@ def tile_causalwaveletfieldattentionbyte_pa_v_kernel(
         fine_taps = [tap for tap in taps if tap[0] % STRIDE != 0]
         band_taps = [tap for tap in taps if tap[0] % STRIDE == 0]
 
-        for offset, table, row in band_taps:
-            nc.vector.tensor_copy(out=rows[:, 0:HEADS, CLASS_TOKENS - 1 - offset // STRIDE], in_=table[:, row, :])
         pitch = (HEADS + 1) * ROW
         scratch = out.rearrange("c i -> (c i)")
-        nc.gpsimd.dma_start(
-            out=scratch[0 : P * pitch].rearrange("(p w) -> p w", w=pitch), in_=rows[:].rearrange("p h l -> p (h l)")
-        )
+        with tc.tile_pool(name="setup", bufs=1) as setup:
+            rows = setup.tile([P, HEADS + 1, ROW], F32)
+            nc.vector.memset(rows[:], 0.0)
+            for offset, table, row in band_taps:
+                nc.vector.tensor_copy(out=rows[:, 0:HEADS, CLASS_TOKENS - 1 - offset // STRIDE], in_=table[:, row, :])
+            nc.gpsimd.dma_start(
+                out=scratch[0 : P * pitch].rearrange("(p w) -> p w", w=pitch), in_=rows[:].rearrange("p h l -> p (h l)")
+            )
+        terms = ctx.enter_context(tc.tile_pool(name="terms", bufs=6 * PRODUCT_TAPS))
         skewed = scratch[P - 1 : P - 1 + P * (pitch - 1)].rearrange("(p w) -> p w", w=pitch - 1)
         band = keep.tile([P, HEADS, BAND_COLS], F32)
         nc.gpsimd.dma_start(
@@ -150,20 +153,28 @@ def tile_causalwaveletfieldattentionbyte_pa_v_kernel(
                 in1=acc[:, first:last], op0=ALU.mult, op1=ALU.add,
             )
 
-        def first_term(h):
-            offset, table, row = fine_taps[0]
+        def scalar_products(h):
+            parts = []
+            for offset, table, row in fine_taps[:PRODUCT_TAPS]:
+                product = terms.tile([P, TOKENS + ZERO_PAD], F32)
+                nc.scalar.activation(out=product[:], in_=grad[:, h, :], func=ACT.Copy, scale=table[:, row, h : h + 1])
+                parts.append((product, offset))
+            offset, table, row = fine_taps[PRODUCT_TAPS]
             acc = sums.tile([P, TOKENS], F32)
             nc.scalar.activation(
                 out=acc[:], in_=grad[:, h, offset : offset + TOKENS], func=ACT.Copy, scale=table[:, row, h : h + 1]
             )
-            return acc
+            return [(acc, 0)] + parts
 
-        def band_sums(h):
+        def transposed_classes(h):
             classes_ps = psum_c.tile([P, STRIDE, P], BF16)
             for r in range(STRIDE):
                 nc.tensor.transpose(classes_ps[:, r, :], grad[:, h, r:TOKENS:STRIDE], identity_bf[:])
             classes = stage.tile([P, STRIDE, P], F32)
             nc.scalar.copy(out=classes[:], in_=classes_ps[:])
+            return classes
+
+        def band_sums(h, classes):
             banks = []
             for bank in range(STRIDE // BANK_CLASSES):
                 band_ps = psum_b.tile([P, BANK_CLASSES, BAND_COLS], F32)
@@ -181,45 +192,25 @@ def tile_causalwaveletfieldattentionbyte_pa_v_kernel(
                 part = by_class[:, :, bank * BANK_CLASSES : (bank + 1) * BANK_CLASSES]
                 nc.vector.tensor_tensor(out=part, in0=part, in1=band_ps[:].rearrange("p r q -> p q r"), op=ALU.add)
 
-        next_accs = [first_term(0), first_term(1)]
-        next_banks = [band_sums(0), band_sums(1)]
-        for s in range(PASSES):
-            quantise_x(s)
+        def turn_and_scale(h, head_parts, dv_cols):
+            for g in range(PASSES_PER_BATCH):
+                turned = psum_t.tile([P, PACK, P], F32)
+                for t in range(PACK):
+                    first = g * K_PASS + t * P
+                    for i, (part, offset) in enumerate(head_parts):
+                        nc.tensor.matmul(
+                            out=turned[:, t, :], lhsT=part[:, first + offset : first + offset + P], rhs=identity[:],
+                            is_transpose=True, start=(i == 0), stop=(i == len(head_parts) - 1),
+                        )
+                kmag_g = kmag[:, :, h].rearrange("p (b g t) -> p b g t", b=BATCH, t=PACK)[:, :, g, :]
+                nc.vector.tensor_tensor(
+                    out=dv_cols[:, g::PASSES_PER_BATCH, :, :],
+                    in0=turned[:].rearrange("p t (b c) -> p b c t", b=BATCH),
+                    in1=kmag_g.unsqueeze(2).to_broadcast([P, BATCH, HEAD_DIM, PACK]),
+                    op=ALU.mult,
+                )
 
-        for pair in range(HEADS // 2):
-            heads = (2 * pair, 2 * pair + 1)
-            accs, banks = next_accs, next_banks
-            if pair + 1 < HEADS // 2:
-                next_accs = [first_term(2 * pair + 2), first_term(2 * pair + 3)]
-            for offset, table, row in fine_taps[1:]:
-                for acc, h in zip(accs, heads):
-                    add_tap(acc, h, offset, table[:, row, h : h + 1], 0)
-            for offset, table, row in band_taps:
-                if BAND_TOKENS + offset < TOKENS:
-                    for acc, h in zip(accs, heads):
-                        add_tap(acc, h, offset, table[:, row, h : h + 1], BAND_TOKENS)
-            for acc, head_banks in zip(accs, banks):
-                add_band_sums(acc, head_banks)
-            if pair + 1 < HEADS // 2:
-                next_banks = [band_sums(2 * pair + 2), band_sums(2 * pair + 3)]
-
-            dv_grouped = stage.tile([P, PASSES, P, PACK], BF16, align_bytes=64)
-            for side, (acc, h) in enumerate(zip(accs, heads)):
-                for g in range(PASSES_PER_BATCH):
-                    turned = psum_t.tile([P, PACK, P], F32)
-                    for t in range(PACK):
-                        first = g * K_PASS + t * P
-                        nc.tensor.transpose(turned[:, t, :], acc[:, first : first + P], identity[:])
-                    for b in range(BATCH):
-                        s = b * PASSES_PER_BATCH + g
-                        for t in range(PACK):
-                            nc.scalar.activation(
-                                out=dv_grouped[:, s, side * HEAD_DIM : (side + 1) * HEAD_DIM, t],
-                                in_=turned[:, t, b * HEAD_DIM : (b + 1) * HEAD_DIM],
-                                func=ACT.Copy,
-                                scale=kmag[:, s * PACK + t, h : h + 1],
-                            )
-
+        def multiply(pair, dv_grouped):
             dv_codes = stage.tile([P, PASSES * P], U32, align_bytes=64)
             dv_scales = stage.tile([P, PASSES * P], U8, align_bytes=64)
             nc.vector.quantize_mx(
@@ -227,7 +218,6 @@ def tile_causalwaveletfieldattentionbyte_pa_v_kernel(
                 scales=dv_scales[:],
                 in_=dv_grouped[:].rearrange("p s c t -> p (s c t)"),
             )
-
             result = stage.tile([P, WIDTH], F32)
             for half in range(WIDTH // N_TILE):
                 cols = slice(half * N_TILE, (half + 1) * N_TILE)
@@ -244,3 +234,44 @@ def tile_causalwaveletfieldattentionbyte_pa_v_kernel(
                     )
                 nc.scalar.copy(out=result[:, cols], in_=product[:])
             nc.sync.dma_start(out=out[pair * P : (pair + 1) * P, :], in_=result[:])
+
+        def heads_of(pair):
+            return (2 * pair, 2 * pair + 1)
+
+        PAIRS = HEADS // 2
+        parts = {0: [scalar_products(h) for h in heads_of(0)]}
+        banks = {0: [band_sums(h, transposed_classes(h)) for h in heads_of(0)]}
+        for s in range(PASSES):
+            quantise_x(s)
+
+        for pair in range(PAIRS + 1):
+            filtering = pair < PAIRS
+            preparing = pair + 1 < PAIRS
+            finishing = pair >= 1
+            if preparing:
+                parts[pair + 1] = [scalar_products(h) for h in heads_of(pair + 1)]
+            if filtering:
+                accs = [head_parts[0][0] for head_parts in parts[pair]]
+            if finishing:
+                dv_grouped = stage.tile([P, PASSES, P, PACK], BF16, align_bytes=64)
+                turn_and_scale(heads_of(pair - 1)[0], parts[pair - 1][0], dv_grouped[:, :, 0:HEAD_DIM, :])
+            if filtering:
+                for offset, table, row in fine_taps[PRODUCT_TAPS + 1 :]:
+                    for acc, h in zip(accs, heads_of(pair)):
+                        add_tap(acc, h, offset, table[:, row, h : h + 1], 0)
+            if preparing:
+                classes = [transposed_classes(h) for h in heads_of(pair + 1)]
+            if finishing:
+                turn_and_scale(heads_of(pair - 1)[1], parts[pair - 1][1], dv_grouped[:, :, HEAD_DIM:P, :])
+            if filtering:
+                for offset, table, row in band_taps:
+                    if BAND_TOKENS + offset < TOKENS:
+                        for acc, h in zip(accs, heads_of(pair)):
+                            add_tap(acc, h, offset, table[:, row, h : h + 1], BAND_TOKENS)
+            if finishing:
+                multiply(pair - 1, dv_grouped)
+            if filtering:
+                for acc, head_banks in zip(accs, banks[pair]):
+                    add_band_sums(acc, head_banks)
+            if preparing:
+                banks[pair + 1] = [band_sums(h, c) for h, c in zip(heads_of(pair + 1), classes)]

@@ -27,6 +27,7 @@ BAND_COLS = 96
 BAND_TOKENS = STRIDE * BAND_COLS
 BANK_CLASSES = 4
 ROW = 224
+VECTOR_X_PASSES = 2
 PRODUCT_TAPS = 3
 ZERO_PAD = 16
 TAP0, TAP1, TAP2, TAP3 = 0.4829629131445341, 0.8365163037378079, 0.2241438680420134, -0.1294095225512604
@@ -40,9 +41,13 @@ def tile_causalwaveletfieldattentionbyte_pa_v_kernel(
 ):
     nc = tc.nc
     with ExitStack() as ctx:
+        ctx.enter_context(tc.manual_schedule())
         keep = ctx.enter_context(tc.tile_pool(name="keep", bufs=1))
         sums = ctx.enter_context(tc.tile_pool(name="sums", bufs=6))
-        stage = ctx.enter_context(tc.tile_pool(name="stage", bufs=2))
+        terms = ctx.enter_context(tc.tile_pool(name="terms", bufs=5 * PRODUCT_TAPS))
+        early = ctx.enter_context(tc.tile_pool(name="early", bufs=2))
+        late = ctx.enter_context(tc.tile_pool(name="late", bufs=2))
+        codes = ctx.enter_context(tc.tile_pool(name="codes", bufs=3))
         psum_c = ctx.enter_context(tc.psum_pool(name="psum_c", bufs=1))
         psum_b = ctx.enter_context(tc.psum_pool(name="psum_b", bufs=4))
         psum_t = ctx.enter_context(tc.psum_pool(name="psum_t", bufs=2))
@@ -61,21 +66,32 @@ def tile_causalwaveletfieldattentionbyte_pa_v_kernel(
                     in_=grad_out[b, h * HEAD_DIM : (h + 1) * HEAD_DIM, :],
                 )
 
-        load_head(0)
-        load_head(1)
+        for h in range(4):
+            load_head(h)
         kmag = keep.tile([P, PASSES * PACK, HEADS], F32)
         nc.sync.dma_start(out=kmag[:], in_=k_mag.rearrange("b (i p) h -> p (b i) h", p=P))
-        x_raw = keep.tile([P, PASSES, PACK, WIDTH], BF16)
         x_rows = x.rearrange("b (g t p) i -> (b g) p t i", t=PACK, p=P)
-        for s in range(PASSES):
-            nc.sync.dma_start(out=x_raw[:, s, :, :], in_=x_rows[s])
-        for h in range(2, HEADS):
+        x_raw = {}
+
+        def load_x(s):
+            x_raw[s] = early.tile([P, PACK, WIDTH], BF16, name="x_raw")
+            nc.sync.dma_start(out=x_raw[s][:], in_=x_rows[s])
+
+        load_x(0)
+        load_x(1)
+        for h in range(4, 8):
+            load_head(h)
+        load_x(2)
+        load_x(3)
+        for h in range(8, HEADS):
             load_head(h)
 
-        identity = keep.tile([P, P], F32)
-        make_identity(nc, identity[:])
         identity_bf = keep.tile([P, P], BF16)
         make_identity(nc, identity_bf[:])
+        identity = keep.tile([P, P], F32)
+        make_identity(nc, identity[:])
+        rows = keep.tile([P, HEADS + 1, ROW], F32)
+        nc.vector.memset(rows[:], 0.0)
 
         logits = keep.tile([P, SCALES, HEADS], F32)
         nc.vector.tensor_copy(out=logits[:].rearrange("p j h -> p (j h)"), in_=logits_bf[:])
@@ -113,64 +129,64 @@ def tile_causalwaveletfieldattentionbyte_pa_v_kernel(
         taps = sorted(taps, key=lambda tap: tap[0])
         fine_taps = [tap for tap in taps if tap[0] % STRIDE != 0]
         band_taps = [tap for tap in taps if tap[0] % STRIDE == 0]
+        product_taps = fine_taps[:PRODUCT_TAPS]
+        start_tap = fine_taps[PRODUCT_TAPS]
+        vector_taps = fine_taps[PRODUCT_TAPS + 1 :]
+        tail_taps = vector_taps + [tap for tap in band_taps if BAND_TOKENS + tap[0] < TOKENS]
 
-        pitch = (HEADS + 1) * ROW
-        scratch = out.rearrange("c i -> (c i)")
-        with tc.tile_pool(name="setup", bufs=1) as setup:
-            rows = setup.tile([P, HEADS + 1, ROW], F32)
-            nc.vector.memset(rows[:], 0.0)
-            for offset, table, row in band_taps:
-                nc.vector.tensor_copy(out=rows[:, 0:HEADS, CLASS_TOKENS - 1 - offset // STRIDE], in_=table[:, row, :])
-            nc.gpsimd.dma_start(
-                out=scratch[0 : P * pitch].rearrange("(p w) -> p w", w=pitch), in_=rows[:].rearrange("p h l -> p (h l)")
-            )
-        terms = ctx.enter_context(tc.tile_pool(name="terms", bufs=6 * PRODUCT_TAPS))
-        skewed = scratch[P - 1 : P - 1 + P * (pitch - 1)].rearrange("(p w) -> p w", w=pitch - 1)
-        band = keep.tile([P, HEADS, BAND_COLS], F32)
-        nc.gpsimd.dma_start(
-            out=band[:], in_=skewed[:, 0 : HEADS * ROW].rearrange("p (h l) -> p h l", l=ROW)[:, :, 0:BAND_COLS]
-        )
 
         x_codes = keep.tile([P, PASSES, WIDTH], U32, align_bytes=64)
         x_scales = keep.tile([P, PASSES, WIDTH], U8, align_bytes=64)
+        band = keep.tile([P, HEADS, BAND_COLS], F32)
 
-        def quantise_x(s):
-            x_grouped = stage.tile([P, WIDTH, PACK], BF16, align_bytes=64)
-            nc.scalar.copy(
+        def regroup_x(copy, s):
+            x_grouped = early.tile([P, WIDTH, PACK], BF16, align_bytes=64)
+            copy(
                 out=x_grouped[:].rearrange("p (c i) t -> p c t i", i=4),
-                in_=x_raw[:, s, :, :].rearrange("p t (c i) -> p c t i", i=4),
+                in_=x_raw[s][:].rearrange("p t (c i) -> p c t i", i=4),
             )
+            return x_grouped
+
+        def quantise_x(s, x_grouped):
             nc.vector.quantize_mx(
                 out=x_codes[:, s, :].bitcast(E4M3X4),
                 scales=x_scales[:, s, :],
                 in_=x_grouped[:].rearrange("p c t -> p (c t)"),
             )
 
-        def add_tap(acc, h, offset, weight, first):
-            last = TOKENS if offset <= ZERO_PAD else TOKENS - offset
+        def add_tap(acc, h, tap, first, stop):
+            offset, table, row = tap
+            if stop + offset > TOKENS + ZERO_PAD:
+                stop = TOKENS - offset
             nc.vector.scalar_tensor_tensor(
-                out=acc[:, first:last], in0=grad[:, h, first + offset : last + offset], scalar=weight,
-                in1=acc[:, first:last], op0=ALU.mult, op1=ALU.add,
+                out=acc[:, first:stop], in0=grad[:, h, first + offset : stop + offset],
+                scalar=table[:, row, h : h + 1], in1=acc[:, first:stop], op0=ALU.mult, op1=ALU.add,
             )
 
-        def scalar_products(h):
-            parts = []
-            for offset, table, row in fine_taps[:PRODUCT_TAPS]:
-                product = terms.tile([P, TOKENS + ZERO_PAD], F32)
-                nc.scalar.activation(out=product[:], in_=grad[:, h, :], func=ACT.Copy, scale=table[:, row, h : h + 1])
-                parts.append((product, offset))
-            offset, table, row = fine_taps[PRODUCT_TAPS]
+        def start_sum(h):
+            offset, table, row = start_tap
             acc = sums.tile([P, TOKENS], F32)
             nc.scalar.activation(
                 out=acc[:], in_=grad[:, h, offset : offset + TOKENS], func=ACT.Copy, scale=table[:, row, h : h + 1]
             )
-            return [(acc, 0)] + parts
+            return acc
 
-        def transposed_classes(h):
+        def scalar_products(h):
+            parts = []
+            for offset, table, row in product_taps:
+                product = terms.tile([P, TOKENS + ZERO_PAD], F32)
+                nc.scalar.activation(out=product[:], in_=grad[:, h, :], func=ACT.Copy, scale=table[:, row, h : h + 1])
+                parts.append((product, offset))
+            return parts
+
+        def transpose_classes(h):
             classes_ps = psum_c.tile([P, STRIDE, P], BF16)
             for r in range(STRIDE):
                 nc.tensor.transpose(classes_ps[:, r, :], grad[:, h, r:TOKENS:STRIDE], identity_bf[:])
-            classes = stage.tile([P, STRIDE, P], F32)
+            return classes_ps
+
+        def copy_classes(classes_ps):
+            classes = early.tile([P, STRIDE, P], F32)
             nc.scalar.copy(out=classes[:], in_=classes_ps[:])
             return classes
 
@@ -186,92 +202,140 @@ def tile_causalwaveletfieldattentionbyte_pa_v_kernel(
                 banks.append(band_ps)
             return banks
 
-        def add_band_sums(acc, banks):
+        def add_band_sums(acc, band_ps, bank):
             by_class = acc[:, 0:BAND_TOKENS].rearrange("p (q r) -> p q r", r=STRIDE)
-            for bank, band_ps in enumerate(banks):
-                part = by_class[:, :, bank * BANK_CLASSES : (bank + 1) * BANK_CLASSES]
-                nc.vector.tensor_tensor(out=part, in0=part, in1=band_ps[:].rearrange("p r q -> p q r"), op=ALU.add)
+            part = by_class[:, :, bank * BANK_CLASSES : (bank + 1) * BANK_CLASSES]
+            nc.vector.tensor_tensor(out=part, in0=part, in1=band_ps[:].rearrange("p r q -> p q r"), op=ALU.add)
 
-        def turn_and_scale(h, head_parts, dv_cols):
-            for g in range(PASSES_PER_BATCH):
-                turned = psum_t.tile([P, PACK, P], F32)
-                for t in range(PACK):
-                    first = g * K_PASS + t * P
-                    for i, (part, offset) in enumerate(head_parts):
-                        nc.tensor.matmul(
-                            out=turned[:, t, :], lhsT=part[:, first + offset : first + offset + P], rhs=identity[:],
-                            is_transpose=True, start=(i == 0), stop=(i == len(head_parts) - 1),
-                        )
-                kmag_g = kmag[:, :, h].rearrange("p (b g t) -> p b g t", b=BATCH, t=PACK)[:, :, g, :]
-                nc.vector.tensor_tensor(
-                    out=dv_cols[:, g::PASSES_PER_BATCH, :, :],
-                    in0=turned[:].rearrange("p t (b c) -> p b c t", b=BATCH),
-                    in1=kmag_g.unsqueeze(2).to_broadcast([P, BATCH, HEAD_DIM, PACK]),
-                    op=ALU.mult,
-                )
-
-        def multiply(pair, dv_grouped):
-            dv_codes = stage.tile([P, PASSES * P], U32, align_bytes=64)
-            dv_scales = stage.tile([P, PASSES * P], U8, align_bytes=64)
-            nc.vector.quantize_mx(
-                out=dv_codes[:].bitcast(E5M2X4),
-                scales=dv_scales[:],
-                in_=dv_grouped[:].rearrange("p s c t -> p (s c t)"),
-            )
-            result = stage.tile([P, WIDTH], F32)
-            for half in range(WIDTH // N_TILE):
-                cols = slice(half * N_TILE, (half + 1) * N_TILE)
-                product = psum_o.tile([P, N_TILE], F32)
-                for s in range(PASSES):
-                    nc.tensor.matmul_mx(
-                        out=product[:],
-                        lhsT=dv_codes[:, s * P : (s + 1) * P].bitcast(E5M2X4),
-                        lhsT_scale=dv_scales[:, s * P : (s + 1) * P],
-                        rhs=x_codes[:, s, cols].bitcast(E4M3X4),
-                        rhs_scale=x_scales[:, s, cols],
-                        start=(s == 0),
-                        stop=(s == PASSES - 1),
+        def turn(parts, g):
+            turned = psum_t.tile([P, PACK, P], F32)
+            for t in range(PACK):
+                first = g * K_PASS + t * P
+                for i, (part, offset) in enumerate(parts):
+                    nc.tensor.matmul(
+                        out=turned[:, t, :], lhsT=part[:, first + offset : first + offset + P], rhs=identity[:],
+                        is_transpose=True, start=(i == 0), stop=(i == len(parts) - 1),
                     )
-                nc.scalar.copy(out=result[:, cols], in_=product[:])
-            nc.sync.dma_start(out=out[pair * P : (pair + 1) * P, :], in_=result[:])
+            return turned
+
+        def scale(turned, h, g, dv_cols):
+            kmag_g = kmag[:, :, h].rearrange("p (b g t) -> p b g t", b=BATCH, t=PACK)[:, :, g, :]
+            nc.vector.tensor_tensor(
+                out=dv_cols[:, g::PASSES_PER_BATCH, :, :],
+                in0=turned[:].rearrange("p t (b c) -> p b c t", b=BATCH),
+                in1=kmag_g.unsqueeze(2).to_broadcast([P, BATCH, HEAD_DIM, PACK]),
+                op=ALU.mult,
+            )
+
+        def multiply(dv_codes, dv_scales, half):
+            cols = slice(half * N_TILE, (half + 1) * N_TILE)
+            product = psum_o.tile([P, N_TILE], F32)
+            for s in range(PASSES):
+                nc.tensor.matmul_mx(
+                    out=product[:],
+                    lhsT=dv_codes[:, s * P : (s + 1) * P].bitcast(E5M2X4),
+                    lhsT_scale=dv_scales[:, s * P : (s + 1) * P],
+                    rhs=x_codes[:, s, cols].bitcast(E4M3X4),
+                    rhs_scale=x_scales[:, s, cols],
+                    start=(s == 0),
+                    stop=(s == PASSES - 1),
+                )
+            return product
+
+        QUARTERS = 4
+        SHORT = len(tail_taps) // QUARTERS
+        assert SHORT * QUARTERS == len(tail_taps) and SHORT == 3
+        assert len(vector_taps) + STRIDE // BANK_CLASSES == QUARTERS
+        PAIRS = HEADS // 2
 
         def heads_of(pair):
             return (2 * pair, 2 * pair + 1)
 
-        PAIRS = HEADS // 2
-        parts = {0: [scalar_products(h) for h in heads_of(0)]}
-        banks = {0: [band_sums(h, transposed_classes(h)) for h in heads_of(0)]}
-        for s in range(PASSES):
-            quantise_x(s)
+        for offset, table, row in band_taps:
+            nc.vector.tensor_copy(out=rows[:, 0:HEADS, CLASS_TOKENS - 1 - offset // STRIDE], in_=table[:, row, :])
+        accs = {0: [start_sum(h) for h in heads_of(0)]}
+        pitch = (HEADS + 1) * ROW
+        scratch = out.rearrange("c i -> (c i)")
+        nc.scalar.dma_start(
+            out=scratch[0 : P * pitch].rearrange("(p w) -> p w", w=pitch), in_=rows[:].rearrange("p h l -> p (h l)")
+        )
+        products = {0: [scalar_products(h) for h in heads_of(0)]}
+        skewed = scratch[P - 1 : P - 1 + P * (pitch - 1)].rearrange("(p w) -> p w", w=pitch - 1)
+        nc.scalar.dma_start(
+            out=band[:], in_=skewed[:, 0 : HEADS * ROW].rearrange("p (h l) -> p h l", l=ROW)[:, :, 0:BAND_COLS]
+        )
+        classes = {0: [copy_classes(transpose_classes(h)) for h in heads_of(0)]}
+        quantised = {}
+        x_late = {}
 
-        for pair in range(PAIRS + 1):
-            filtering = pair < PAIRS
-            preparing = pair + 1 < PAIRS
-            finishing = pair >= 1
+        for rnd in range(PAIRS + 2):
+            filtering = rnd < PAIRS
+            preparing = rnd + 1 < PAIRS
+            scaling = 1 <= rnd <= PAIRS
+            multiplying = rnd >= 2
+            turned = {}
+            banks = {}
+
             if preparing:
-                parts[pair + 1] = [scalar_products(h) for h in heads_of(pair + 1)]
-            if filtering:
-                accs = [head_parts[0][0] for head_parts in parts[pair]]
-            if finishing:
-                dv_grouped = stage.tile([P, PASSES, P, PACK], BF16, align_bytes=64)
-                turn_and_scale(heads_of(pair - 1)[0], parts[pair - 1][0], dv_grouped[:, :, 0:HEAD_DIM, :])
-            if filtering:
-                for offset, table, row in fine_taps[PRODUCT_TAPS + 1 :]:
-                    for acc, h in zip(accs, heads_of(pair)):
-                        add_tap(acc, h, offset, table[:, row, h : h + 1], 0)
+                accs[rnd + 1] = [start_sum(h) for h in heads_of(rnd + 1)]
+            if scaling:
+                summands = [[(acc, 0)] + parts for acc, parts in zip(accs[rnd - 1], products[rnd - 1])]
+                dv_grouped = late.tile([P, PASSES, P, PACK], BF16, align_bytes=64)
+                turned[0] = turn(summands[0], 0)
+                turned[1] = turn(summands[0], 1)
             if preparing:
-                classes = [transposed_classes(h) for h in heads_of(pair + 1)]
-            if finishing:
-                turn_and_scale(heads_of(pair - 1)[1], parts[pair - 1][1], dv_grouped[:, :, HEAD_DIM:P, :])
-            if filtering:
-                for offset, table, row in band_taps:
-                    if BAND_TOKENS + offset < TOKENS:
-                        for acc, h in zip(accs, heads_of(pair)):
-                            add_tap(acc, h, offset, table[:, row, h : h + 1], BAND_TOKENS)
-            if finishing:
-                multiply(pair - 1, dv_grouped)
-            if filtering:
-                for acc, head_banks in zip(accs, banks[pair]):
-                    add_band_sums(acc, head_banks)
-            if preparing:
-                banks[pair + 1] = [band_sums(h, c) for h, c in zip(heads_of(pair + 1), classes)]
+                products[rnd + 1] = [scalar_products(h) for h in heads_of(rnd + 1)]
+            if multiplying:
+                dv_codes, dv_scales = quantised[rnd - 2]
+                result = late.tile([P, WIDTH], F32)
+
+            for quarter in range(QUARTERS):
+                if quarter == 2 and rnd - 1 in x_late:
+                    quantise_x(VECTOR_X_PASSES + rnd - 1, x_late[rnd - 1])
+                if quarter < 2 and filtering:
+                    banks[quarter] = band_sums(heads_of(rnd)[quarter], classes[rnd][quarter])
+                if 1 <= quarter <= 2 and scaling:
+                    turned[quarter + 1] = turn(summands[1], quarter - 1)
+                if quarter >= 2:
+                    half = quarter - 2
+                    if multiplying:
+                        product = multiply(dv_codes, dv_scales, half)
+                        nc.scalar.copy(out=result[:, half * N_TILE : (half + 1) * N_TILE], in_=product[:])
+                    if preparing:
+                        if half == 0:
+                            classes[rnd + 1] = []
+                        classes[rnd + 1].append(copy_classes(transpose_classes(heads_of(rnd + 1)[half])))
+                if rnd == 0 and quarter == len(vector_taps):
+                    x_early = [regroup_x(nc.vector.tensor_copy, s) for s in range(VECTOR_X_PASSES)]
+                    for s in range(VECTOR_X_PASSES):
+                        quantise_x(s, x_early[s])
+                for k in range(SHORT):
+                    if filtering:
+                        for acc, h in zip(accs[rnd], heads_of(rnd)):
+                            add_tap(acc, h, tail_taps[quarter * SHORT + k], BAND_TOKENS, TOKENS)
+                    if k < 2 and filtering:
+                        if quarter < len(vector_taps):
+                            add_tap(accs[rnd][k], heads_of(rnd)[k], vector_taps[quarter], 0, BAND_TOKENS)
+                        else:
+                            bank = quarter - len(vector_taps)
+                            add_band_sums(accs[rnd][k], banks[k][bank], bank)
+                    if k == 2 and scaling:
+                        side, g = quarter // PASSES_PER_BATCH, quarter % PASSES_PER_BATCH
+                        scale(
+                            turned[quarter], heads_of(rnd - 1)[side], g,
+                            dv_grouped[:, :, side * HEAD_DIM : (side + 1) * HEAD_DIM, :],
+                        )
+
+            if multiplying:
+                nc.sync.dma_start(out=out[(rnd - 2) * P : (rnd - 1) * P, :], in_=result[:])
+            if VECTOR_X_PASSES + rnd < PASSES:
+                x_late[rnd] = regroup_x(nc.scalar.copy, VECTOR_X_PASSES + rnd)
+            if scaling:
+                dv_codes_new = codes.tile([P, PASSES * P], U32, align_bytes=64)
+                dv_scales_new = codes.tile([P, PASSES * P], U8, align_bytes=64)
+                nc.vector.quantize_mx(
+                    out=dv_codes_new[:].bitcast(E5M2X4),
+                    scales=dv_scales_new[:],
+                    in_=dv_grouped[:].rearrange("p s c t -> p (s c t)"),
+                )
+                quantised[rnd - 1] = (dv_codes_new, dv_scales_new)

@@ -23,11 +23,11 @@ PASSES_PER_BATCH = TOKENS // K_PASS
 N_TILE = 512
 STRIDE = 8
 CLASS_TOKENS = TOKENS // STRIDE
-BAND_COLS = 96
+MX_FLOPS = 2 * CHANNELS * BATCH * TOKENS * WIDTH
+BAND_COLS = MX_FLOPS // 10 // (HEADS * STRIDE * 2 * P * P) // 2 * 2
 BAND_TOKENS = STRIDE * BAND_COLS
 BANK_CLASSES = 4
-ROW = 224
-VECTOR_X_PASSES = 2
+ROW = 232
 PRODUCT_TAPS = 3
 ZERO_PAD = 16
 TAP0, TAP1, TAP2, TAP3 = 0.4829629131445341, 0.8365163037378079, 0.2241438680420134, -0.1294095225512604
@@ -41,13 +41,9 @@ def tile_causalwaveletfieldattentionbyte_pa_v_kernel(
 ):
     nc = tc.nc
     with ExitStack() as ctx:
-        ctx.enter_context(tc.manual_schedule())
         keep = ctx.enter_context(tc.tile_pool(name="keep", bufs=1))
         sums = ctx.enter_context(tc.tile_pool(name="sums", bufs=6))
-        terms = ctx.enter_context(tc.tile_pool(name="terms", bufs=5 * PRODUCT_TAPS))
-        early = ctx.enter_context(tc.tile_pool(name="early", bufs=2))
-        late = ctx.enter_context(tc.tile_pool(name="late", bufs=2))
-        codes = ctx.enter_context(tc.tile_pool(name="codes", bufs=3))
+        stage = ctx.enter_context(tc.tile_pool(name="stage", bufs=2))
         psum_c = ctx.enter_context(tc.psum_pool(name="psum_c", bufs=1))
         psum_b = ctx.enter_context(tc.psum_pool(name="psum_b", bufs=4))
         psum_t = ctx.enter_context(tc.psum_pool(name="psum_t", bufs=2))
@@ -66,32 +62,19 @@ def tile_causalwaveletfieldattentionbyte_pa_v_kernel(
                     in_=grad_out[b, h * HEAD_DIM : (h + 1) * HEAD_DIM, :],
                 )
 
-        for h in range(4):
-            load_head(h)
+        load_head(0)
+        load_head(1)
         kmag = keep.tile([P, PASSES * PACK, HEADS], F32)
         nc.sync.dma_start(out=kmag[:], in_=k_mag.rearrange("b (i p) h -> p (b i) h", p=P))
+        x_raw = keep.tile([P, PASSES, PACK, WIDTH], BF16)
         x_rows = x.rearrange("b (g t p) i -> (b g) p t i", t=PACK, p=P)
-        x_raw = {}
-
-        def load_x(s):
-            x_raw[s] = early.tile([P, PACK, WIDTH], BF16, name="x_raw")
-            nc.sync.dma_start(out=x_raw[s][:], in_=x_rows[s])
-
-        load_x(0)
-        load_x(1)
-        for h in range(4, 8):
-            load_head(h)
-        load_x(2)
-        load_x(3)
-        for h in range(8, HEADS):
+        for s in range(PASSES):
+            nc.sync.dma_start(out=x_raw[:, s, :, :], in_=x_rows[s])
+        for h in range(2, HEADS):
             load_head(h)
 
-        identity_bf = keep.tile([P, P], BF16)
-        make_identity(nc, identity_bf[:])
         identity = keep.tile([P, P], F32)
         make_identity(nc, identity[:])
-        rows = keep.tile([P, HEADS + 1, ROW], F32)
-        nc.vector.memset(rows[:], 0.0)
 
         logits = keep.tile([P, SCALES, HEADS], F32)
         nc.vector.tensor_copy(out=logits[:].rearrange("p j h -> p (j h)"), in_=logits_bf[:])
@@ -129,65 +112,69 @@ def tile_causalwaveletfieldattentionbyte_pa_v_kernel(
         taps = sorted(taps, key=lambda tap: tap[0])
         fine_taps = [tap for tap in taps if tap[0] % STRIDE != 0]
         band_taps = [tap for tap in taps if tap[0] % STRIDE == 0]
-        product_taps = fine_taps[:PRODUCT_TAPS]
-        start_tap = fine_taps[PRODUCT_TAPS]
-        vector_taps = fine_taps[PRODUCT_TAPS + 1 :]
-        tail_taps = vector_taps + [tap for tap in band_taps if BAND_TOKENS + tap[0] < TOKENS]
 
+        pitch = (HEADS + 1) * ROW
+        scratch = out.rearrange("c i -> (c i)")
+        with tc.tile_pool(name="setup", bufs=1) as setup:
+            rows = setup.tile([P, HEADS + 1, ROW], F32)
+            nc.vector.memset(rows[:], 0.0)
+            for offset, table, row in band_taps:
+                nc.vector.tensor_copy(out=rows[:, 0:HEADS, CLASS_TOKENS - 1 - offset // STRIDE], in_=table[:, row, :])
+            nc.gpsimd.dma_start(
+                out=scratch[0 : P * pitch].rearrange("(p w) -> p w", w=pitch), in_=rows[:].rearrange("p h l -> p (h l)")
+            )
+        terms = ctx.enter_context(tc.tile_pool(name="terms", bufs=6 * PRODUCT_TAPS))
+        skewed = scratch[P - 1 : P - 1 + P * (pitch - 1)].rearrange("(p w) -> p w", w=pitch - 1)
+        band = keep.tile([P, HEADS, BAND_COLS], F32)
+        nc.gpsimd.dma_start(
+            out=band[:], in_=skewed[:, 0 : HEADS * ROW].rearrange("p (h l) -> p h l", l=ROW)[:, :, 0:BAND_COLS]
+        )
 
         x_codes = keep.tile([P, PASSES, WIDTH], U32, align_bytes=64)
         x_scales = keep.tile([P, PASSES, WIDTH], U8, align_bytes=64)
-        band = keep.tile([P, HEADS, BAND_COLS], F32)
 
-        def regroup_x(copy, s):
-            x_grouped = early.tile([P, WIDTH, PACK], BF16, align_bytes=64)
-            copy(
+        def quantise_x(s):
+            x_grouped = stage.tile([P, WIDTH, PACK], BF16, align_bytes=64)
+            nc.scalar.copy(
                 out=x_grouped[:].rearrange("p (c i) t -> p c t i", i=4),
-                in_=x_raw[s][:].rearrange("p t (c i) -> p c t i", i=4),
+                in_=x_raw[:, s, :, :].rearrange("p t (c i) -> p c t i", i=4),
             )
-            return x_grouped
-
-        def quantise_x(s, x_grouped):
             nc.vector.quantize_mx(
                 out=x_codes[:, s, :].bitcast(E4M3X4),
                 scales=x_scales[:, s, :],
                 in_=x_grouped[:].rearrange("p c t -> p (c t)"),
             )
 
-        def add_tap(acc, h, tap, first, stop):
-            offset, table, row = tap
-            if stop + offset > TOKENS + ZERO_PAD:
-                stop = TOKENS - offset
+        def add_tap(acc, h, offset, weight, first):
+            last = TOKENS if offset <= ZERO_PAD else TOKENS - offset
             nc.vector.scalar_tensor_tensor(
-                out=acc[:, first:stop], in0=grad[:, h, first + offset : stop + offset],
-                scalar=table[:, row, h : h + 1], in1=acc[:, first:stop], op0=ALU.mult, op1=ALU.add,
+                out=acc[:, first:last], in0=grad[:, h, first + offset : last + offset], scalar=weight,
+                in1=acc[:, first:last], op0=ALU.mult, op1=ALU.add,
             )
 
-        def start_sum(h):
-            offset, table, row = start_tap
+        def scalar_products(h):
+            parts = []
+            for offset, table, row in fine_taps[:PRODUCT_TAPS]:
+                product = terms.tile([P, TOKENS + ZERO_PAD], F32)
+                nc.scalar.activation(out=product[:], in_=grad[:, h, :], func=ACT.Copy, scale=table[:, row, h : h + 1])
+                parts.append((product, offset))
+            offset, table, row = fine_taps[PRODUCT_TAPS]
             acc = sums.tile([P, TOKENS], F32)
             nc.scalar.activation(
                 out=acc[:], in_=grad[:, h, offset : offset + TOKENS], func=ACT.Copy, scale=table[:, row, h : h + 1]
             )
-            return acc
+            return [(acc, 0)] + parts
 
-        def scalar_products(h):
-            parts = []
-            for offset, table, row in product_taps:
-                product = terms.tile([P, TOKENS + ZERO_PAD], F32)
-                nc.scalar.activation(out=product[:], in_=grad[:, h, :], func=ACT.Copy, scale=table[:, row, h : h + 1])
-                parts.append((product, offset))
-            return parts
-
-        def transpose_classes(h):
-            classes_ps = psum_c.tile([P, STRIDE, P], BF16)
-            for r in range(STRIDE):
-                nc.tensor.transpose(classes_ps[:, r, :], grad[:, h, r:TOKENS:STRIDE], identity_bf[:])
-            return classes_ps
-
-        def copy_classes(classes_ps):
-            classes = early.tile([P, STRIDE, P], F32)
-            nc.scalar.copy(out=classes[:], in_=classes_ps[:])
+        def transposed_classes(h):
+            words = grad[:, h, 0:TOKENS].bitcast(F32)
+            classes_ps = psum_c.tile([P, STRIDE // 2, P], F32)
+            for w in range(STRIDE // 2):
+                nc.tensor.transpose(classes_ps[:, w, :], words[:, w : TOKENS // 2 : STRIDE // 2], identity[:])
+            classes = stage.tile([P, STRIDE, P], F32)
+            nc.scalar.copy(
+                out=classes[:].rearrange("p (w e) c -> p w e c", e=2),
+                in_=classes_ps[:].bitcast(BF16).rearrange("p w (c e) -> p w e c", e=2),
+            )
             return classes
 
         def band_sums(h, classes):
@@ -202,140 +189,92 @@ def tile_causalwaveletfieldattentionbyte_pa_v_kernel(
                 banks.append(band_ps)
             return banks
 
-        def add_band_sums(acc, band_ps, bank):
+        def add_band_sums(acc, banks):
             by_class = acc[:, 0:BAND_TOKENS].rearrange("p (q r) -> p q r", r=STRIDE)
-            part = by_class[:, :, bank * BANK_CLASSES : (bank + 1) * BANK_CLASSES]
-            nc.vector.tensor_tensor(out=part, in0=part, in1=band_ps[:].rearrange("p r q -> p q r"), op=ALU.add)
+            for bank, band_ps in enumerate(banks):
+                part = by_class[:, :, bank * BANK_CLASSES : (bank + 1) * BANK_CLASSES]
+                nc.vector.tensor_tensor(out=part, in0=part, in1=band_ps[:].rearrange("p r q -> p q r"), op=ALU.add)
 
-        def turn(parts, g):
-            turned = psum_t.tile([P, PACK, P], F32)
-            for t in range(PACK):
-                first = g * K_PASS + t * P
-                for i, (part, offset) in enumerate(parts):
-                    nc.tensor.matmul(
-                        out=turned[:, t, :], lhsT=part[:, first + offset : first + offset + P], rhs=identity[:],
-                        is_transpose=True, start=(i == 0), stop=(i == len(parts) - 1),
-                    )
-            return turned
-
-        def scale(turned, h, g, dv_cols):
-            kmag_g = kmag[:, :, h].rearrange("p (b g t) -> p b g t", b=BATCH, t=PACK)[:, :, g, :]
-            nc.vector.tensor_tensor(
-                out=dv_cols[:, g::PASSES_PER_BATCH, :, :],
-                in0=turned[:].rearrange("p t (b c) -> p b c t", b=BATCH),
-                in1=kmag_g.unsqueeze(2).to_broadcast([P, BATCH, HEAD_DIM, PACK]),
-                op=ALU.mult,
-            )
-
-        def multiply(dv_codes, dv_scales, half):
-            cols = slice(half * N_TILE, (half + 1) * N_TILE)
-            product = psum_o.tile([P, N_TILE], F32)
-            for s in range(PASSES):
-                nc.tensor.matmul_mx(
-                    out=product[:],
-                    lhsT=dv_codes[:, s * P : (s + 1) * P].bitcast(E5M2X4),
-                    lhsT_scale=dv_scales[:, s * P : (s + 1) * P],
-                    rhs=x_codes[:, s, cols].bitcast(E4M3X4),
-                    rhs_scale=x_scales[:, s, cols],
-                    start=(s == 0),
-                    stop=(s == PASSES - 1),
+        def turn_and_scale(h, head_parts, dv_cols):
+            for g in range(PASSES_PER_BATCH):
+                turned = psum_t.tile([P, PACK, P], F32)
+                for t in range(PACK):
+                    first = g * K_PASS + t * P
+                    for i, (part, offset) in enumerate(head_parts):
+                        nc.tensor.matmul(
+                            out=turned[:, t, :], lhsT=part[:, first + offset : first + offset + P], rhs=identity[:],
+                            is_transpose=True, start=(i == 0), stop=(i == len(head_parts) - 1),
+                        )
+                kmag_g = kmag[:, :, h].rearrange("p (b g t) -> p b g t", b=BATCH, t=PACK)[:, :, g, :]
+                nc.vector.tensor_tensor(
+                    out=dv_cols[:, g::PASSES_PER_BATCH, :, :],
+                    in0=turned[:].rearrange("p t (b c) -> p b c t", b=BATCH),
+                    in1=kmag_g.unsqueeze(2).to_broadcast([P, BATCH, HEAD_DIM, PACK]),
+                    op=ALU.mult,
                 )
-            return product
 
-        QUARTERS = 4
-        SHORT = len(tail_taps) // QUARTERS
-        assert SHORT * QUARTERS == len(tail_taps) and SHORT == 3
-        assert len(vector_taps) + STRIDE // BANK_CLASSES == QUARTERS
-        PAIRS = HEADS // 2
+        def multiply(pair, dv_grouped):
+            dv_codes = stage.tile([P, PASSES * P], U32, align_bytes=64)
+            dv_scales = stage.tile([P, PASSES * P], U8, align_bytes=64)
+            nc.vector.quantize_mx(
+                out=dv_codes[:].bitcast(E5M2X4),
+                scales=dv_scales[:],
+                in_=dv_grouped[:].rearrange("p s c t -> p (s c t)"),
+            )
+            result = stage.tile([P, WIDTH], F32)
+            for half in range(WIDTH // N_TILE):
+                cols = slice(half * N_TILE, (half + 1) * N_TILE)
+                product = psum_o.tile([P, N_TILE], F32)
+                for s in range(PASSES):
+                    nc.tensor.matmul_mx(
+                        out=product[:],
+                        lhsT=dv_codes[:, s * P : (s + 1) * P].bitcast(E5M2X4),
+                        lhsT_scale=dv_scales[:, s * P : (s + 1) * P],
+                        rhs=x_codes[:, s, cols].bitcast(E4M3X4),
+                        rhs_scale=x_scales[:, s, cols],
+                        start=(s == 0),
+                        stop=(s == PASSES - 1),
+                    )
+                nc.scalar.copy(out=result[:, cols], in_=product[:])
+            nc.sync.dma_start(out=out[pair * P : (pair + 1) * P, :], in_=result[:])
 
         def heads_of(pair):
             return (2 * pair, 2 * pair + 1)
 
-        for offset, table, row in band_taps:
-            nc.vector.tensor_copy(out=rows[:, 0:HEADS, CLASS_TOKENS - 1 - offset // STRIDE], in_=table[:, row, :])
-        accs = {0: [start_sum(h) for h in heads_of(0)]}
-        pitch = (HEADS + 1) * ROW
-        scratch = out.rearrange("c i -> (c i)")
-        nc.scalar.dma_start(
-            out=scratch[0 : P * pitch].rearrange("(p w) -> p w", w=pitch), in_=rows[:].rearrange("p h l -> p (h l)")
-        )
-        products = {0: [scalar_products(h) for h in heads_of(0)]}
-        skewed = scratch[P - 1 : P - 1 + P * (pitch - 1)].rearrange("(p w) -> p w", w=pitch - 1)
-        nc.scalar.dma_start(
-            out=band[:], in_=skewed[:, 0 : HEADS * ROW].rearrange("p (h l) -> p h l", l=ROW)[:, :, 0:BAND_COLS]
-        )
-        classes = {0: [copy_classes(transpose_classes(h)) for h in heads_of(0)]}
-        quantised = {}
-        x_late = {}
+        PAIRS = HEADS // 2
+        parts = {0: [scalar_products(h) for h in heads_of(0)]}
+        banks = {0: [band_sums(h, transposed_classes(h)) for h in heads_of(0)]}
+        for s in range(PASSES):
+            quantise_x(s)
 
-        for rnd in range(PAIRS + 2):
-            filtering = rnd < PAIRS
-            preparing = rnd + 1 < PAIRS
-            scaling = 1 <= rnd <= PAIRS
-            multiplying = rnd >= 2
-            turned = {}
-            banks = {}
-
+        for pair in range(PAIRS + 1):
+            filtering = pair < PAIRS
+            preparing = pair + 1 < PAIRS
+            finishing = pair >= 1
             if preparing:
-                accs[rnd + 1] = [start_sum(h) for h in heads_of(rnd + 1)]
-            if scaling:
-                summands = [[(acc, 0)] + parts for acc, parts in zip(accs[rnd - 1], products[rnd - 1])]
-                dv_grouped = late.tile([P, PASSES, P, PACK], BF16, align_bytes=64)
-                turned[0] = turn(summands[0], 0)
-                turned[1] = turn(summands[0], 1)
+                parts[pair + 1] = [scalar_products(h) for h in heads_of(pair + 1)]
+            if filtering:
+                accs = [head_parts[0][0] for head_parts in parts[pair]]
+            if finishing:
+                dv_grouped = stage.tile([P, PASSES, P, PACK], BF16, align_bytes=64)
+                turn_and_scale(heads_of(pair - 1)[0], parts[pair - 1][0], dv_grouped[:, :, 0:HEAD_DIM, :])
+            if filtering:
+                for offset, table, row in fine_taps[PRODUCT_TAPS + 1 :]:
+                    for acc, h in zip(accs, heads_of(pair)):
+                        add_tap(acc, h, offset, table[:, row, h : h + 1], 0)
             if preparing:
-                products[rnd + 1] = [scalar_products(h) for h in heads_of(rnd + 1)]
-            if multiplying:
-                dv_codes, dv_scales = quantised[rnd - 2]
-                result = late.tile([P, WIDTH], F32)
-
-            for quarter in range(QUARTERS):
-                if quarter == 2 and rnd - 1 in x_late:
-                    quantise_x(VECTOR_X_PASSES + rnd - 1, x_late[rnd - 1])
-                if quarter < 2 and filtering:
-                    banks[quarter] = band_sums(heads_of(rnd)[quarter], classes[rnd][quarter])
-                if 1 <= quarter <= 2 and scaling:
-                    turned[quarter + 1] = turn(summands[1], quarter - 1)
-                if quarter >= 2:
-                    half = quarter - 2
-                    if multiplying:
-                        product = multiply(dv_codes, dv_scales, half)
-                        nc.scalar.copy(out=result[:, half * N_TILE : (half + 1) * N_TILE], in_=product[:])
-                    if preparing:
-                        if half == 0:
-                            classes[rnd + 1] = []
-                        classes[rnd + 1].append(copy_classes(transpose_classes(heads_of(rnd + 1)[half])))
-                if rnd == 0 and quarter == len(vector_taps):
-                    x_early = [regroup_x(nc.vector.tensor_copy, s) for s in range(VECTOR_X_PASSES)]
-                    for s in range(VECTOR_X_PASSES):
-                        quantise_x(s, x_early[s])
-                for k in range(SHORT):
-                    if filtering:
-                        for acc, h in zip(accs[rnd], heads_of(rnd)):
-                            add_tap(acc, h, tail_taps[quarter * SHORT + k], BAND_TOKENS, TOKENS)
-                    if k < 2 and filtering:
-                        if quarter < len(vector_taps):
-                            add_tap(accs[rnd][k], heads_of(rnd)[k], vector_taps[quarter], 0, BAND_TOKENS)
-                        else:
-                            bank = quarter - len(vector_taps)
-                            add_band_sums(accs[rnd][k], banks[k][bank], bank)
-                    if k == 2 and scaling:
-                        side, g = quarter // PASSES_PER_BATCH, quarter % PASSES_PER_BATCH
-                        scale(
-                            turned[quarter], heads_of(rnd - 1)[side], g,
-                            dv_grouped[:, :, side * HEAD_DIM : (side + 1) * HEAD_DIM, :],
-                        )
-
-            if multiplying:
-                nc.sync.dma_start(out=out[(rnd - 2) * P : (rnd - 1) * P, :], in_=result[:])
-            if VECTOR_X_PASSES + rnd < PASSES:
-                x_late[rnd] = regroup_x(nc.scalar.copy, VECTOR_X_PASSES + rnd)
-            if scaling:
-                dv_codes_new = codes.tile([P, PASSES * P], U32, align_bytes=64)
-                dv_scales_new = codes.tile([P, PASSES * P], U8, align_bytes=64)
-                nc.vector.quantize_mx(
-                    out=dv_codes_new[:].bitcast(E5M2X4),
-                    scales=dv_scales_new[:],
-                    in_=dv_grouped[:].rearrange("p s c t -> p (s c t)"),
-                )
-                quantised[rnd - 1] = (dv_codes_new, dv_scales_new)
+                classes = [transposed_classes(h) for h in heads_of(pair + 1)]
+            if finishing:
+                turn_and_scale(heads_of(pair - 1)[1], parts[pair - 1][1], dv_grouped[:, :, HEAD_DIM:P, :])
+            if filtering:
+                for offset, table, row in band_taps:
+                    if BAND_TOKENS + offset < TOKENS:
+                        for acc, h in zip(accs, heads_of(pair)):
+                            add_tap(acc, h, offset, table[:, row, h : h + 1], BAND_TOKENS)
+            if finishing:
+                multiply(pair - 1, dv_grouped)
+            if filtering:
+                for acc, head_banks in zip(accs, banks[pair]):
+                    add_band_sums(acc, head_banks)
+            if preparing:
+                banks[pair + 1] = [band_sums(h, c) for h, c in zip(heads_of(pair + 1), classes)]

@@ -44,6 +44,8 @@ def tile_causalwaveletfieldattentionbyte_pa_v_kernel(
         keep = ctx.enter_context(tc.tile_pool(name="keep", bufs=1))
         sums = ctx.enter_context(tc.tile_pool(name="sums", bufs=6))
         stage = ctx.enter_context(tc.tile_pool(name="stage", bufs=2))
+        heads_in = ctx.enter_context(tc.tile_pool(name="heads_in", bufs=6))
+        terms = ctx.enter_context(tc.tile_pool(name="terms", bufs=6 * PRODUCT_TAPS))
         psum_c = ctx.enter_context(tc.psum_pool(name="psum_c", bufs=1))
         psum_b = ctx.enter_context(tc.psum_pool(name="psum_b", bufs=4))
         psum_t = ctx.enter_context(tc.psum_pool(name="psum_t", bufs=2))
@@ -52,13 +54,14 @@ def tile_causalwaveletfieldattentionbyte_pa_v_kernel(
         logits_bf = keep.tile([P, SCALES * HEADS], BF16)
         nc.sync.dma_start(out=logits_bf[:], in_=scale_gain.rearrange("j h -> (j h)").partition_broadcast(P))
 
-        grad = keep.tile([P, HEADS, TOKENS + ZERO_PAD], BF16)
-        nc.vector.memset(grad[:, :, TOKENS:], 0.0)
+        grad = {}
 
         def load_head(h):
+            grad[h] = heads_in.tile([P, TOKENS + ZERO_PAD], BF16, name="grad_head")
+            nc.gpsimd.memset(grad[h][:, TOKENS:], 0.0)
             for b in range(BATCH):
                 nc.sync.dma_start(
-                    out=grad[b * HEAD_DIM : (b + 1) * HEAD_DIM, h, 0:TOKENS],
+                    out=grad[h][b * HEAD_DIM : (b + 1) * HEAD_DIM, 0:TOKENS],
                     in_=grad_out[b, h * HEAD_DIM : (h + 1) * HEAD_DIM, :],
                 )
 
@@ -66,11 +69,16 @@ def tile_causalwaveletfieldattentionbyte_pa_v_kernel(
         load_head(1)
         kmag = keep.tile([P, PASSES * PACK, HEADS], F32)
         nc.sync.dma_start(out=kmag[:], in_=k_mag.rearrange("b (i p) h -> p (b i) h", p=P))
-        x_raw = keep.tile([P, PASSES, PACK, WIDTH], BF16)
         x_rows = x.rearrange("b (g t p) i -> (b g) p t i", t=PACK, p=P)
-        for s in range(PASSES):
-            nc.sync.dma_start(out=x_raw[:, s, :, :], in_=x_rows[s])
-        for h in range(2, HEADS):
+        x_raw = {}
+
+        def load_x(s):
+            x_raw[s] = stage.tile([P, PACK, WIDTH], BF16, name="x_raw")
+            nc.sync.dma_start(out=x_raw[s][:], in_=x_rows[s])
+
+        load_x(0)
+        load_x(1)
+        for h in range(2, 6):
             load_head(h)
 
         identity = keep.tile([P, P], F32)
@@ -115,15 +123,13 @@ def tile_causalwaveletfieldattentionbyte_pa_v_kernel(
 
         pitch = (HEADS + 1) * ROW
         scratch = out.rearrange("c i -> (c i)")
-        with tc.tile_pool(name="setup", bufs=1) as setup:
-            rows = setup.tile([P, HEADS + 1, ROW], F32)
-            nc.vector.memset(rows[:], 0.0)
-            for offset, table, row in band_taps:
-                nc.vector.tensor_copy(out=rows[:, 0:HEADS, CLASS_TOKENS - 1 - offset // STRIDE], in_=table[:, row, :])
-            nc.gpsimd.dma_start(
-                out=scratch[0 : P * pitch].rearrange("(p w) -> p w", w=pitch), in_=rows[:].rearrange("p h l -> p (h l)")
-            )
-        terms = ctx.enter_context(tc.tile_pool(name="terms", bufs=6 * PRODUCT_TAPS))
+        rows = keep.tile([P, HEADS + 1, ROW], F32)
+        nc.vector.memset(rows[:], 0.0)
+        for offset, table, row in band_taps:
+            nc.vector.tensor_copy(out=rows[:, 0:HEADS, CLASS_TOKENS - 1 - offset // STRIDE], in_=table[:, row, :])
+        nc.gpsimd.dma_start(
+            out=scratch[0 : P * pitch].rearrange("(p w) -> p w", w=pitch), in_=rows[:].rearrange("p h l -> p (h l)")
+        )
         skewed = scratch[P - 1 : P - 1 + P * (pitch - 1)].rearrange("(p w) -> p w", w=pitch - 1)
         band = keep.tile([P, HEADS, BAND_COLS], F32)
         nc.gpsimd.dma_start(
@@ -137,7 +143,7 @@ def tile_causalwaveletfieldattentionbyte_pa_v_kernel(
             x_grouped = stage.tile([P, WIDTH, PACK], BF16, align_bytes=64)
             nc.scalar.copy(
                 out=x_grouped[:].rearrange("p (c i) t -> p c t i", i=4),
-                in_=x_raw[:, s, :, :].rearrange("p t (c i) -> p c t i", i=4),
+                in_=x_raw[s][:].rearrange("p t (c i) -> p c t i", i=4),
             )
             nc.vector.quantize_mx(
                 out=x_codes[:, s, :].bitcast(E4M3X4),
@@ -148,25 +154,28 @@ def tile_causalwaveletfieldattentionbyte_pa_v_kernel(
         def add_tap(acc, h, offset, weight, first):
             last = TOKENS if offset <= ZERO_PAD else TOKENS - offset
             nc.vector.scalar_tensor_tensor(
-                out=acc[:, first:last], in0=grad[:, h, first + offset : last + offset], scalar=weight,
+                out=acc[:, first:last], in0=grad[h][:, first + offset : last + offset], scalar=weight,
                 in1=acc[:, first:last], op0=ALU.mult, op1=ALU.add,
             )
 
-        def scalar_products(h):
+        def scalar_products(pair):
             parts = []
-            for offset, table, row in fine_taps[:PRODUCT_TAPS]:
-                product = terms.tile([P, TOKENS + ZERO_PAD], F32)
-                nc.scalar.activation(out=product[:], in_=grad[:, h, :], func=ACT.Copy, scale=table[:, row, h : h + 1])
-                parts.append((product, offset))
             offset, table, row = fine_taps[PRODUCT_TAPS]
-            acc = sums.tile([P, TOKENS], F32)
-            nc.scalar.activation(
-                out=acc[:], in_=grad[:, h, offset : offset + TOKENS], func=ACT.Copy, scale=table[:, row, h : h + 1]
-            )
-            return [(acc, 0)] + parts
+            for h in heads_of(pair):
+                acc = sums.tile([P, TOKENS], F32)
+                nc.scalar.activation(
+                    out=acc[:], in_=grad[h][:, offset : offset + TOKENS], func=ACT.Copy, scale=table[:, row, h : h + 1]
+                )
+                parts.append([(acc, 0)])
+            for head_parts, h in zip(parts, heads_of(pair)):
+                for offset, table, row in fine_taps[:PRODUCT_TAPS]:
+                    product = terms.tile([P, TOKENS + ZERO_PAD], F32)
+                    nc.scalar.activation(out=product[:], in_=grad[h][:, :], func=ACT.Copy, scale=table[:, row, h : h + 1])
+                    head_parts.append((product, offset))
+            return parts
 
         def transposed_classes(h):
-            words = grad[:, h, 0:TOKENS].bitcast(F32)
+            words = grad[h][:, 0:TOKENS].bitcast(F32)
             classes_ps = psum_c.tile([P, STRIDE // 2, P], F32)
             for w in range(STRIDE // 2):
                 nc.tensor.transpose(classes_ps[:, w, :], words[:, w : TOKENS // 2 : STRIDE // 2], identity[:])
@@ -242,17 +251,18 @@ def tile_causalwaveletfieldattentionbyte_pa_v_kernel(
             return (2 * pair, 2 * pair + 1)
 
         PAIRS = HEADS // 2
-        parts = {0: [scalar_products(h) for h in heads_of(0)]}
+        parts = {0: scalar_products(0)}
         banks = {0: [band_sums(h, transposed_classes(h)) for h in heads_of(0)]}
-        for s in range(PASSES):
-            quantise_x(s)
-
         for pair in range(PAIRS + 1):
             filtering = pair < PAIRS
             preparing = pair + 1 < PAIRS
             finishing = pair >= 1
             if preparing:
-                parts[pair + 1] = [scalar_products(h) for h in heads_of(pair + 1)]
+                parts[pair + 1] = scalar_products(pair + 1)
+            for s in range(2 * pair, min(2 * pair + 2, PASSES)):
+                quantise_x(s)
+                if s + 2 < PASSES:
+                    load_x(s + 2)
             if filtering:
                 accs = [head_parts[0][0] for head_parts in parts[pair]]
             if finishing:
@@ -278,3 +288,6 @@ def tile_causalwaveletfieldattentionbyte_pa_v_kernel(
                     add_band_sums(acc, head_banks)
             if preparing:
                 banks[pair + 1] = [band_sums(h, c) for h, c in zip(heads_of(pair + 1), classes)]
+            if pair + 3 < PAIRS:
+                for h in heads_of(pair + 3):
+                    load_head(h)

@@ -28,7 +28,7 @@ BAND_COLS = MX_FLOPS // 10 // (HEADS * STRIDE * 2 * P * P) // 2 * 2
 BAND_TOKENS = STRIDE * BAND_COLS
 BANK_CLASSES = 4
 ROW = 232
-PRODUCT_TAPS = 3
+PRODUCT_TAPS = 2
 ZERO_PAD = 16
 TAP0, TAP1, TAP2, TAP3 = 0.4829629131445341, 0.8365163037378079, 0.2241438680420134, -0.1294095225512604
 

@@ -28,7 +28,7 @@ BAND_COLS = MX_FLOPS // 10 // (HEADS * STRIDE * 2 * P * P) // 2 * 2
 BAND_TOKENS = STRIDE * BAND_COLS
 BANK_CLASSES = 4
 ROW = 232
-PRODUCT_TAPS = 2
+PRODUCT_TAPS = 4
 ZERO_PAD = 16
 TAP0, TAP1, TAP2, TAP3 = 0.4829629131445341, 0.8365163037378079, 0.2241438680420134, -0.1294095225512604
 
@@ -42,10 +42,10 @@ def tile_causalwaveletfieldattentionbyte_pa_v_kernel(
     nc = tc.nc
     with ExitStack() as ctx:
         keep = ctx.enter_context(tc.tile_pool(name="keep", bufs=1))
-        sums = ctx.enter_context(tc.tile_pool(name="sums", bufs=6))
+        sums = ctx.enter_context(tc.tile_pool(name="sums", bufs=4))
         stage = ctx.enter_context(tc.tile_pool(name="stage", bufs=2))
         heads_in = ctx.enter_context(tc.tile_pool(name="heads_in", bufs=6))
-        terms = ctx.enter_context(tc.tile_pool(name="terms", bufs=6 * PRODUCT_TAPS))
+        terms = ctx.enter_context(tc.tile_pool(name="terms", bufs=4 * PRODUCT_TAPS))
         psum_c = ctx.enter_context(tc.psum_pool(name="psum_c", bufs=1))
         psum_b = ctx.enter_context(tc.psum_pool(name="psum_b", bufs=4))
         psum_t = ctx.enter_context(tc.psum_pool(name="psum_t", bufs=2))
@@ -121,34 +121,48 @@ def tile_causalwaveletfieldattentionbyte_pa_v_kernel(
         fine_taps = [tap for tap in taps if tap[0] % STRIDE != 0]
         band_taps = [tap for tap in taps if tap[0] % STRIDE == 0]
 
-        pitch = (HEADS + 1) * ROW
         scratch = out.rearrange("c i -> (c i)")
-        rows = keep.tile([P, HEADS + 1, ROW], F32)
-        nc.vector.memset(rows[:], 0.0)
-        for offset, table, row in band_taps:
-            nc.vector.tensor_copy(out=rows[:, 0:HEADS, CLASS_TOKENS - 1 - offset // STRIDE], in_=table[:, row, :])
-        nc.gpsimd.dma_start(
-            out=scratch[0 : P * pitch].rearrange("(p w) -> p w", w=pitch), in_=rows[:].rearrange("p h l -> p (h l)")
-        )
-        skewed = scratch[P - 1 : P - 1 + P * (pitch - 1)].rearrange("(p w) -> p w", w=pitch - 1)
-        band = keep.tile([P, HEADS, BAND_COLS], F32)
-        nc.gpsimd.dma_start(
-            out=band[:], in_=skewed[:, 0 : HEADS * ROW].rearrange("p (h l) -> p h l", l=ROW)[:, :, 0:BAND_COLS]
-        )
+        band_of = {}
+        used = 0
+        for group in (slice(0, 2), slice(2, HEADS)):
+            heads = group.stop - group.start
+            pitch = (heads + 1) * ROW
+            rows = keep.tile([P, heads + 1, ROW], F32, name=f"rows{group.start}")
+            nc.gpsimd.memset(rows[:], 0.0)
+            for offset, table, row in band_taps:
+                nc.vector.tensor_copy(out=rows[:, 0:heads, CLASS_TOKENS - 1 - offset // STRIDE], in_=table[:, row, group])
+            nc.gpsimd.dma_start(
+                out=scratch[used : used + P * pitch].rearrange("(p w) -> p w", w=pitch),
+                in_=rows[:].rearrange("p h l -> p (h l)"),
+            )
+            skewed = scratch[used + P - 1 : used + P - 1 + P * (pitch - 1)].rearrange("(p w) -> p w", w=pitch - 1)
+            band = keep.tile([P, heads, BAND_COLS], F32, name=f"band{group.start}")
+            nc.gpsimd.dma_start(
+                out=band[:],
+                in_=skewed[:, 0 : heads * ROW].rearrange("p (h l) -> p h l", l=ROW)[:, :, 0:BAND_COLS],
+            )
+            for h in range(group.start, group.stop):
+                band_of[h] = band[:, h - group.start, :]
+            used += P * pitch
 
         x_codes = keep.tile([P, PASSES, WIDTH], U32, align_bytes=64)
         x_scales = keep.tile([P, PASSES, WIDTH], U8, align_bytes=64)
 
-        def quantise_x(s):
-            x_grouped = stage.tile([P, WIDTH, PACK], BF16, align_bytes=64)
-            nc.scalar.copy(
-                out=x_grouped[:].rearrange("p (c i) t -> p c t i", i=4),
+        x_grouped = {}
+
+        def regroup_x(s):
+            x_grouped[s] = stage.tile([P, WIDTH, PACK], BF16, align_bytes=64, name="x_grouped")
+            copy = nc.vector.tensor_copy if s < 2 else nc.scalar.copy
+            copy(
+                out=x_grouped[s][:].rearrange("p (c i) t -> p c t i", i=4),
                 in_=x_raw[s][:].rearrange("p t (c i) -> p c t i", i=4),
             )
+
+        def quantise_x(s):
             nc.vector.quantize_mx(
                 out=x_codes[:, s, :].bitcast(E4M3X4),
                 scales=x_scales[:, s, :],
-                in_=x_grouped[:].rearrange("p c t -> p (c t)"),
+                in_=x_grouped[s][:].rearrange("p c t -> p (c t)"),
             )
 
         def add_tap(acc, h, offset, weight, first):
@@ -160,19 +174,21 @@ def tile_causalwaveletfieldattentionbyte_pa_v_kernel(
 
         def scalar_products(pair):
             parts = []
-            offset, table, row = fine_taps[PRODUCT_TAPS]
             for h in heads_of(pair):
-                acc = sums.tile([P, TOKENS], F32)
-                nc.scalar.activation(
-                    out=acc[:], in_=grad[h][:, offset : offset + TOKENS], func=ACT.Copy, scale=table[:, row, h : h + 1]
-                )
-                parts.append([(acc, 0)])
-            for head_parts, h in zip(parts, heads_of(pair)):
+                head_parts = []
                 for offset, table, row in fine_taps[:PRODUCT_TAPS]:
                     product = terms.tile([P, TOKENS + ZERO_PAD], F32)
                     nc.scalar.activation(out=product[:], in_=grad[h][:, :], func=ACT.Copy, scale=table[:, row, h : h + 1])
                     head_parts.append((product, offset))
+                parts.append(head_parts)
             return parts
+
+        def start_tail(acc, h):
+            offset, table, row = fine_taps[PRODUCT_TAPS]
+            nc.vector.tensor_scalar_mul(
+                out=acc[:, BAND_TOKENS:TOKENS], in0=grad[h][:, BAND_TOKENS + offset : TOKENS + offset],
+                scalar1=table[:, row, h : h + 1],
+            )
 
         def transposed_classes(h):
             words = grad[h][:, 0:TOKENS].bitcast(F32)
@@ -192,35 +208,38 @@ def tile_causalwaveletfieldattentionbyte_pa_v_kernel(
                 band_ps = psum_b.tile([P, BANK_CLASSES, BAND_COLS], F32)
                 for r in range(BANK_CLASSES):
                     nc.tensor.matmul(
-                        out=band_ps[:, r, :], lhsT=classes[:, bank * BANK_CLASSES + r, :], rhs=band[:, h, :],
+                        out=band_ps[:, r, :], lhsT=classes[:, bank * BANK_CLASSES + r, :], rhs=band_of[h],
                         start=True, stop=True,
                     )
                 banks.append(band_ps)
             return banks
 
-        def add_band_sums(acc, banks):
+        def start_from_band(acc, h, band_ps, bank):
+            offset, table, row = fine_taps[PRODUCT_TAPS]
             by_class = acc[:, 0:BAND_TOKENS].rearrange("p (q r) -> p q r", r=STRIDE)
-            for bank, band_ps in enumerate(banks):
-                part = by_class[:, :, bank * BANK_CLASSES : (bank + 1) * BANK_CLASSES]
-                nc.vector.tensor_tensor(out=part, in0=part, in1=band_ps[:].rearrange("p r q -> p q r"), op=ALU.add)
+            shifted = grad[h][:, offset : offset + BAND_TOKENS].rearrange("p (q r) -> p q r", r=STRIDE)
+            of_bank = slice(bank * BANK_CLASSES, (bank + 1) * BANK_CLASSES)
+            nc.vector.scalar_tensor_tensor(
+                out=by_class[:, :, of_bank], in0=shifted[:, :, of_bank], scalar=table[:, row, h : h + 1],
+                in1=band_ps[:].rearrange("p r q -> p q r"), op0=ALU.mult, op1=ALU.add,
+            )
 
-        def turn_and_scale(h, head_parts, dv_cols):
-            for g in range(PASSES_PER_BATCH):
-                turned = psum_t.tile([P, PACK, P], F32)
-                for t in range(PACK):
-                    first = g * K_PASS + t * P
-                    for i, (part, offset) in enumerate(head_parts):
-                        nc.tensor.matmul(
-                            out=turned[:, t, :], lhsT=part[:, first + offset : first + offset + P], rhs=identity[:],
-                            is_transpose=True, start=(i == 0), stop=(i == len(head_parts) - 1),
-                        )
-                kmag_g = kmag[:, :, h].rearrange("p (b g t) -> p b g t", b=BATCH, t=PACK)[:, :, g, :]
-                nc.vector.tensor_tensor(
-                    out=dv_cols[:, g::PASSES_PER_BATCH, :, :],
-                    in0=turned[:].rearrange("p t (b c) -> p b c t", b=BATCH),
-                    in1=kmag_g.unsqueeze(2).to_broadcast([P, BATCH, HEAD_DIM, PACK]),
-                    op=ALU.mult,
-                )
+        def turn_and_scale(h, head_parts, dv_cols, g):
+            turned = psum_t.tile([P, PACK, P], F32)
+            for t in range(PACK):
+                first = g * K_PASS + t * P
+                for i, (part, offset) in enumerate(head_parts):
+                    nc.tensor.matmul(
+                        out=turned[:, t, :], lhsT=part[:, first + offset : first + offset + P], rhs=identity[:],
+                        is_transpose=True, start=(i == 0), stop=(i == len(head_parts) - 1),
+                    )
+            kmag_g = kmag[:, :, h].rearrange("p (b g t) -> p b g t", b=BATCH, t=PACK)[:, :, g, :]
+            nc.vector.tensor_tensor(
+                out=dv_cols[:, g::PASSES_PER_BATCH, :, :],
+                in0=turned[:].rearrange("p t (b c) -> p b c t", b=BATCH),
+                in1=kmag_g.unsqueeze(2).to_broadcast([P, BATCH, HEAD_DIM, PACK]),
+                op=ALU.mult,
+            )
 
         def multiply(pair, dv_grouped):
             dv_codes = stage.tile([P, PASSES * P], U32, align_bytes=64)
@@ -251,41 +270,69 @@ def tile_causalwaveletfieldattentionbyte_pa_v_kernel(
             return (2 * pair, 2 * pair + 1)
 
         PAIRS = HEADS // 2
-        parts = {0: scalar_products(0)}
+        parts = {}
         banks = {0: [band_sums(h, transposed_classes(h)) for h in heads_of(0)]}
         for pair in range(PAIRS + 1):
             filtering = pair < PAIRS
             preparing = pair + 1 < PAIRS
             finishing = pair >= 1
-            if preparing:
-                parts[pair + 1] = scalar_products(pair + 1)
+            if filtering:
+                parts[pair] = scalar_products(pair)
             for s in range(2 * pair, min(2 * pair + 2, PASSES)):
-                quantise_x(s)
+                regroup_x(s)
                 if s + 2 < PASSES:
                     load_x(s + 2)
+            short = []
+            long = []
             if filtering:
-                accs = [head_parts[0][0] for head_parts in parts[pair]]
+                accs = [sums.tile([P, TOKENS], F32, name="acc") for h in heads_of(pair)]
+                short.append([lambda acc=acc, h=h: start_tail(acc, h) for acc, h in zip(accs, heads_of(pair))])
+                for offset, table, row in band_taps:
+                    if BAND_TOKENS + offset < TOKENS:
+                        short.append([
+                            lambda acc=acc, h=h, o=offset, w=table[:, row, h : h + 1]: add_tap(acc, h, o, w, BAND_TOKENS)
+                            for acc, h in zip(accs, heads_of(pair))
+                        ])
+                starts = [
+                    [lambda acc=acc, h=h, b=b, k=k: start_from_band(acc, h, b, k) for k, b in enumerate(head_banks)]
+                    for acc, h, head_banks in zip(accs, heads_of(pair), banks[pair])
+                ]
             if finishing:
                 dv_grouped = stage.tile([P, PASSES, P, PACK], BF16, align_bytes=64)
-                turn_and_scale(heads_of(pair - 1)[0], parts[pair - 1][0], dv_grouped[:, :, 0:HEAD_DIM, :])
+                turns = [
+                    [
+                        lambda h=h, p=p, g=g, d=dv_grouped[:, :, i * HEAD_DIM : (i + 1) * HEAD_DIM, :]: turn_and_scale(h, p, d, g)
+                        for g in range(PASSES_PER_BATCH)
+                    ]
+                    for i, (h, p) in enumerate(zip(heads_of(pair - 1), parts[pair - 1]))
+                ]
+            if filtering and finishing:
+                long = starts[0] + turns[0] + starts[1] + turns[1]
+            elif filtering:
+                long = []
+            else:
+                long = turns[0] + turns[1]
+            for i in range(max(len(short), len(long))):
+                if i < len(short):
+                    for step in short[i]:
+                        step()
+                if i < len(long):
+                    long[i]()
+                if i == 3 and preparing:
+                    classes = [transposed_classes(h) for h in heads_of(pair + 1)]
+            if filtering and not finishing:
+                for step in starts[0] + starts[1]:
+                    step()
+            for s in range(2 * pair, min(2 * pair + 2, PASSES)):
+                quantise_x(s)
             if filtering:
                 for offset, table, row in fine_taps[PRODUCT_TAPS + 1 :]:
                     for acc, h in zip(accs, heads_of(pair)):
                         add_tap(acc, h, offset, table[:, row, h : h + 1], 0)
-            if preparing:
-                classes = [transposed_classes(h) for h in heads_of(pair + 1)]
-            if finishing:
-                turn_and_scale(heads_of(pair - 1)[1], parts[pair - 1][1], dv_grouped[:, :, HEAD_DIM:P, :])
-            if filtering:
-                for offset, table, row in band_taps:
-                    if BAND_TOKENS + offset < TOKENS:
-                        for acc, h in zip(accs, heads_of(pair)):
-                            add_tap(acc, h, offset, table[:, row, h : h + 1], BAND_TOKENS)
+                for acc, head_parts in zip(accs, parts[pair]):
+                    head_parts.append((acc, 0))
             if finishing:
                 multiply(pair - 1, dv_grouped)
-            if filtering:
-                for acc, head_banks in zip(accs, banks[pair]):
-                    add_band_sums(acc, head_banks)
             if preparing:
                 banks[pair + 1] = [band_sums(h, c) for h, c in zip(heads_of(pair + 1), classes)]
             if pair + 3 < PAIRS:

@@ -28,7 +28,7 @@ BAND_COLS = MX_FLOPS // 10 // (HEADS * STRIDE * 2 * P * P) // 2 * 2
 BAND_TOKENS = STRIDE * BAND_COLS
 BANK_CLASSES = 4
 ROW = 232
-PRODUCT_TAPS = 4
+PRODUCT_TAPS = 3
 ZERO_PAD = 16
 TAP0, TAP1, TAP2, TAP3 = 0.4829629131445341, 0.8365163037378079, 0.2241438680420134, -0.1294095225512604
 
@@ -44,8 +44,9 @@ def tile_causalwaveletfieldattentionbyte_pa_v_kernel(
         keep = ctx.enter_context(tc.tile_pool(name="keep", bufs=1))
         sums = ctx.enter_context(tc.tile_pool(name="sums", bufs=4))
         stage = ctx.enter_context(tc.tile_pool(name="stage", bufs=2))
-        heads_in = ctx.enter_context(tc.tile_pool(name="heads_in", bufs=6))
+        heads_in = ctx.enter_context(tc.tile_pool(name="heads_in", bufs=8))
         terms = ctx.enter_context(tc.tile_pool(name="terms", bufs=4 * PRODUCT_TAPS))
+        class_pool = ctx.enter_context(tc.tile_pool(name="class_pool", bufs=4))
         psum_c = ctx.enter_context(tc.psum_pool(name="psum_c", bufs=1))
         psum_b = ctx.enter_context(tc.psum_pool(name="psum_b", bufs=4))
         psum_t = ctx.enter_context(tc.psum_pool(name="psum_t", bufs=2))
@@ -78,7 +79,7 @@ def tile_causalwaveletfieldattentionbyte_pa_v_kernel(
 
         load_x(0)
         load_x(1)
-        for h in range(2, 6):
+        for h in range(2, 8):
             load_head(h)
 
         identity = keep.tile([P, P], F32)
@@ -172,16 +173,13 @@ def tile_causalwaveletfieldattentionbyte_pa_v_kernel(
                 in1=acc[:, first:last], op0=ALU.mult, op1=ALU.add,
             )
 
-        def scalar_products(pair):
-            parts = []
-            for h in heads_of(pair):
-                head_parts = []
-                for offset, table, row in fine_taps[:PRODUCT_TAPS]:
-                    product = terms.tile([P, TOKENS + ZERO_PAD], F32)
-                    nc.scalar.activation(out=product[:], in_=grad[h][:, :], func=ACT.Copy, scale=table[:, row, h : h + 1])
-                    head_parts.append((product, offset))
-                parts.append(head_parts)
-            return parts
+        def scalar_products(h):
+            products = []
+            for offset, table, row in fine_taps[:PRODUCT_TAPS]:
+                product = terms.tile([P, TOKENS + ZERO_PAD], F32)
+                nc.scalar.activation(out=product[:], in_=grad[h][:, :], func=ACT.Copy, scale=table[:, row, h : h + 1])
+                products.append((product, offset))
+            return products
 
         def start_tail(acc, h):
             offset, table, row = fine_taps[PRODUCT_TAPS]
@@ -195,146 +193,152 @@ def tile_causalwaveletfieldattentionbyte_pa_v_kernel(
             classes_ps = psum_c.tile([P, STRIDE // 2, P], F32)
             for w in range(STRIDE // 2):
                 nc.tensor.transpose(classes_ps[:, w, :], words[:, w : TOKENS // 2 : STRIDE // 2], identity[:])
-            classes = stage.tile([P, STRIDE, P], F32)
+            classes[h] = class_pool.tile([P, STRIDE, P], F32, name="classes")
             nc.scalar.copy(
-                out=classes[:].rearrange("p (w e) c -> p w e c", e=2),
+                out=classes[h][:].rearrange("p (w e) c -> p w e c", e=2),
                 in_=classes_ps[:].bitcast(BF16).rearrange("p w (c e) -> p w e c", e=2),
             )
-            return classes
 
-        def band_sums(h, classes):
-            banks = []
-            for bank in range(STRIDE // BANK_CLASSES):
-                band_ps = psum_b.tile([P, BANK_CLASSES, BAND_COLS], F32)
-                for r in range(BANK_CLASSES):
-                    nc.tensor.matmul(
-                        out=band_ps[:, r, :], lhsT=classes[:, bank * BANK_CLASSES + r, :], rhs=band_of[h],
-                        start=True, stop=True,
-                    )
-                banks.append(band_ps)
-            return banks
+        def band_sum(h, r):
+            if r % BANK_CLASSES == 0:
+                banks[h, r // BANK_CLASSES] = psum_b.tile([P, BANK_CLASSES, BAND_COLS], F32, name="band_ps")
+            nc.tensor.matmul(
+                out=banks[h, r // BANK_CLASSES][:, r % BANK_CLASSES, :], lhsT=classes[h][:, r, :], rhs=band_of[h],
+                start=True, stop=True,
+            )
 
-        def start_from_band(acc, h, band_ps, bank):
+        def start_from_band(acc, h, bank):
             offset, table, row = fine_taps[PRODUCT_TAPS]
             by_class = acc[:, 0:BAND_TOKENS].rearrange("p (q r) -> p q r", r=STRIDE)
             shifted = grad[h][:, offset : offset + BAND_TOKENS].rearrange("p (q r) -> p q r", r=STRIDE)
             of_bank = slice(bank * BANK_CLASSES, (bank + 1) * BANK_CLASSES)
             nc.vector.scalar_tensor_tensor(
                 out=by_class[:, :, of_bank], in0=shifted[:, :, of_bank], scalar=table[:, row, h : h + 1],
-                in1=band_ps[:].rearrange("p r q -> p q r"), op0=ALU.mult, op1=ALU.add,
+                in1=banks[h, bank][:].rearrange("p r q -> p q r"), op0=ALU.mult, op1=ALU.add,
             )
 
-        def turn_and_scale(h, head_parts, dv_cols, g):
-            turned = psum_t.tile([P, PACK, P], F32)
-            for t in range(PACK):
-                first = g * K_PASS + t * P
-                for i, (part, offset) in enumerate(head_parts):
-                    nc.tensor.matmul(
-                        out=turned[:, t, :], lhsT=part[:, first + offset : first + offset + P], rhs=identity[:],
-                        is_transpose=True, start=(i == 0), stop=(i == len(head_parts) - 1),
-                    )
+        def turn(h, g, t):
+            if t == 0:
+                turned[h, g] = psum_t.tile([P, PACK, P], F32, name="turned")
+            first = g * K_PASS + t * P
+            for i, (part, offset) in enumerate(parts[h]):
+                nc.tensor.matmul(
+                    out=turned[h, g][:, t, :], lhsT=part[:, first + offset : first + offset + P], rhs=identity[:],
+                    is_transpose=True, start=(i == 0), stop=(i == len(parts[h]) - 1),
+                )
+
+        def scale(h, g):
+            if h % 2 == 0 and g == 0:
+                dv_grouped[h // 2] = stage.tile([P, PASSES, P, PACK], BF16, align_bytes=64, name="dv_grouped")
+            first = h % 2 * HEAD_DIM
             kmag_g = kmag[:, :, h].rearrange("p (b g t) -> p b g t", b=BATCH, t=PACK)[:, :, g, :]
             nc.vector.tensor_tensor(
-                out=dv_cols[:, g::PASSES_PER_BATCH, :, :],
-                in0=turned[:].rearrange("p t (b c) -> p b c t", b=BATCH),
+                out=dv_grouped[h // 2][:, g::PASSES_PER_BATCH, first : first + HEAD_DIM, :],
+                in0=turned[h, g][:].rearrange("p t (b c) -> p b c t", b=BATCH),
                 in1=kmag_g.unsqueeze(2).to_broadcast([P, BATCH, HEAD_DIM, PACK]),
                 op=ALU.mult,
             )
 
-        def multiply(pair, dv_grouped):
-            dv_codes = stage.tile([P, PASSES * P], U32, align_bytes=64)
-            dv_scales = stage.tile([P, PASSES * P], U8, align_bytes=64)
+        def quantise_dv(pair):
+            codes = stage.tile([P, PASSES * P], U32, align_bytes=64, name="dv_codes")
+            scales = stage.tile([P, PASSES * P], U8, align_bytes=64, name="dv_scales")
             nc.vector.quantize_mx(
-                out=dv_codes[:].bitcast(E5M2X4),
-                scales=dv_scales[:],
-                in_=dv_grouped[:].rearrange("p s c t -> p (s c t)"),
+                out=codes[:].bitcast(E5M2X4), scales=scales[:], in_=dv_grouped[pair][:].rearrange("p s c t -> p (s c t)")
             )
-            result = stage.tile([P, WIDTH], F32)
-            for half in range(WIDTH // N_TILE):
-                cols = slice(half * N_TILE, (half + 1) * N_TILE)
-                product = psum_o.tile([P, N_TILE], F32)
-                for s in range(PASSES):
-                    nc.tensor.matmul_mx(
-                        out=product[:],
-                        lhsT=dv_codes[:, s * P : (s + 1) * P].bitcast(E5M2X4),
-                        lhsT_scale=dv_scales[:, s * P : (s + 1) * P],
-                        rhs=x_codes[:, s, cols].bitcast(E4M3X4),
-                        rhs_scale=x_scales[:, s, cols],
-                        start=(s == 0),
-                        stop=(s == PASSES - 1),
-                    )
-                nc.scalar.copy(out=result[:, cols], in_=product[:])
-            nc.sync.dma_start(out=out[pair * P : (pair + 1) * P, :], in_=result[:])
+            dv_codes[pair] = codes
+            dv_scales[pair] = scales
+
+        def multiply(pair, half):
+            if half == 0:
+                result[pair] = stage.tile([P, WIDTH], F32, name="result")
+            cols = slice(half * N_TILE, (half + 1) * N_TILE)
+            product = psum_o.tile([P, N_TILE], F32)
+            for s in range(PASSES):
+                nc.tensor.matmul_mx(
+                    out=product[:],
+                    lhsT=dv_codes[pair][:, s * P : (s + 1) * P].bitcast(E5M2X4),
+                    lhsT_scale=dv_scales[pair][:, s * P : (s + 1) * P],
+                    rhs=x_codes[:, s, cols].bitcast(E4M3X4),
+                    rhs_scale=x_scales[:, s, cols],
+                    start=(s == 0),
+                    stop=(s == PASSES - 1),
+                )
+            nc.scalar.copy(out=result[pair][:, cols], in_=product[:])
+            if cols.stop == WIDTH:
+                nc.sync.dma_start(out=out[pair * P : (pair + 1) * P, :], in_=result[pair][:])
 
         def heads_of(pair):
             return (2 * pair, 2 * pair + 1)
 
         PAIRS = HEADS // 2
         parts = {}
-        banks = {0: [band_sums(h, transposed_classes(h)) for h in heads_of(0)]}
-        for pair in range(PAIRS + 1):
-            filtering = pair < PAIRS
-            preparing = pair + 1 < PAIRS
-            finishing = pair >= 1
+        classes = {}
+        banks = {}
+        turned = {}
+        dv_grouped = {}
+        dv_codes = {}
+        dv_scales = {}
+        result = {}
+        ctx.enter_context(tc.manual_schedule(engines={mybir.EngineType.PE}))
+        for h in range(4):
+            transposed_classes(h)
+        for h in range(2):
+            for r in range(STRIDE):
+                band_sum(h, r)
+        for rnd in range(PAIRS + 2):
+            filtering = rnd < PAIRS
+            preparing = rnd + 1 < PAIRS
+            loading = rnd + 2 < PAIRS
+            turning = 1 <= rnd <= PAIRS
+            multiplying = rnd >= 2
+            accs = {}
             if filtering:
-                parts[pair] = scalar_products(pair)
-            for s in range(2 * pair, min(2 * pair + 2, PASSES)):
+                for h in heads_of(rnd):
+                    parts[h] = scalar_products(h)
+                    accs[h] = sums.tile([P, TOKENS], F32, name="acc")
+            for s in range(2 * rnd, min(2 * rnd + 2, PASSES)):
                 regroup_x(s)
                 if s + 2 < PASSES:
                     load_x(s + 2)
-            short = []
-            long = []
+
+            quarters = [[], [], [], []]
             if filtering:
-                accs = [sums.tile([P, TOKENS], F32, name="acc") for h in heads_of(pair)]
-                short.append([lambda acc=acc, h=h: start_tail(acc, h) for acc, h in zip(accs, heads_of(pair))])
+                tails = [[(start_tail, acc, h) for h, acc in accs.items()]]
                 for offset, table, row in band_taps:
                     if BAND_TOKENS + offset < TOKENS:
-                        short.append([
-                            lambda acc=acc, h=h, o=offset, w=table[:, row, h : h + 1]: add_tap(acc, h, o, w, BAND_TOKENS)
-                            for acc, h in zip(accs, heads_of(pair))
-                        ])
-                starts = [
-                    [lambda acc=acc, h=h, b=b, k=k: start_from_band(acc, h, b, k) for k, b in enumerate(head_banks)]
-                    for acc, h, head_banks in zip(accs, heads_of(pair), banks[pair])
-                ]
-            if finishing:
-                dv_grouped = stage.tile([P, PASSES, P, PACK], BF16, align_bytes=64)
-                turns = [
-                    [
-                        lambda h=h, p=p, g=g, d=dv_grouped[:, :, i * HEAD_DIM : (i + 1) * HEAD_DIM, :]: turn_and_scale(h, p, d, g)
-                        for g in range(PASSES_PER_BATCH)
-                    ]
-                    for i, (h, p) in enumerate(zip(heads_of(pair - 1), parts[pair - 1]))
-                ]
-            if filtering and finishing:
-                long = starts[0] + turns[0] + starts[1] + turns[1]
-            elif filtering:
-                long = []
-            else:
-                long = turns[0] + turns[1]
-            for i in range(max(len(short), len(long))):
-                if i < len(short):
-                    for step in short[i]:
-                        step()
-                if i < len(long):
-                    long[i]()
-                if i == 3 and preparing:
-                    classes = [transposed_classes(h) for h in heads_of(pair + 1)]
-            if filtering and not finishing:
-                for step in starts[0] + starts[1]:
-                    step()
-            for s in range(2 * pair, min(2 * pair + 2, PASSES)):
-                quantise_x(s)
-            if filtering:
-                for offset, table, row in fine_taps[PRODUCT_TAPS + 1 :]:
-                    for acc, h in zip(accs, heads_of(pair)):
-                        add_tap(acc, h, offset, table[:, row, h : h + 1], 0)
-                for acc, head_parts in zip(accs, parts[pair]):
-                    head_parts.append((acc, 0))
-            if finishing:
-                multiply(pair - 1, dv_grouped)
+                        tails.append([(add_tap, acc, h, offset, table[:, row, h : h + 1], BAND_TOKENS) for h, acc in accs.items()])
+                starts = [(start_from_band, acc, h, k) for h, acc in accs.items() for k in range(STRIDE // BANK_CLASSES)]
+                for i, pair_of_taps in enumerate(tails):
+                    if i < len(starts):
+                        quarters[i // 6].append(starts[i])
+                    quarters[i // 6].extend(pair_of_taps)
+                for i, (offset, table, row) in enumerate(fine_taps[PRODUCT_TAPS + 1 :]):
+                    quarters[2 + i % 2].extend((add_tap, acc, h, offset, table[:, row, h : h + 1], 0) for h, acc in accs.items())
+            for i, quarter in enumerate(quarters):
+                h_turned, g_turned = 2 * (rnd - 1) + i // PASSES_PER_BATCH, i % PASSES_PER_BATCH
+                for step in quarter:
+                    step[0](*step[1:])
+                if i == 0 and 0 <= rnd - 2:
+                    quantise_dv(rnd - 2)
+                for t in range(PACK):
+                    if turning:
+                        turn(h_turned, g_turned, t)
+                    k = i * PACK + t - 1
+                    if preparing and k >= 0:
+                        band_sum(2 * (rnd + 1) + k // STRIDE, k % STRIDE)
+                if turning:
+                    scale(h_turned, g_turned)
+                if multiplying and i in (1, 2):
+                    multiply(rnd - 2, i - 1)
+                if loading and i in (1, 3):
+                    transposed_classes(2 * (rnd + 2) + i // 2)
+                if rnd < 2:
+                    if i % 2 == 1:
+                        quantise_x(2 * rnd + i // 2)
             if preparing:
-                banks[pair + 1] = [band_sums(h, c) for h, c in zip(heads_of(pair + 1), classes)]
-            if pair + 3 < PAIRS:
-                for h in heads_of(pair + 3):
+                band_sum(2 * (rnd + 1) + 1, STRIDE - 1)
+            for h, acc in accs.items():
+                parts[h].append((acc, 0))
+            if rnd + 4 < PAIRS:
+                for h in heads_of(rnd + 4):
                     load_head(h)

@@ -176,9 +176,11 @@ def tile_causalwaveletfieldattentionbyte_pa_v_kernel(
         def scalar_products(h):
             products = []
             for offset, table, row in fine_taps[:PRODUCT_TAPS]:
-                product = terms.tile([P, TOKENS + ZERO_PAD], F32)
-                nc.scalar.activation(out=product[:], in_=grad[h][:, :], func=ACT.Copy, scale=table[:, row, h : h + 1])
-                products.append((product, offset))
+                product = terms.tile([P, TOKENS], F32)
+                nc.scalar.activation(
+                    out=product[:], in_=grad[h][:, offset : offset + TOKENS], func=ACT.Copy, scale=table[:, row, h : h + 1]
+                )
+                products.append(product)
             return products
 
         def start_tail(acc, h):
@@ -221,9 +223,9 @@ def tile_causalwaveletfieldattentionbyte_pa_v_kernel(
             if t == 0:
                 turned[h, g] = psum_t.tile([P, PACK, P], F32, name="turned")
             first = g * K_PASS + t * P
-            for i, (part, offset) in enumerate(parts[h]):
+            for i, part in enumerate(parts[h]):
                 nc.tensor.matmul(
-                    out=turned[h, g][:, t, :], lhsT=part[:, first + offset : first + offset + P], rhs=identity[:],
+                    out=turned[h, g][:, t, :], lhsT=part[:, first : first + P], rhs=identity[:],
                     is_transpose=True, start=(i == 0), stop=(i == len(parts[h]) - 1),
                 )
 
@@ -338,7 +340,7 @@ def tile_causalwaveletfieldattentionbyte_pa_v_kernel(
             if preparing:
                 band_sum(2 * (rnd + 1) + 1, STRIDE - 1)
             for h, acc in accs.items():
-                parts[h].append((acc, 0))
+                parts[h].append(acc)
             if rnd + 4 < PAIRS:
                 for h in heads_of(rnd + 4):
                     load_head(h)

@@ -28,7 +28,7 @@ BAND_COLS = MX_FLOPS // 10 // (HEADS * STRIDE * 2 * P * P) // 2 * 2
 BAND_TOKENS = STRIDE * BAND_COLS
 BANK_CLASSES = 4
 ROW = 232
-PRODUCT_TAPS = 3
+PRODUCT_TAPS = 2
 ZERO_PAD = 16
 TAP0, TAP1, TAP2, TAP3 = 0.4829629131445341, 0.8365163037378079, 0.2241438680420134, -0.1294095225512604
 

@@ -24,12 +24,13 @@ N_TILE = 512
 STRIDE = 8
 CLASS_TOKENS = TOKENS // STRIDE
 MX_FLOPS = 2 * CHANNELS * BATCH * TOKENS * WIDTH
-BAND_COLS = MX_FLOPS // 10 // (HEADS * STRIDE * 2 * P * P) // 2 * 2
-BAND_TOKENS = STRIDE * BAND_COLS
-BANK_CLASSES = 4
-ROW = 232
-PRODUCT_TAPS = 2
+BAND_UNITS = MX_FLOPS // 10 // (2 * P * P * P)
+BAND_HEADS = -(-BAND_UNITS // STRIDE)
+ROW = 2 * P
 ZERO_PAD = 16
+CLASS_COLS = (TOKENS + ZERO_PAD) // STRIDE
+CLASS_PITCH = 136
+SHIFTED_COLS = P + 1
 TAP0, TAP1, TAP2, TAP3 = 0.4829629131445341, 0.8365163037378079, 0.2241438680420134, -0.1294095225512604
 
 FLOPS = 2 * CHANNELS * BATCH * TOKENS * WIDTH + 2 * 20 * CHANNELS * BATCH * TOKENS
@@ -42,15 +43,15 @@ def tile_causalwaveletfieldattentionbyte_pa_v_kernel(
     nc = tc.nc
     with ExitStack() as ctx:
         keep = ctx.enter_context(tc.tile_pool(name="keep", bufs=1))
-        sums = ctx.enter_context(tc.tile_pool(name="sums", bufs=4))
         stage = ctx.enter_context(tc.tile_pool(name="stage", bufs=2))
-        heads_in = ctx.enter_context(tc.tile_pool(name="heads_in", bufs=8))
-        terms = ctx.enter_context(tc.tile_pool(name="terms", bufs=4 * PRODUCT_TAPS))
+        heads_in = ctx.enter_context(tc.tile_pool(name="heads_in", bufs=6))
+        by_class_pool = ctx.enter_context(tc.tile_pool(name="by_class", bufs=5))
         class_pool = ctx.enter_context(tc.tile_pool(name="class_pool", bufs=4))
+        sums = ctx.enter_context(tc.tile_pool(name="sums", bufs=4))
+        terms = ctx.enter_context(tc.tile_pool(name="terms", bufs=12))
         psum_c = ctx.enter_context(tc.psum_pool(name="psum_c", bufs=1))
-        psum_b = ctx.enter_context(tc.psum_pool(name="psum_b", bufs=4))
-        psum_t = ctx.enter_context(tc.psum_pool(name="psum_t", bufs=2))
-        psum_o = ctx.enter_context(tc.psum_pool(name="psum_o", bufs=1))
+        psum_t = ctx.enter_context(tc.psum_pool(name="psum_t", bufs=5))
+        psum_o = ctx.enter_context(tc.psum_pool(name="psum_o", bufs=2))
 
         logits_bf = keep.tile([P, SCALES * HEADS], BF16)
         nc.sync.dma_start(out=logits_bf[:], in_=scale_gain.rearrange("j h -> (j h)").partition_broadcast(P))
@@ -66,24 +67,29 @@ def tile_causalwaveletfieldattentionbyte_pa_v_kernel(
                     in_=grad_out[b, h * HEAD_DIM : (h + 1) * HEAD_DIM, :],
                 )
 
-        load_head(0)
-        load_head(1)
-        kmag = keep.tile([P, PASSES * PACK, HEADS], F32)
-        nc.sync.dma_start(out=kmag[:], in_=k_mag.rearrange("b (i p) h -> p (b i) h", p=P))
-        x_rows = x.rearrange("b (g t p) i -> (b g) p t i", t=PACK, p=P)
+        x_rows = x.rearrange("b (q g t) i -> b g q t i", g=PASSES_PER_BATCH, t=PACK)
         x_raw = {}
 
         def load_x(s):
             x_raw[s] = stage.tile([P, PACK, WIDTH], BF16, name="x_raw")
-            nc.sync.dma_start(out=x_raw[s][:], in_=x_rows[s])
+            nc.sync.dma_start(out=x_raw[s][:], in_=x_rows[s // PASSES_PER_BATCH, s % PASSES_PER_BATCH])
 
+        load_head(0)
+        load_head(1)
         load_x(0)
         load_x(1)
-        for h in range(2, 8):
+        kmag = keep.tile([P, BATCH, STRIDE, HEADS], F32)
+        nc.sync.dma_start(
+            out=kmag[:].rearrange("p b r h -> p b (r h)"), in_=k_mag.rearrange("b (q r) h -> q b (r h)", r=STRIDE)
+        )
+        load_order = [2, 3, 12, 13, 14, 15, 4, 5, 6, 7, 8, 9, 10, 11]
+        for h in load_order[:4]:
             load_head(h)
 
         identity = keep.tile([P, P], F32)
         make_identity(nc, identity[:])
+        identity_bf = keep.tile([P, P], BF16)
+        make_identity(nc, identity_bf[:])
 
         logits = keep.tile([P, SCALES, HEADS], F32)
         nc.vector.tensor_copy(out=logits[:].rearrange("p j h -> p (j h)"), in_=logits_bf[:])
@@ -119,28 +125,30 @@ def tile_causalwaveletfieldattentionbyte_pa_v_kernel(
         taps += [(2**m, w_pow, m) for m in range(SCALES)]
         taps += [(3 * 2**j, w_tri, j) for j in range(SCALES) if 3 * 2**j < TOKENS]
         taps = sorted(taps, key=lambda tap: tap[0])
-        fine_taps = [tap for tap in taps if tap[0] % STRIDE != 0]
+        fine_taps = {tap[0]: tap for tap in taps if tap[0] % STRIDE != 0}
         band_taps = [tap for tap in taps if tap[0] % STRIDE == 0]
+        product_taps = [fine_taps[offset] for offset in (1, 2, 3, 6)]
+        sum_taps = [fine_taps[offset] for offset in (4, 12)]
 
         scratch = out.rearrange("c i -> (c i)")
         band_of = {}
         used = 0
-        for group in (slice(0, 2), slice(2, HEADS)):
+        for group in (slice(0, 2), slice(2, BAND_HEADS)):
             heads = group.stop - group.start
             pitch = (heads + 1) * ROW
             rows = keep.tile([P, heads + 1, ROW], F32, name=f"rows{group.start}")
             nc.gpsimd.memset(rows[:], 0.0)
             for offset, table, row in band_taps:
-                nc.vector.tensor_copy(out=rows[:, 0:heads, CLASS_TOKENS - 1 - offset // STRIDE], in_=table[:, row, group])
+                nc.vector.tensor_copy(out=rows[:, 0:heads, P - 1 - offset // STRIDE], in_=table[:, row, group])
             nc.gpsimd.dma_start(
                 out=scratch[used : used + P * pitch].rearrange("(p w) -> p w", w=pitch),
                 in_=rows[:].rearrange("p h l -> p (h l)"),
             )
             skewed = scratch[used + P - 1 : used + P - 1 + P * (pitch - 1)].rearrange("(p w) -> p w", w=pitch - 1)
-            band = keep.tile([P, heads, BAND_COLS], F32, name=f"band{group.start}")
+            band = keep.tile([P, heads, P], F32, name=f"band{group.start}")
             nc.gpsimd.dma_start(
                 out=band[:],
-                in_=skewed[:, 0 : heads * ROW].rearrange("p (h l) -> p h l", l=ROW)[:, :, 0:BAND_COLS],
+                in_=skewed[:, 0 : heads * ROW].rearrange("p (h l) -> p h l", l=ROW)[:, :, 0:P],
             )
             for h in range(group.start, group.stop):
                 band_of[h] = band[:, h - group.start, :]
@@ -153,7 +161,7 @@ def tile_causalwaveletfieldattentionbyte_pa_v_kernel(
 
         def regroup_x(s):
             x_grouped[s] = stage.tile([P, WIDTH, PACK], BF16, align_bytes=64, name="x_grouped")
-            copy = nc.vector.tensor_copy if s < 2 else nc.scalar.copy
+            copy = nc.vector.tensor_copy if s % 2 == 1 else nc.scalar.copy
             copy(
                 out=x_grouped[s][:].rearrange("p (c i) t -> p c t i", i=4),
                 in_=x_raw[s][:].rearrange("p t (c i) -> p c t i", i=4),
@@ -166,74 +174,93 @@ def tile_causalwaveletfieldattentionbyte_pa_v_kernel(
                 in_=x_grouped[s][:].rearrange("p c t -> p (c t)"),
             )
 
-        def add_tap(acc, h, offset, weight, first):
-            last = TOKENS if offset <= ZERO_PAD else TOKENS - offset
-            nc.vector.scalar_tensor_tensor(
-                out=acc[:, first:last], in0=grad[h][:, first + offset : last + offset], scalar=weight,
-                in1=acc[:, first:last], op0=ALU.mult, op1=ALU.add,
+        def band_classes(h):
+            return min(max(BAND_UNITS - STRIDE * h, 0), STRIDE)
+
+        def split_classes(h):
+            tile = keep.tile([P, STRIDE, CLASS_PITCH], BF16, name=f"late{h}") if band_classes(h) < STRIDE else (
+                by_class_pool.tile([P, STRIDE, CLASS_PITCH], BF16, name="by_class")
+            )
+            by_class[h] = tile
+            nc.vector.tensor_copy(
+                out=tile[:, :, 0:CLASS_COLS].rearrange("p (a r) q -> p a q r", a=2),
+                in_=grad[h][:].rearrange("p (q a r) -> p a q r", a=2, r=STRIDE // 2),
             )
 
-        def scalar_products(h):
-            products = []
-            for offset, table, row in fine_taps[:PRODUCT_TAPS]:
-                product = terms.tile([P, TOKENS], F32)
-                nc.scalar.activation(
-                    out=product[:], in_=grad[h][:, offset : offset + TOKENS], func=ACT.Copy, scale=table[:, row, h : h + 1]
-                )
-                products.append(product)
-            return products
-
-        def start_tail(acc, h):
-            offset, table, row = fine_taps[PRODUCT_TAPS]
-            nc.vector.tensor_scalar_mul(
-                out=acc[:, BAND_TOKENS:TOKENS], in0=grad[h][:, BAND_TOKENS + offset : TOKENS + offset],
-                scalar1=table[:, row, h : h + 1],
-            )
-
-        def transposed_classes(h):
-            words = grad[h][:, 0:TOKENS].bitcast(F32)
-            classes_ps = psum_c.tile([P, STRIDE // 2, P], F32)
-            for w in range(STRIDE // 2):
-                nc.tensor.transpose(classes_ps[:, w, :], words[:, w : TOKENS // 2 : STRIDE // 2], identity[:])
+        def transpose_classes(h):
+            count = band_classes(h)
+            if count == 0:
+                return
+            classes_ps = psum_c.tile([P, STRIDE, P], BF16, name="classes_ps")
+            for r in range(count):
+                nc.tensor.transpose(classes_ps[:, r, :], by_class[h][:, r, 0:P], identity_bf[:])
             classes[h] = class_pool.tile([P, STRIDE, P], F32, name="classes")
-            nc.scalar.copy(
-                out=classes[h][:].rearrange("p (w e) c -> p w e c", e=2),
-                in_=classes_ps[:].bitcast(BF16).rearrange("p w (c e) -> p w e c", e=2),
-            )
+            nc.scalar.copy(out=classes[h][:, 0:count, :], in_=classes_ps[:, 0:count, :])
 
-        def band_sum(h, r):
-            if r % BANK_CLASSES == 0:
-                banks[h, r // BANK_CLASSES] = psum_b.tile([P, BANK_CLASSES, BAND_COLS], F32, name="band_ps")
-            nc.tensor.matmul(
-                out=banks[h, r // BANK_CLASSES][:, r % BANK_CLASSES, :], lhsT=classes[h][:, r, :], rhs=band_of[h],
-                start=True, stop=True,
-            )
+        def weight(tap, h):
+            offset, table, row = tap
+            return table[:, row, h : h + 1]
 
-        def start_from_band(acc, h, bank):
-            offset, table, row = fine_taps[PRODUCT_TAPS]
-            by_class = acc[:, 0:BAND_TOKENS].rearrange("p (q r) -> p q r", r=STRIDE)
-            shifted = grad[h][:, offset : offset + BAND_TOKENS].rearrange("p (q r) -> p q r", r=STRIDE)
-            of_bank = slice(bank * BANK_CLASSES, (bank + 1) * BANK_CLASSES)
-            nc.vector.scalar_tensor_tensor(
-                out=by_class[:, :, of_bank], in0=shifted[:, :, of_bank], scalar=table[:, row, h : h + 1],
-                in1=banks[h, bank][:].rearrange("p r q -> p q r"), op0=ALU.mult, op1=ALU.add,
-            )
-
-        def turn(h, g, t):
-            if t == 0:
-                turned[h, g] = psum_t.tile([P, PACK, P], F32, name="turned")
-            first = g * K_PASS + t * P
-            for i, part in enumerate(parts[h]):
-                nc.tensor.matmul(
-                    out=turned[h, g][:, t, :], lhsT=part[:, first : first + P], rhs=identity[:],
-                    is_transpose=True, start=(i == 0), stop=(i == len(parts[h]) - 1),
+        def make_products(h):
+            for tap in product_taps:
+                product = terms.tile([P, STRIDE, CLASS_PITCH], F32, name="product")
+                nc.scalar.activation(
+                    out=product[:, :, 0:SHIFTED_COLS], in_=by_class[h][:, :, 0:SHIFTED_COLS], func=ACT.Copy, scale=weight(tap, h)
                 )
+                parts[h].append((product, tap[0]))
+
+        def start_sum(h):
+            acc = sums.tile([P, STRIDE, CLASS_PITCH], F32, name="acc")
+            parts[h].append((acc, sum_taps[0][0]))
+            nc.vector.tensor_scalar_mul(
+                out=acc[:, :, 0:SHIFTED_COLS], in0=by_class[h][:, :, 0:SHIFTED_COLS], scalar1=weight(sum_taps[0], h)
+            )
+
+        def add_to_sum(h):
+            acc = parts[h][-1][0]
+            nc.vector.scalar_tensor_tensor(
+                out=acc[:, :, 0:SHIFTED_COLS], in0=by_class[h][:, :, 1 : SHIFTED_COLS + 1], scalar=weight(sum_taps[1], h),
+                in1=acc[:, :, 0:SHIFTED_COLS], op0=ALU.mult, op1=ALU.add,
+            )
+
+        def coarse_tap(h, tap):
+            first = band_classes(h)
+            k = tap[0] // STRIDE
+            if k == 0:
+                coarse[h] = keep.tile([P, STRIDE - first, P], F32, name=f"coarse{h}")
+                nc.vector.tensor_scalar_mul(out=coarse[h][:], in0=by_class[h][:, first:STRIDE, 0:P], scalar1=weight(tap, h))
+            else:
+                nc.vector.scalar_tensor_tensor(
+                    out=coarse[h][:, :, 0 : P - k], in0=by_class[h][:, first:STRIDE, k:P], scalar=weight(tap, h),
+                    in1=coarse[h][:, :, 0 : P - k], op0=ALU.mult, op1=ALU.add,
+                )
+
+        def turn(h, g):
+            bank = psum_t.tile([P, PACK, P], F32, name="turned")
+            turned[h, g] = bank
+            banded = min(max(band_classes(h) - PACK * g, 0), PACK)
+            if banded:
+                nc.tensor.matmul(
+                    out=bank[:, 0:banded, :].rearrange("p t c -> p (t c)"), lhsT=band_of[h],
+                    rhs=classes[h][:, PACK * g : PACK * g + banded, :].rearrange("p t c -> p (t c)"),
+                    start=True, stop=False,
+                )
+            for t in range(PACK):
+                r = PACK * g + t
+                tiles = [(part, (r + offset) % STRIDE, (r + offset) // STRIDE) for part, offset in parts[h]]
+                if t >= banded:
+                    tiles.append((coarse[h], r - band_classes(h), 0))
+                for i, (part, row, q) in enumerate(tiles):
+                    nc.tensor.matmul(
+                        out=bank[:, t, :], lhsT=part[:, row, q : q + P], rhs=identity[:], is_transpose=True,
+                        start=(t >= banded and i == 0), stop=(i == len(tiles) - 1 and t >= banded - 1),
+                    )
 
         def scale(h, g):
             if h % 2 == 0 and g == 0:
                 dv_grouped[h // 2] = stage.tile([P, PASSES, P, PACK], BF16, align_bytes=64, name="dv_grouped")
             first = h % 2 * HEAD_DIM
-            kmag_g = kmag[:, :, h].rearrange("p (b g t) -> p b g t", b=BATCH, t=PACK)[:, :, g, :]
+            kmag_g = kmag[:, :, PACK * g : PACK * (g + 1), h]
             nc.vector.tensor_tensor(
                 out=dv_grouped[h // 2][:, g::PASSES_PER_BATCH, first : first + HEAD_DIM, :],
                 in0=turned[h, g][:].rearrange("p t (b c) -> p b c t", b=BATCH),
@@ -273,74 +300,70 @@ def tile_causalwaveletfieldattentionbyte_pa_v_kernel(
             return (2 * pair, 2 * pair + 1)
 
         PAIRS = HEADS // 2
-        parts = {}
+        parts = {h: [] for h in range(HEADS)}
+        by_class = {}
         classes = {}
-        banks = {}
+        coarse = {}
         turned = {}
         dv_grouped = {}
         dv_codes = {}
         dv_scales = {}
         result = {}
+        late = [h for h in range(HEADS) if band_classes(h) < STRIDE]
+        background = [(h, tap) for i in range(0, len(late), 2) for tap in band_taps for h in late[i : i + 2]]
+        chunk = -(-len(background) // (PAIRS - 1))
+
         ctx.enter_context(tc.manual_schedule(engines={mybir.EngineType.PE}))
-        for h in range(4):
-            transposed_classes(h)
-        for h in range(2):
-            for r in range(STRIDE):
-                band_sum(h, r)
+        for h in (0, 1):
+            split_classes(h)
+            transpose_classes(h)
         for rnd in range(PAIRS + 2):
             filtering = rnd < PAIRS
             preparing = rnd + 1 < PAIRS
-            loading = rnd + 2 < PAIRS
             turning = 1 <= rnd <= PAIRS
             multiplying = rnd >= 2
-            accs = {}
             if filtering:
                 for h in heads_of(rnd):
-                    parts[h] = scalar_products(h)
-                    accs[h] = sums.tile([P, TOKENS], F32, name="acc")
-            for s in range(2 * rnd, min(2 * rnd + 2, PASSES)):
-                regroup_x(s)
-                if s + 2 < PASSES:
-                    load_x(s + 2)
-
-            quarters = [[], [], [], []]
-            if filtering:
-                tails = [[(start_tail, acc, h) for h, acc in accs.items()]]
-                for offset, table, row in band_taps:
-                    if BAND_TOKENS + offset < TOKENS:
-                        tails.append([(add_tap, acc, h, offset, table[:, row, h : h + 1], BAND_TOKENS) for h, acc in accs.items()])
-                starts = [(start_from_band, acc, h, k) for h, acc in accs.items() for k in range(STRIDE // BANK_CLASSES)]
-                for i, pair_of_taps in enumerate(tails):
-                    if i < len(starts):
-                        quarters[i // 6].append(starts[i])
-                    quarters[i // 6].extend(pair_of_taps)
-                for i, (offset, table, row) in enumerate(fine_taps[PRODUCT_TAPS + 1 :]):
-                    quarters[2 + i % 2].extend((add_tap, acc, h, offset, table[:, row, h : h + 1], 0) for h, acc in accs.items())
-            for i, quarter in enumerate(quarters):
-                h_turned, g_turned = 2 * (rnd - 1) + i // PASSES_PER_BATCH, i % PASSES_PER_BATCH
-                for step in quarter:
-                    step[0](*step[1:])
-                if i == 0 and 0 <= rnd - 2:
+                    make_products(h)
+            if rnd < 2:
+                for s in (2 * rnd, 2 * rnd + 1):
+                    regroup_x(s)
+                    if s + 2 < PASSES:
+                        load_x(s + 2)
+            if rnd == 0:
+                for h in late[:2]:
+                    split_classes(h)
+                for h in load_order[4:6]:
+                    load_head(h)
+            if rnd == 1:
+                for h in late[2:]:
+                    split_classes(h)
+            for h in load_order[6 + 2 * rnd : 8 + 2 * rnd]:
+                load_head(h)
+            work = background[chunk * rnd : chunk * (rnd + 1)]
+            steps = [work[len(work) * i // 4 : len(work) * (i + 1) // 4] for i in range(4)]
+            for i in range(4):
+                if i == 0 and multiplying:
                     quantise_dv(rnd - 2)
-                for t in range(PACK):
-                    if turning:
-                        turn(h_turned, g_turned, t)
-                    k = i * PACK + t - 1
-                    if preparing and k >= 0:
-                        band_sum(2 * (rnd + 1) + k // STRIDE, k % STRIDE)
+                if filtering and i == 0:
+                    for h in heads_of(rnd):
+                        start_sum(h)
+                if filtering and i == 1:
+                    for h in heads_of(rnd):
+                        add_to_sum(h)
+                if preparing and i >= 2:
+                    h = 2 * (rnd + 1) + i - 2
+                    if h not in by_class:
+                        split_classes(h)
+                for step in steps[i]:
+                    coarse_tap(*step)
                 if turning:
-                    scale(h_turned, g_turned)
+                    h, g = 2 * (rnd - 1) + i // PASSES_PER_BATCH, i % PASSES_PER_BATCH
+                    turn(h, g)
+                    scale(h, g)
                 if multiplying and i in (1, 2):
                     multiply(rnd - 2, i - 1)
-                if loading and i in (1, 3):
-                    transposed_classes(2 * (rnd + 2) + i // 2)
-                if rnd < 2:
-                    if i % 2 == 1:
-                        quantise_x(2 * rnd + i // 2)
-            if preparing:
-                band_sum(2 * (rnd + 1) + 1, STRIDE - 1)
-            for h, acc in accs.items():
-                parts[h].append(acc)
-            if rnd + 4 < PAIRS:
-                for h in heads_of(rnd + 4):
-                    load_head(h)
+                if preparing and i >= 2:
+                    transpose_classes(2 * (rnd + 1) + i - 2)
+                if rnd < 2 and i >= 2:
+                    quantise_x(2 * rnd + i - 2)

@@ -27,7 +27,7 @@ MX_FLOPS = 2 * CHANNELS * BATCH * TOKENS * WIDTH
 BAND_UNITS = MX_FLOPS // 10 // (2 * P * P * P)
 BAND_HEADS = -(-BAND_UNITS // STRIDE)
 ROW = 2 * P
-ZERO_PAD = 16
+ZERO_PAD = 32
 CLASS_COLS = (TOKENS + ZERO_PAD) // STRIDE
 CLASS_PITCH = 136
 SHIFTED_COLS = P + 1
@@ -91,6 +91,59 @@ def tile_causalwaveletfieldattentionbyte_pa_v_kernel(
         identity_bf = keep.tile([P, P], BF16)
         make_identity(nc, identity_bf[:])
 
+        by_class = {}
+        classes = {}
+
+        def band_classes(h):
+            return min(max(BAND_UNITS - STRIDE * h, 0), STRIDE)
+
+        def split_classes(h):
+            tile = keep.tile([P, STRIDE, CLASS_PITCH], BF16, name=f"late{h}") if band_classes(h) < STRIDE else (
+                by_class_pool.tile([P, STRIDE, CLASS_PITCH], BF16, name="by_class")
+            )
+            by_class[h] = tile
+            nc.vector.tensor_copy(
+                out=tile[:, :, 0:CLASS_COLS].rearrange("p (a r) (q i) -> p a q r i", a=2, i=4),
+                in_=grad[h][:].rearrange("p (q i a r) -> p a q r i", i=4, a=2, r=STRIDE // 2),
+            )
+
+        def transpose_classes(h):
+            count = band_classes(h)
+            if count == 0:
+                return
+            classes_ps = psum_c.tile([P, STRIDE, P], BF16, name="classes_ps")
+            for r in range(count):
+                nc.tensor.transpose(classes_ps[:, r, :], by_class[h][:, r, 0:P], identity_bf[:])
+            classes[h] = class_pool.tile([P, STRIDE, P], F32, name="classes")
+            nc.scalar.copy(out=classes[h][:, 0:count, :], in_=classes_ps[:, 0:count, :])
+
+        for h in (0, 1):
+            split_classes(h)
+            transpose_classes(h)
+
+        x_codes = keep.tile([P, PASSES, WIDTH], U32, align_bytes=64)
+        x_scales = keep.tile([P, PASSES, WIDTH], U8, align_bytes=64)
+
+        x_grouped = {}
+
+        def regroup_x(s):
+            x_grouped[s] = stage.tile([P, WIDTH, PACK], BF16, align_bytes=64, name="x_grouped")
+            copy = nc.vector.tensor_copy if s % 2 == 1 else nc.scalar.copy
+            copy(
+                out=x_grouped[s][:].rearrange("p (c i) t -> p c t i", i=4),
+                in_=x_raw[s][:].rearrange("p t (c i) -> p c t i", i=4),
+            )
+
+        def quantise_x(s):
+            nc.vector.quantize_mx(
+                out=x_codes[:, s, :].bitcast(E4M3X4),
+                scales=x_scales[:, s, :],
+                in_=x_grouped[s][:].rearrange("p c t -> p (c t)"),
+            )
+
+        regroup_x(0)
+        regroup_x(1)
+
         logits = keep.tile([P, SCALES, HEADS], F32)
         nc.vector.tensor_copy(out=logits[:].rearrange("p j h -> p (j h)"), in_=logits_bf[:])
         top = keep.tile([P, HEADS], F32)
@@ -140,62 +193,19 @@ def tile_causalwaveletfieldattentionbyte_pa_v_kernel(
             nc.gpsimd.memset(rows[:], 0.0)
             for offset, table, row in band_taps:
                 nc.vector.tensor_copy(out=rows[:, 0:heads, P - 1 - offset // STRIDE], in_=table[:, row, group])
-            nc.gpsimd.dma_start(
+            nc.sync.dma_start(
                 out=scratch[used : used + P * pitch].rearrange("(p w) -> p w", w=pitch),
                 in_=rows[:].rearrange("p h l -> p (h l)"),
             )
             skewed = scratch[used + P - 1 : used + P - 1 + P * (pitch - 1)].rearrange("(p w) -> p w", w=pitch - 1)
             band = keep.tile([P, heads, P], F32, name=f"band{group.start}")
-            nc.gpsimd.dma_start(
+            nc.sync.dma_start(
                 out=band[:],
                 in_=skewed[:, 0 : heads * ROW].rearrange("p (h l) -> p h l", l=ROW)[:, :, 0:P],
             )
             for h in range(group.start, group.stop):
                 band_of[h] = band[:, h - group.start, :]
             used += P * pitch
-
-        x_codes = keep.tile([P, PASSES, WIDTH], U32, align_bytes=64)
-        x_scales = keep.tile([P, PASSES, WIDTH], U8, align_bytes=64)
-
-        x_grouped = {}
-
-        def regroup_x(s):
-            x_grouped[s] = stage.tile([P, WIDTH, PACK], BF16, align_bytes=64, name="x_grouped")
-            copy = nc.vector.tensor_copy if s % 2 == 1 else nc.scalar.copy
-            copy(
-                out=x_grouped[s][:].rearrange("p (c i) t -> p c t i", i=4),
-                in_=x_raw[s][:].rearrange("p t (c i) -> p c t i", i=4),
-            )
-
-        def quantise_x(s):
-            nc.vector.quantize_mx(
-                out=x_codes[:, s, :].bitcast(E4M3X4),
-                scales=x_scales[:, s, :],
-                in_=x_grouped[s][:].rearrange("p c t -> p (c t)"),
-            )
-
-        def band_classes(h):
-            return min(max(BAND_UNITS - STRIDE * h, 0), STRIDE)
-
-        def split_classes(h):
-            tile = keep.tile([P, STRIDE, CLASS_PITCH], BF16, name=f"late{h}") if band_classes(h) < STRIDE else (
-                by_class_pool.tile([P, STRIDE, CLASS_PITCH], BF16, name="by_class")
-            )
-            by_class[h] = tile
-            nc.vector.tensor_copy(
-                out=tile[:, :, 0:CLASS_COLS].rearrange("p (a r) q -> p a q r", a=2),
-                in_=grad[h][:].rearrange("p (q a r) -> p a q r", a=2, r=STRIDE // 2),
-            )
-
-        def transpose_classes(h):
-            count = band_classes(h)
-            if count == 0:
-                return
-            classes_ps = psum_c.tile([P, STRIDE, P], BF16, name="classes_ps")
-            for r in range(count):
-                nc.tensor.transpose(classes_ps[:, r, :], by_class[h][:, r, 0:P], identity_bf[:])
-            classes[h] = class_pool.tile([P, STRIDE, P], F32, name="classes")
-            nc.scalar.copy(out=classes[h][:, 0:count, :], in_=classes_ps[:, 0:count, :])
 
         def weight(tap, h):
             offset, table, row = tap
@@ -301,8 +311,6 @@ def tile_causalwaveletfieldattentionbyte_pa_v_kernel(
 
         PAIRS = HEADS // 2
         parts = {h: [] for h in range(HEADS)}
-        by_class = {}
-        classes = {}
         coarse = {}
         turned = {}
         dv_grouped = {}
@@ -313,10 +321,7 @@ def tile_causalwaveletfieldattentionbyte_pa_v_kernel(
         background = [(h, tap) for i in range(0, len(late), 2) for tap in band_taps for h in late[i : i + 2]]
         chunk = -(-len(background) // (PAIRS - 1))
 
-        ctx.enter_context(tc.manual_schedule(engines={mybir.EngineType.PE}))
-        for h in (0, 1):
-            split_classes(h)
-            transpose_classes(h)
+        ctx.enter_context(tc.manual_schedule(engines={mybir.EngineType.PE, mybir.EngineType.DVE}))
         for rnd in range(PAIRS + 2):
             filtering = rnd < PAIRS
             preparing = rnd + 1 < PAIRS
@@ -325,12 +330,9 @@ def tile_causalwaveletfieldattentionbyte_pa_v_kernel(
             if filtering:
                 for h in heads_of(rnd):
                     make_products(h)
-            if rnd < 2:
-                for s in (2 * rnd, 2 * rnd + 1):
-                    regroup_x(s)
-                    if s + 2 < PASSES:
-                        load_x(s + 2)
             if rnd == 0:
+                load_x(2)
+                load_x(3)
                 for h in late[:2]:
                     split_classes(h)
                 for h in load_order[4:6]:
@@ -340,7 +342,7 @@ def tile_causalwaveletfieldattentionbyte_pa_v_kernel(
                     split_classes(h)
             for h in load_order[6 + 2 * rnd : 8 + 2 * rnd]:
                 load_head(h)
-            work = background[chunk * rnd : chunk * (rnd + 1)]
+            work = background[chunk * (rnd - 1) : chunk * rnd] if rnd else []
             steps = [work[len(work) * i // 4 : len(work) * (i + 1) // 4] for i in range(4)]
             for i in range(4):
                 if i == 0 and multiplying:
@@ -365,5 +367,10 @@ def tile_causalwaveletfieldattentionbyte_pa_v_kernel(
                     multiply(rnd - 2, i - 1)
                 if preparing and i >= 2:
                     transpose_classes(2 * (rnd + 1) + i - 2)
-                if rnd < 2 and i >= 2:
-                    quantise_x(2 * rnd + i - 2)
+                if rnd == 1 and i < 2:
+                    quantise_x(1 - i)
+                    regroup_x(3 - i)
+                if rnd == 1 and i == 3:
+                    quantise_x(3)
+                if rnd == 2 and i == 0:
+                    quantise_x(2)

@@ -49,8 +49,8 @@ def tile_causalwaveletfieldattentionbyte_pa_v_kernel(
         class_pool = ctx.enter_context(tc.tile_pool(name="class_pool", bufs=4))
         sums = ctx.enter_context(tc.tile_pool(name="sums", bufs=4))
         terms = ctx.enter_context(tc.tile_pool(name="terms", bufs=12))
-        psum_c = ctx.enter_context(tc.psum_pool(name="psum_c", bufs=1))
-        psum_t = ctx.enter_context(tc.psum_pool(name="psum_t", bufs=5))
+        psum_c = ctx.enter_context(tc.psum_pool(name="psum_c", bufs=2))
+        psum_t = ctx.enter_context(tc.psum_pool(name="psum_t", bufs=4))
         psum_o = ctx.enter_context(tc.psum_pool(name="psum_o", bufs=2))
 
         logits_bf = keep.tile([P, SCALES * HEADS], BF16)
@@ -128,7 +128,7 @@ def tile_causalwaveletfieldattentionbyte_pa_v_kernel(
 
         def regroup_x(s):
             x_grouped[s] = stage.tile([P, WIDTH, PACK], BF16, align_bytes=64, name="x_grouped")
-            copy = nc.vector.tensor_copy if s % 2 == 1 else nc.scalar.copy
+            copy = nc.vector.tensor_copy if s < 2 else nc.scalar.copy
             copy(
                 out=x_grouped[s][:].rearrange("p (c i) t -> p c t i", i=4),
                 in_=x_raw[s][:].rearrange("p t (c i) -> p c t i", i=4),
@@ -245,25 +245,27 @@ def tile_causalwaveletfieldattentionbyte_pa_v_kernel(
                     in1=coarse[h][:, :, 0 : P - k], op0=ALU.mult, op1=ALU.add,
                 )
 
-        def turn(h, g):
-            bank = psum_t.tile([P, PACK, P], F32, name="turned")
-            turned[h, g] = bank
-            banded = min(max(band_classes(h) - PACK * g, 0), PACK)
+        def turn(h, g, half):
+            if half == 0:
+                turned[h, g] = psum_t.tile([P, PACK, P], F32, name="turned")
+            bank = turned[h, g]
+            slots = range(2 * half, 2 * half + 2)
+            banded = [t for t in slots if PACK * g + t < band_classes(h)]
             if banded:
                 nc.tensor.matmul(
-                    out=bank[:, 0:banded, :].rearrange("p t c -> p (t c)"), lhsT=band_of[h],
-                    rhs=classes[h][:, PACK * g : PACK * g + banded, :].rearrange("p t c -> p (t c)"),
+                    out=bank[:, slots.start : slots.stop, :].rearrange("p t c -> p (t c)"), lhsT=band_of[h],
+                    rhs=classes[h][:, PACK * g + slots.start : PACK * g + slots.stop, :].rearrange("p t c -> p (t c)"),
                     start=True, stop=False,
                 )
-            for t in range(PACK):
+            for t in slots:
                 r = PACK * g + t
                 tiles = [(part, (r + offset) % STRIDE, (r + offset) // STRIDE) for part, offset in parts[h]]
-                if t >= banded:
+                if not banded:
                     tiles.append((coarse[h], r - band_classes(h), 0))
                 for i, (part, row, q) in enumerate(tiles):
                     nc.tensor.matmul(
                         out=bank[:, t, :], lhsT=part[:, row, q : q + P], rhs=identity[:], is_transpose=True,
-                        start=(t >= banded and i == 0), stop=(i == len(tiles) - 1 and t >= banded - 1),
+                        start=(not banded and i == 0), stop=(i == len(tiles) - 1 and (not banded or t == banded[-1])),
                     )
 
         def scale(h, g):
@@ -287,14 +289,16 @@ def tile_causalwaveletfieldattentionbyte_pa_v_kernel(
             dv_codes[pair] = codes
             dv_scales[pair] = scales
 
-        def multiply(pair, half):
-            if half == 0:
+        def multiply(pair, step):
+            half = step // 2
+            if step == 0:
                 result[pair] = stage.tile([P, WIDTH], F32, name="result")
+            if step % 2 == 0:
+                products[pair] = psum_o.tile([P, N_TILE], F32, name="product")
             cols = slice(half * N_TILE, (half + 1) * N_TILE)
-            product = psum_o.tile([P, N_TILE], F32)
-            for s in range(PASSES):
+            for s in range(2 * (step % 2), 2 * (step % 2) + 2):
                 nc.tensor.matmul_mx(
-                    out=product[:],
+                    out=products[pair][:],
                     lhsT=dv_codes[pair][:, s * P : (s + 1) * P].bitcast(E5M2X4),
                     lhsT_scale=dv_scales[pair][:, s * P : (s + 1) * P],
                     rhs=x_codes[:, s, cols].bitcast(E4M3X4),
@@ -302,8 +306,9 @@ def tile_causalwaveletfieldattentionbyte_pa_v_kernel(
                     start=(s == 0),
                     stop=(s == PASSES - 1),
                 )
-            nc.scalar.copy(out=result[pair][:, cols], in_=product[:])
-            if cols.stop == WIDTH:
+            if step % 2 == 1:
+                nc.scalar.copy(out=result[pair][:, cols], in_=products[pair][:])
+            if step == 3:
                 nc.sync.dma_start(out=out[pair * P : (pair + 1) * P, :], in_=result[pair][:])
 
         def heads_of(pair):
@@ -317,6 +322,7 @@ def tile_causalwaveletfieldattentionbyte_pa_v_kernel(
         dv_codes = {}
         dv_scales = {}
         result = {}
+        products = {}
         late = [h for h in range(HEADS) if band_classes(h) < STRIDE]
         background = [(h, tap) for i in range(0, len(late), 2) for tap in band_taps for h in late[i : i + 2]]
         chunk = -(-len(background) // (PAIRS - 1))
@@ -333,13 +339,8 @@ def tile_causalwaveletfieldattentionbyte_pa_v_kernel(
             if rnd == 0:
                 load_x(2)
                 load_x(3)
-                for h in late[:2]:
-                    split_classes(h)
                 for h in load_order[4:6]:
                     load_head(h)
-            if rnd == 1:
-                for h in late[2:]:
-                    split_classes(h)
             for h in load_order[6 + 2 * rnd : 8 + 2 * rnd]:
                 load_head(h)
             work = background[chunk * (rnd - 1) : chunk * rnd] if rnd else []
@@ -361,10 +362,16 @@ def tile_causalwaveletfieldattentionbyte_pa_v_kernel(
                     coarse_tap(*step)
                 if turning:
                     h, g = 2 * (rnd - 1) + i // PASSES_PER_BATCH, i % PASSES_PER_BATCH
-                    turn(h, g)
-                    scale(h, g)
-                if multiplying and i in (1, 2):
+                    turn(h, g, 0)
+                if multiplying and i >= 1:
                     multiply(rnd - 2, i - 1)
+                if turning:
+                    turn(h, g, 1)
+                    scale(h, g)
+                if multiplying and i == 3:
+                    multiply(rnd - 2, 3)
+                if rnd < 2 and i >= 2:
+                    split_classes(late[2 * rnd + i - 2])
                 if preparing and i >= 2:
                     transpose_classes(2 * (rnd + 1) + i - 2)
                 if rnd == 1 and i < 2:

@@ -192,7 +192,8 @@ def tile_causalwaveletfieldattentionbyte_pa_v_kernel(
             rows = keep.tile([P, heads + 1, ROW], F32, name=f"rows{group.start}")
             nc.gpsimd.memset(rows[:], 0.0)
             for offset, table, row in band_taps:
-                nc.vector.tensor_copy(out=rows[:, 0:heads, P - 1 - offset // STRIDE], in_=table[:, row, group])
+                copy = nc.vector.tensor_copy if group.start == 0 else nc.gpsimd.tensor_copy
+                copy(out=rows[:, 0:heads, P - 1 - offset // STRIDE], in_=table[:, row, group])
             nc.sync.dma_start(
                 out=scratch[used : used + P * pitch].rearrange("(p w) -> p w", w=pitch),
                 in_=rows[:].rearrange("p h l -> p (h l)"),
@@ -211,26 +212,27 @@ def tile_causalwaveletfieldattentionbyte_pa_v_kernel(
             offset, table, row = tap
             return table[:, row, h : h + 1]
 
-        def make_products(h):
-            for tap in product_taps:
-                product = terms.tile([P, STRIDE, CLASS_PITCH], F32, name="product")
-                nc.scalar.activation(
-                    out=product[:, :, 0:SHIFTED_COLS], in_=by_class[h][:, :, 0:SHIFTED_COLS], func=ACT.Copy, scale=weight(tap, h)
-                )
-                parts[h].append((product, tap[0]))
+        def product_on(engine, tile, h, tap):
+            out, in_ = tile[:, :, 0:SHIFTED_COLS], by_class[h][:, :, 0:SHIFTED_COLS]
+            if engine == "vector":
+                nc.vector.tensor_scalar_mul(out=out, in0=in_, scalar1=weight(tap, h))
+            else:
+                nc.scalar.activation(out=out, in_=in_, func=ACT.Copy, scale=weight(tap, h))
 
-        def start_sum(h):
-            acc = sums.tile([P, STRIDE, CLASS_PITCH], F32, name="acc")
-            parts[h].append((acc, sum_taps[0][0]))
-            nc.vector.tensor_scalar_mul(
-                out=acc[:, :, 0:SHIFTED_COLS], in0=by_class[h][:, :, 0:SHIFTED_COLS], scalar1=weight(sum_taps[0], h)
-            )
+        def make_product(h, tap, engine):
+            product = terms.tile([P, STRIDE, CLASS_PITCH], F32, name="product")
+            product_on(engine, product, h, tap)
+            parts[h].append((product, tap[0]))
+
+        def start_sum(h, engine):
+            acc[h] = sums.tile([P, STRIDE, CLASS_PITCH], F32, name="acc")
+            product_on(engine, acc[h], h, sum_taps[0])
 
         def add_to_sum(h):
-            acc = parts[h][-1][0]
+            parts[h].append((acc[h], sum_taps[0][0]))
             nc.vector.scalar_tensor_tensor(
-                out=acc[:, :, 0:SHIFTED_COLS], in0=by_class[h][:, :, 1 : SHIFTED_COLS + 1], scalar=weight(sum_taps[1], h),
-                in1=acc[:, :, 0:SHIFTED_COLS], op0=ALU.mult, op1=ALU.add,
+                out=acc[h][:, :, 0:SHIFTED_COLS], in0=by_class[h][:, :, 1 : SHIFTED_COLS + 1], scalar=weight(sum_taps[1], h),
+                in1=acc[h][:, :, 0:SHIFTED_COLS], op0=ALU.mult, op1=ALU.add,
             )
 
         def coarse_tap(h, tap):
@@ -316,6 +318,7 @@ def tile_causalwaveletfieldattentionbyte_pa_v_kernel(
 
         PAIRS = HEADS // 2
         parts = {h: [] for h in range(HEADS)}
+        acc = {}
         coarse = {}
         turned = {}
         dv_grouped = {}
@@ -334,8 +337,16 @@ def tile_causalwaveletfieldattentionbyte_pa_v_kernel(
             turning = 1 <= rnd <= PAIRS
             multiplying = rnd >= 2
             if filtering:
-                for h in heads_of(rnd):
-                    make_products(h)
+                first, second = heads_of(rnd)
+                if rnd > 0:
+                    start_sum(second, "scalar")
+                for h in (first, second):
+                    for i, tap in enumerate(product_taps):
+                        make_product(h, tap, "vector" if rnd == 0 and i < 2 else "scalar")
+                    if rnd == 0:
+                        start_sum(h, "vector")
+                        add_to_sum(h)
+                        split_classes(2 + h)
             if rnd == 0:
                 load_x(2)
                 load_x(3)
@@ -348,15 +359,14 @@ def tile_causalwaveletfieldattentionbyte_pa_v_kernel(
             for i in range(4):
                 if i == 0 and multiplying:
                     quantise_dv(rnd - 2)
-                if filtering and i == 0:
-                    for h in heads_of(rnd):
-                        start_sum(h)
-                if filtering and i == 1:
-                    for h in heads_of(rnd):
-                        add_to_sum(h)
+                if filtering and rnd > 0 and i == 0:
+                    start_sum(first, "vector")
+                if filtering and rnd > 0 and i == 1:
+                    add_to_sum(second)
+                    add_to_sum(first)
                 if preparing and i >= 2:
                     h = 2 * (rnd + 1) + i - 2
-                    if h not in by_class:
+                    if rnd > 0 and h not in by_class:
                         split_classes(h)
                 for step in steps[i]:
                     coarse_tap(*step)

@@ -44,17 +44,22 @@ def tile_causalwaveletfieldattentionbyte_pa_v_kernel(
     with ExitStack() as ctx:
         keep = ctx.enter_context(tc.tile_pool(name="keep", bufs=1))
         stage = ctx.enter_context(tc.tile_pool(name="stage", bufs=2))
-        heads_in = ctx.enter_context(tc.tile_pool(name="heads_in", bufs=6))
+        heads_in = ctx.enter_context(tc.tile_pool(name="heads_in", bufs=5))
         by_class_pool = ctx.enter_context(tc.tile_pool(name="by_class", bufs=5))
         class_pool = ctx.enter_context(tc.tile_pool(name="class_pool", bufs=4))
-        sums = ctx.enter_context(tc.tile_pool(name="sums", bufs=4))
+        sums = ctx.enter_context(tc.tile_pool(name="sums", bufs=5))
         terms = ctx.enter_context(tc.tile_pool(name="terms", bufs=12))
         psum_c = ctx.enter_context(tc.psum_pool(name="psum_c", bufs=2))
         psum_t = ctx.enter_context(tc.psum_pool(name="psum_t", bufs=4))
         psum_o = ctx.enter_context(tc.psum_pool(name="psum_o", bufs=2))
 
-        logits_bf = keep.tile([P, SCALES * HEADS], BF16)
-        nc.sync.dma_start(out=logits_bf[:], in_=scale_gain.rearrange("j h -> (j h)").partition_broadcast(P))
+        logits = keep.tile([P, SCALES, HEADS], BF16)
+        nc.sync.dma_start(
+            out=logits[:].rearrange("p j h -> p (j h)"), in_=scale_gain.rearrange("j h -> (j h)").partition_broadcast(P)
+        )
+        warm = keep.tile([P, 1], F32)
+        nc.vector.memset(warm[:], 0.0)
+        nc.scalar.activation(out=warm[:], in_=warm[:], func=ACT.Exp)
 
         grad = {}
 
@@ -72,7 +77,7 @@ def tile_causalwaveletfieldattentionbyte_pa_v_kernel(
 
         def load_x(s):
             x_raw[s] = stage.tile([P, PACK, WIDTH], BF16, name="x_raw")
-            nc.sync.dma_start(out=x_raw[s][:], in_=x_rows[s // PASSES_PER_BATCH, s % PASSES_PER_BATCH])
+            nc.sync.dma_start(out=x_raw[s][:], in_=x_rows[s % BATCH, s // BATCH])
 
         load_head(0)
         load_head(1)
@@ -128,11 +133,13 @@ def tile_causalwaveletfieldattentionbyte_pa_v_kernel(
 
         def regroup_x(s):
             x_grouped[s] = stage.tile([P, WIDTH, PACK], BF16, align_bytes=64, name="x_grouped")
-            copy = nc.vector.tensor_copy if s < 2 else nc.scalar.copy
-            copy(
-                out=x_grouped[s][:].rearrange("p (c i) t -> p c t i", i=4),
-                in_=x_raw[s][:].rearrange("p t (c i) -> p c t i", i=4),
-            )
+            copy, parts_of_x = (nc.scalar.copy, 1) if s in (0, 3) else (nc.vector.tensor_copy, 4)
+            for k in range(parts_of_x):
+                cols = slice(k * WIDTH // parts_of_x, (k + 1) * WIDTH // parts_of_x)
+                copy(
+                    out=x_grouped[s][:, cols, :].rearrange("p (c i) t -> p c t i", i=4),
+                    in_=x_raw[s][:, :, cols].rearrange("p t (c i) -> p c t i", i=4),
+                )
 
         def quantise_x(s):
             nc.vector.quantize_mx(
@@ -144,35 +151,34 @@ def tile_causalwaveletfieldattentionbyte_pa_v_kernel(
         regroup_x(0)
         regroup_x(1)
 
-        logits = keep.tile([P, SCALES, HEADS], F32)
-        nc.vector.tensor_copy(out=logits[:].rearrange("p j h -> p (j h)"), in_=logits_bf[:])
         top = keep.tile([P, HEADS], F32)
         nc.vector.tensor_reduce(out=top[:], in_=logits[:].rearrange("p j h -> p h j"), axis=AXIS.X, op=ALU.max)
+        shifted = keep.tile([P, SCALES, HEADS], F32)
         nc.vector.tensor_tensor(
-            out=logits[:], in0=logits[:], in1=top[:].unsqueeze(1).to_broadcast([P, SCALES, HEADS]), op=ALU.subtract
+            out=shifted[:], in0=logits[:], in1=top[:].unsqueeze(1).to_broadcast([P, SCALES, HEADS]), op=ALU.subtract
         )
         grown = keep.tile([P, SCALES, HEADS], F32)
-        nc.scalar.activation(out=grown[:], in_=logits[:], func=ACT.Exp)
-        total = keep.tile([P, HEADS], F32)
-        nc.vector.tensor_reduce(out=total[:], in_=grown[:].rearrange("p j h -> p h j"), axis=AXIS.X, op=ALU.add)
-        inverse = keep.tile([P, HEADS], F32)
+        nc.scalar.activation(out=grown[:], in_=shifted[:], func=ACT.Exp)
+        total = keep.tile([P, 1, HEADS], F32)
+        nc.vector.tensor_reduce(out=total[:, 0, :], in_=grown[:].rearrange("p j h -> p h j"), axis=AXIS.X, op=ALU.add)
+        inverse = keep.tile([P, 1, HEADS], F32)
         nc.vector.reciprocal(out=inverse[:], in_=total[:])
-        gain = keep.tile([P, SCALES, HEADS], F32)
-        nc.vector.tensor_tensor(
-            out=gain[:], in0=grown[:], in1=inverse[:].unsqueeze(1).to_broadcast([P, SCALES, HEADS]), op=ALU.mult
-        )
-
-        w_pow = keep.tile([P, SCALES, HEADS], F32)
-        nc.vector.tensor_scalar_mul(out=w_pow[:], in0=gain[:], scalar1=TAP2)
+        inverse_of_all = inverse[:].to_broadcast([P, SCALES, HEADS])
+        w_tri = keep.tile([P, SCALES, HEADS], F32)
         nc.vector.scalar_tensor_tensor(
-            out=w_pow[:, 1:, :], in0=gain[:, : SCALES - 1, :], scalar=TAP1, in1=w_pow[:, 1:, :],
+            out=w_tri[:], in0=grown[:], scalar=TAP0, in1=inverse_of_all, op0=ALU.mult, op1=ALU.mult
+        )
+        w_pow = keep.tile([P, SCALES, HEADS], F32)
+        nc.vector.tensor_scalar_mul(out=w_pow[:], in0=grown[:], scalar1=TAP2)
+        nc.vector.scalar_tensor_tensor(
+            out=w_pow[:, 1:, :], in0=grown[:, : SCALES - 1, :], scalar=TAP1, in1=w_pow[:, 1:, :],
             op0=ALU.mult, op1=ALU.add,
         )
-        w_tri = keep.tile([P, SCALES, HEADS], F32)
-        nc.vector.tensor_scalar_mul(out=w_tri[:], in0=gain[:], scalar1=TAP0)
+        nc.vector.tensor_tensor(out=w_pow[:], in0=w_pow[:], in1=inverse_of_all, op=ALU.mult)
         w_zero = keep.tile([P, 1, HEADS], F32)
-        nc.vector.tensor_reduce(out=w_zero[:, 0, :], in_=gain[:].rearrange("p j h -> p h j"), axis=AXIS.X, op=ALU.add)
-        nc.vector.tensor_scalar_mul(out=w_zero[:], in0=w_zero[:], scalar1=TAP3)
+        nc.vector.scalar_tensor_tensor(
+            out=w_zero[:], in0=total[:], scalar=TAP3, in1=inverse[:], op0=ALU.mult, op1=ALU.mult
+        )
 
         taps = [(0, w_zero, 0)]
         taps += [(2**m, w_pow, m) for m in range(SCALES)]
@@ -180,33 +186,35 @@ def tile_causalwaveletfieldattentionbyte_pa_v_kernel(
         taps = sorted(taps, key=lambda tap: tap[0])
         fine_taps = {tap[0]: tap for tap in taps if tap[0] % STRIDE != 0}
         band_taps = [tap for tap in taps if tap[0] % STRIDE == 0]
-        product_taps = [fine_taps[offset] for offset in (1, 2, 3, 6)]
+        product_taps = [fine_taps[offset] for offset in (3, 6, 1, 2)]
         sum_taps = [fine_taps[offset] for offset in (4, 12)]
+
 
         scratch = out.rearrange("c i -> (c i)")
         band_of = {}
         used = 0
-        for group in (slice(0, 2), slice(2, BAND_HEADS)):
-            heads = group.stop - group.start
-            pitch = (heads + 1) * ROW
-            rows = keep.tile([P, heads + 1, ROW], F32, name=f"rows{group.start}")
-            nc.gpsimd.memset(rows[:], 0.0)
-            for offset, table, row in band_taps:
-                copy = nc.vector.tensor_copy if group.start == 0 else nc.gpsimd.tensor_copy
-                copy(out=rows[:, 0:heads, P - 1 - offset // STRIDE], in_=table[:, row, group])
-            nc.sync.dma_start(
-                out=scratch[used : used + P * pitch].rearrange("(p w) -> p w", w=pitch),
-                in_=rows[:].rearrange("p h l -> p (h l)"),
-            )
-            skewed = scratch[used + P - 1 : used + P - 1 + P * (pitch - 1)].rearrange("(p w) -> p w", w=pitch - 1)
-            band = keep.tile([P, heads, P], F32, name=f"band{group.start}")
-            nc.sync.dma_start(
-                out=band[:],
-                in_=skewed[:, 0 : heads * ROW].rearrange("p (h l) -> p h l", l=ROW)[:, :, 0:P],
-            )
-            for h in range(group.start, group.stop):
-                band_of[h] = band[:, h - group.start, :]
-            used += P * pitch
+        with tc.tile_pool(name="rows_tiles", bufs=1) as rows_tiles:
+            for group in (slice(0, 2), slice(2, BAND_HEADS)):
+                heads = group.stop - group.start
+                pitch = (heads + 1) * ROW
+                rows = rows_tiles.tile([P, heads + 1, ROW], F32, name=f"rows{group.start}")
+                nc.gpsimd.memset(rows[:], 0.0)
+                for offset, table, row in band_taps:
+                    nc.vector.tensor_copy(out=rows[:, 0:heads, P - 1 - offset // STRIDE], in_=table[:, row, group])
+                nc.sync.dma_start(
+                    out=scratch[used : used + P * pitch].rearrange("(p w) -> p w", w=pitch),
+                    in_=rows[:].rearrange("p h l -> p (h l)"),
+                )
+                skewed = scratch[used + P - 1 : used + P - 1 + P * (pitch - 1)].rearrange("(p w) -> p w", w=pitch - 1)
+                band = keep.tile([P, heads, P], F32, name=f"band{group.start}")
+                nc.sync.dma_start(
+                    out=band[:],
+                    in_=skewed[:, 0 : heads * ROW].rearrange("p (h l) -> p h l", l=ROW)[:, :, 0:P],
+                )
+                for h in range(group.start, group.stop):
+                    band_of[h] = band[:, h - group.start, :]
+                used += P * pitch
+        more_terms = ctx.enter_context(tc.tile_pool(name="more_terms", bufs=4))
 
         def weight(tap, h):
             offset, table, row = tap
@@ -220,7 +228,8 @@ def tile_causalwaveletfieldattentionbyte_pa_v_kernel(
                 nc.scalar.activation(out=out, in_=in_, func=ACT.Copy, scale=weight(tap, h))
 
         def make_product(h, tap, engine):
-            product = terms.tile([P, STRIDE, CLASS_PITCH], F32, name="product")
+            pool = more_terms if h >= 2 and tap == product_taps[-1] else terms
+            product = pool.tile([P, STRIDE, CLASS_PITCH], F32, name="product")
             product_on(engine, product, h, tap)
             parts[h].append((product, tap[0]))
 
@@ -247,60 +256,67 @@ def tile_causalwaveletfieldattentionbyte_pa_v_kernel(
                     in1=coarse[h][:, :, 0 : P - k], op0=ALU.mult, op1=ALU.add,
                 )
 
-        def turn(h, g, half):
-            if half == 0:
-                turned[h, g] = psum_t.tile([P, PACK, P], F32, name="turned")
-            bank = turned[h, g]
-            slots = range(2 * half, 2 * half + 2)
-            banded = [t for t in slots if PACK * g + t < band_classes(h)]
-            if banded:
+        def banded(h, g, half):
+            return PACK * g + 2 * half < band_classes(h)
+
+        def add_bands(h, g, half, opens):
+            if banded(h, g, half):
+                cols = slice(2 * half, 2 * half + 2)
+                rows = slice(PACK * g + 2 * half, PACK * g + 2 * half + 2)
                 nc.tensor.matmul(
-                    out=bank[:, slots.start : slots.stop, :].rearrange("p t c -> p (t c)"), lhsT=band_of[h],
-                    rhs=classes[h][:, PACK * g + slots.start : PACK * g + slots.stop, :].rearrange("p t c -> p (t c)"),
-                    start=True, stop=False,
+                    out=turned[h, g][:, cols, :].rearrange("p t c -> p (t c)"), lhsT=band_of[h],
+                    rhs=classes[h][:, rows, :].rearrange("p t c -> p (t c)"), start=opens, stop=not opens and half == 1,
                 )
-            for t in slots:
+
+        def add_transposes(h, g, half, opens, closes):
+            for t in (2 * half, 2 * half + 1):
                 r = PACK * g + t
                 tiles = [(part, (r + offset) % STRIDE, (r + offset) // STRIDE) for part, offset in parts[h]]
-                if not banded:
+                if not banded(h, g, half):
                     tiles.append((coarse[h], r - band_classes(h), 0))
                 for i, (part, row, q) in enumerate(tiles):
                     nc.tensor.matmul(
-                        out=bank[:, t, :], lhsT=part[:, row, q : q + P], rhs=identity[:], is_transpose=True,
-                        start=(not banded and i == 0), stop=(i == len(tiles) - 1 and (not banded or t == banded[-1])),
+                        out=turned[h, g][:, t, :], lhsT=part[:, row, q : q + P], rhs=identity[:], is_transpose=True,
+                        start=opens and i == 0 and t % 2 == 0, stop=closes and i == len(tiles) - 1 and t % 2 == 1,
                     )
 
+        def turn(h, g, half):
+            if half == 0:
+                turned[h, g] = psum_t.tile([P, PACK, P], F32, name="turned")
+            add_bands(h, g, half, True)
+            add_transposes(h, g, half, not banded(h, g, half), True)
+
         def scale(h, g):
-            if h % 2 == 0 and g == 0:
+            if h // 2 not in dv_grouped:
                 dv_grouped[h // 2] = stage.tile([P, PASSES, P, PACK], BF16, align_bytes=64, name="dv_grouped")
             first = h % 2 * HEAD_DIM
             kmag_g = kmag[:, :, PACK * g : PACK * (g + 1), h]
             nc.vector.tensor_tensor(
-                out=dv_grouped[h // 2][:, g::PASSES_PER_BATCH, first : first + HEAD_DIM, :],
+                out=dv_grouped[h // 2][:, BATCH * g : BATCH * (g + 1), first : first + HEAD_DIM, :],
                 in0=turned[h, g][:].rearrange("p t (b c) -> p b c t", b=BATCH),
                 in1=kmag_g.unsqueeze(2).to_broadcast([P, BATCH, HEAD_DIM, PACK]),
                 op=ALU.mult,
             )
 
-        def quantise_dv(pair):
-            codes = stage.tile([P, PASSES * P], U32, align_bytes=64, name="dv_codes")
-            scales = stage.tile([P, PASSES * P], U8, align_bytes=64, name="dv_scales")
+        def quantise_dv(pair, first, last):
+            if first == 0:
+                dv_codes[pair] = stage.tile([P, PASSES * P], U32, align_bytes=64, name="dv_codes")
+                dv_scales[pair] = stage.tile([P, PASSES * P], U8, align_bytes=64, name="dv_scales")
+            cols = slice(first * P, last * P)
             nc.vector.quantize_mx(
-                out=codes[:].bitcast(E5M2X4), scales=scales[:], in_=dv_grouped[pair][:].rearrange("p s c t -> p (s c t)")
+                out=dv_codes[pair][:, cols].bitcast(E5M2X4), scales=dv_scales[pair][:, cols],
+                in_=dv_grouped[pair][:, first:last, :, :].rearrange("p s c t -> p (s c t)"),
             )
-            dv_codes[pair] = codes
-            dv_scales[pair] = scales
 
-        def multiply(pair, step):
-            half = step // 2
-            if step == 0:
+        def multiply(pair, half, first):
+            if first == 0 and half == 0:
                 result[pair] = stage.tile([P, WIDTH], F32, name="result")
-            if step % 2 == 0:
-                products[pair] = psum_o.tile([P, N_TILE], F32, name="product")
+            if first == 0:
+                products[pair, half] = psum_o.tile([P, N_TILE], F32, name="product")
             cols = slice(half * N_TILE, (half + 1) * N_TILE)
-            for s in range(2 * (step % 2), 2 * (step % 2) + 2):
+            for s in (first, first + 1):
                 nc.tensor.matmul_mx(
-                    out=products[pair][:],
+                    out=products[pair, half][:],
                     lhsT=dv_codes[pair][:, s * P : (s + 1) * P].bitcast(E5M2X4),
                     lhsT_scale=dv_scales[pair][:, s * P : (s + 1) * P],
                     rhs=x_codes[:, s, cols].bitcast(E4M3X4),
@@ -308,10 +324,11 @@ def tile_causalwaveletfieldattentionbyte_pa_v_kernel(
                     start=(s == 0),
                     stop=(s == PASSES - 1),
                 )
-            if step % 2 == 1:
-                nc.scalar.copy(out=result[pair][:, cols], in_=products[pair][:])
-            if step == 3:
-                nc.sync.dma_start(out=out[pair * P : (pair + 1) * P, :], in_=result[pair][:])
+
+        def store(pair, half, copy):
+            cols = slice(half * N_TILE, (half + 1) * N_TILE)
+            copy(out=result[pair][:, cols], in_=products[pair, half][:])
+            nc.sync.dma_start(out=out[pair * P : (pair + 1) * P, cols], in_=result[pair][:, cols])
 
         def heads_of(pair):
             return (2 * pair, 2 * pair + 1)
@@ -331,15 +348,14 @@ def tile_causalwaveletfieldattentionbyte_pa_v_kernel(
         chunk = -(-len(background) // (PAIRS - 1))
 
         ctx.enter_context(tc.manual_schedule(engines={mybir.EngineType.PE, mybir.EngineType.DVE}))
-        for rnd in range(PAIRS + 2):
+        for rnd in range(PAIRS + 1):
             filtering = rnd < PAIRS
             preparing = rnd + 1 < PAIRS
-            turning = 1 <= rnd <= PAIRS
+            turning = rnd >= 1
+            last = rnd == PAIRS
             multiplying = rnd >= 2
             if filtering:
                 first, second = heads_of(rnd)
-                if rnd > 0:
-                    start_sum(second, "scalar")
                 for h in (first, second):
                     for i, tap in enumerate(product_taps):
                         make_product(h, tap, "vector" if rnd == 0 and i < 2 else "scalar")
@@ -356,34 +372,58 @@ def tile_causalwaveletfieldattentionbyte_pa_v_kernel(
                 load_head(h)
             work = background[chunk * (rnd - 1) : chunk * rnd] if rnd else []
             steps = [work[len(work) * i // 4 : len(work) * (i + 1) // 4] for i in range(4)]
+            turns = [(h, g) for h in heads_of(rnd - 1) for g in range(PASSES_PER_BATCH)]
+            if last:
+                turns = [(h, g) for g in range(PASSES_PER_BATCH) for h in heads_of(rnd - 1)]
+            mx = [[], [(0, 0)], [(0, 2)], [(1, 0)], [(1, 2)]]
+            if last:
+                mx = [[], [(0, 0), (0, 2)], [(1, 0), (1, 2)], [], []]
+
+            def multiply_and_store(steps):
+                for half, first_pass in steps:
+                    multiply(rnd - 2, half, first_pass)
+                    if first_pass == 2:
+                        store(rnd - 2, half, nc.scalar.copy)
+
             for i in range(4):
                 if i == 0 and multiplying:
-                    quantise_dv(rnd - 2)
+                    quantise_dv(rnd - 2, 0, PASSES)
                 if filtering and rnd > 0 and i == 0:
                     start_sum(first, "vector")
                 if filtering and rnd > 0 and i == 1:
-                    add_to_sum(second)
                     add_to_sum(first)
+                    add_to_sum(second)
                 if preparing and i >= 2:
                     h = 2 * (rnd + 1) + i - 2
                     if rnd > 0 and h not in by_class:
                         split_classes(h)
                 for step in steps[i]:
                     coarse_tap(*step)
-                if turning:
-                    h, g = 2 * (rnd - 1) + i // PASSES_PER_BATCH, i % PASSES_PER_BATCH
-                    turn(h, g, 0)
-                if multiplying and i >= 1:
-                    multiply(rnd - 2, i - 1)
-                if turning:
-                    turn(h, g, 1)
-                    scale(h, g)
+                if rnd == 1:
+                    add_bands(*turns[i], 0, False)
+                    add_bands(*turns[i], 1, False)
+                elif turning:
+                    turn(*turns[i], 0)
+                    if multiplying:
+                        multiply_and_store(mx[i])
+                    turn(*turns[i], 1)
+                if rnd == 0 and i >= 2:
+                    for g in range(PASSES_PER_BATCH):
+                        turned[i - 2, g] = psum_t.tile([P, PACK, P], F32, name="turned")
+                        add_transposes(i - 2, g, 0, True, False)
+                        add_transposes(i - 2, g, 1, False, False)
+                for ready in ([], [], turns[0:2], turns[2:4])[i] if rnd == 1 else turns[i : i + 1] if turning else []:
+                    scale(*ready)
+                if last and i == 1:
+                    quantise_dv(PAIRS - 1, 0, 2)
                 if multiplying and i == 3:
-                    multiply(rnd - 2, 3)
+                    multiply_and_store(mx[4])
                 if rnd < 2 and i >= 2:
                     split_classes(late[2 * rnd + i - 2])
                 if preparing and i >= 2:
                     transpose_classes(2 * (rnd + 1) + i - 2)
+                if preparing and i == 3:
+                    start_sum(heads_of(rnd + 1)[1], "scalar")
                 if rnd == 1 and i < 2:
                     quantise_x(1 - i)
                     regroup_x(3 - i)
@@ -391,3 +431,10 @@ def tile_causalwaveletfieldattentionbyte_pa_v_kernel(
                     quantise_x(3)
                 if rnd == 2 and i == 0:
                     quantise_x(2)
+        multiply(PAIRS - 1, 0, 0)
+        multiply(PAIRS - 1, 1, 0)
+        quantise_dv(PAIRS - 1, 2, 4)
+        multiply(PAIRS - 1, 0, 2)
+        store(PAIRS - 1, 0, nc.scalar.copy)
+        multiply(PAIRS - 1, 1, 2)
+        store(PAIRS - 1, 1, nc.vector.tensor_copy)

@@ -47,7 +47,7 @@ def tile_causalwaveletfieldattentionbyte_pa_v_kernel(
         heads_in = ctx.enter_context(tc.tile_pool(name="heads_in", bufs=5))
         by_class_pool = ctx.enter_context(tc.tile_pool(name="by_class", bufs=5))
         class_pool = ctx.enter_context(tc.tile_pool(name="class_pool", bufs=4))
-        sums = ctx.enter_context(tc.tile_pool(name="sums", bufs=5))
+        sums = ctx.enter_context(tc.tile_pool(name="sums", bufs=6))
         terms = ctx.enter_context(tc.tile_pool(name="terms", bufs=12))
         psum_c = ctx.enter_context(tc.psum_pool(name="psum_c", bufs=2))
         psum_t = ctx.enter_context(tc.psum_pool(name="psum_t", bufs=4))
@@ -133,7 +133,7 @@ def tile_causalwaveletfieldattentionbyte_pa_v_kernel(
 
         def regroup_x(s):
             x_grouped[s] = stage.tile([P, WIDTH, PACK], BF16, align_bytes=64, name="x_grouped")
-            copy, parts_of_x = (nc.scalar.copy, 1) if s in (0, 3) else (nc.vector.tensor_copy, 4)
+            copy, parts_of_x = (nc.scalar.copy, 1) if s != 1 else (nc.vector.tensor_copy, 4)
             for k in range(parts_of_x):
                 cols = slice(k * WIDTH // parts_of_x, (k + 1) * WIDTH // parts_of_x)
                 copy(
@@ -186,7 +186,6 @@ def tile_causalwaveletfieldattentionbyte_pa_v_kernel(
         taps = sorted(taps, key=lambda tap: tap[0])
         fine_taps = {tap[0]: tap for tap in taps if tap[0] % STRIDE != 0}
         band_taps = [tap for tap in taps if tap[0] % STRIDE == 0]
-        product_taps = [fine_taps[offset] for offset in (3, 6, 1, 2)]
         sum_taps = [fine_taps[offset] for offset in (4, 12)]
 
 
@@ -194,16 +193,16 @@ def tile_causalwaveletfieldattentionbyte_pa_v_kernel(
         band_of = {}
         used = 0
         with tc.tile_pool(name="rows_tiles", bufs=1) as rows_tiles:
+            rows = rows_tiles.tile([P, BAND_HEADS + 1, ROW], F32)
+            nc.gpsimd.memset(rows[:], 0.0)
+            for offset, table, row in band_taps:
+                nc.vector.tensor_copy(out=rows[:, 0:BAND_HEADS, P - 1 - offset // STRIDE], in_=table[:, row, 0:BAND_HEADS])
             for group in (slice(0, 2), slice(2, BAND_HEADS)):
                 heads = group.stop - group.start
                 pitch = (heads + 1) * ROW
-                rows = rows_tiles.tile([P, heads + 1, ROW], F32, name=f"rows{group.start}")
-                nc.gpsimd.memset(rows[:], 0.0)
-                for offset, table, row in band_taps:
-                    nc.vector.tensor_copy(out=rows[:, 0:heads, P - 1 - offset // STRIDE], in_=table[:, row, group])
                 nc.sync.dma_start(
                     out=scratch[used : used + P * pitch].rearrange("(p w) -> p w", w=pitch),
-                    in_=rows[:].rearrange("p h l -> p (h l)"),
+                    in_=rows[:, group.start : group.stop + 1, :].rearrange("p h l -> p (h l)"),
                 )
                 skewed = scratch[used + P - 1 : used + P - 1 + P * (pitch - 1)].rearrange("(p w) -> p w", w=pitch - 1)
                 band = keep.tile([P, heads, P], F32, name=f"band{group.start}")
@@ -214,6 +213,7 @@ def tile_causalwaveletfieldattentionbyte_pa_v_kernel(
                 for h in range(group.start, group.stop):
                     band_of[h] = band[:, h - group.start, :]
                 used += P * pitch
+
         more_terms = ctx.enter_context(tc.tile_pool(name="more_terms", bufs=4))
 
         def weight(tap, h):
@@ -228,7 +228,7 @@ def tile_causalwaveletfieldattentionbyte_pa_v_kernel(
                 nc.scalar.activation(out=out, in_=in_, func=ACT.Copy, scale=weight(tap, h))
 
         def make_product(h, tap, engine):
-            pool = more_terms if h >= 2 and tap == product_taps[-1] else terms
+            pool = more_terms if h >= 2 and tap[0] == 2 else terms
             product = pool.tile([P, STRIDE, CLASS_PITCH], F32, name="product")
             product_on(engine, product, h, tap)
             parts[h].append((product, tap[0]))
@@ -243,6 +243,14 @@ def tile_causalwaveletfieldattentionbyte_pa_v_kernel(
                 out=acc[h][:, :, 0:SHIFTED_COLS], in0=by_class[h][:, :, 1 : SHIFTED_COLS + 1], scalar=weight(sum_taps[1], h),
                 in1=acc[h][:, :, 0:SHIFTED_COLS], op0=ALU.mult, op1=ALU.add,
             )
+
+        def merge_three(h):
+            tile = parts[h][0][0]
+            for rows, source, q in ((slice(0, 6), slice(2, 8), 0), (slice(6, 8), slice(0, 2), 1)):
+                nc.vector.scalar_tensor_tensor(
+                    out=tile[:, rows, 0:SHIFTED_COLS], in0=by_class[h][:, source, q : q + SHIFTED_COLS],
+                    scalar=weight(fine_taps[3], h), in1=tile[:, rows, 0:SHIFTED_COLS], op0=ALU.mult, op1=ALU.add,
+                )
 
         def coarse_tap(h, tap):
             first = band_classes(h)
@@ -356,13 +364,18 @@ def tile_causalwaveletfieldattentionbyte_pa_v_kernel(
             multiplying = rnd >= 2
             if filtering:
                 first, second = heads_of(rnd)
-                for h in (first, second):
-                    for i, tap in enumerate(product_taps):
-                        make_product(h, tap, "vector" if rnd == 0 and i < 2 else "scalar")
-                    if rnd == 0:
+                if rnd == 0:
+                    for h in (first, second):
+                        for offset, engine in ((3, "vector"), (6, "vector"), (1, "scalar"), (2, "scalar")):
+                            make_product(h, fine_taps[offset], engine)
                         start_sum(h, "vector")
                         add_to_sum(h)
                         split_classes(2 + h)
+                else:
+                    for offset in (1, 2, 3, 6):
+                        make_product(first, fine_taps[offset], "scalar")
+                    for offset in (2, 6):
+                        make_product(second, fine_taps[offset], "scalar")
             if rnd == 0:
                 load_x(2)
                 load_x(3)
@@ -388,11 +401,12 @@ def tile_causalwaveletfieldattentionbyte_pa_v_kernel(
             for i in range(4):
                 if i == 0 and multiplying:
                     quantise_dv(rnd - 2, 0, PASSES)
-                if filtering and rnd > 0 and i == 0:
-                    start_sum(first, "vector")
                 if filtering and rnd > 0 and i == 1:
                     add_to_sum(first)
+                if filtering and rnd > 0 and i == 2:
                     add_to_sum(second)
+                if filtering and rnd > 0 and i == 3:
+                    merge_three(second)
                 if preparing and i >= 2:
                     h = 2 * (rnd + 1) + i - 2
                     if rnd > 0 and h not in by_class:
@@ -423,7 +437,9 @@ def tile_causalwaveletfieldattentionbyte_pa_v_kernel(
                 if preparing and i >= 2:
                     transpose_classes(2 * (rnd + 1) + i - 2)
                 if preparing and i == 3:
-                    start_sum(heads_of(rnd + 1)[1], "scalar")
+                    for h in heads_of(rnd + 1):
+                        start_sum(h, "scalar")
+                    make_product(heads_of(rnd + 1)[1], fine_taps[1], "scalar")
                 if rnd == 1 and i < 2:
                     quantise_x(1 - i)
                     regroup_x(3 - i)

@@ -44,7 +44,7 @@ def tile_causalwaveletfieldattentionbyte_pa_v_kernel(
     with ExitStack() as ctx:
         keep = ctx.enter_context(tc.tile_pool(name="keep", bufs=1))
         stage = ctx.enter_context(tc.tile_pool(name="stage", bufs=2))
-        heads_in = ctx.enter_context(tc.tile_pool(name="heads_in", bufs=5))
+        heads_in = ctx.enter_context(tc.tile_pool(name="heads_in", bufs=6))
         by_class_pool = ctx.enter_context(tc.tile_pool(name="by_class", bufs=5))
         class_pool = ctx.enter_context(tc.tile_pool(name="class_pool", bufs=4))
         sums = ctx.enter_context(tc.tile_pool(name="sums", bufs=6))
@@ -87,8 +87,8 @@ def tile_causalwaveletfieldattentionbyte_pa_v_kernel(
         nc.sync.dma_start(
             out=kmag[:].rearrange("p b r h -> p b (r h)"), in_=k_mag.rearrange("b (q r) h -> q b (r h)", r=STRIDE)
         )
-        load_order = [2, 3, 12, 13, 14, 15, 4, 5, 6, 7, 8, 9, 10, 11]
-        for h in load_order[:4]:
+        load_order = [2, 3, 4, 5, 12, 13, 6, 7, 14, 15, 8, 9, 10, 11]
+        for h in load_order[:6]:
             load_head(h)
 
         identity = keep.tile([P, P], F32)
@@ -133,7 +133,7 @@ def tile_causalwaveletfieldattentionbyte_pa_v_kernel(
 
         def regroup_x(s):
             x_grouped[s] = stage.tile([P, WIDTH, PACK], BF16, align_bytes=64, name="x_grouped")
-            copy, parts_of_x = (nc.scalar.copy, 1) if s != 1 else (nc.vector.tensor_copy, 4)
+            copy, parts_of_x = (nc.scalar.copy, 1) if s in (0, 3) else (nc.vector.tensor_copy, 4)
             for k in range(parts_of_x):
                 cols = slice(k * WIDTH // parts_of_x, (k + 1) * WIDTH // parts_of_x)
                 copy(
@@ -295,12 +295,13 @@ def tile_causalwaveletfieldattentionbyte_pa_v_kernel(
             add_transposes(h, g, half, not banded(h, g, half), True)
 
         def scale(h, g):
-            if h // 2 not in dv_grouped:
-                dv_grouped[h // 2] = stage.tile([P, PASSES, P, PACK], BF16, align_bytes=64, name="dv_grouped")
-            first = h % 2 * HEAD_DIM
+            pair = pair_of[h]
+            if pair not in dv_grouped:
+                dv_grouped[pair] = stage.tile([P, PASSES, P, PACK], BF16, align_bytes=64, name="dv_grouped")
+            first = pairs[pair].index(h) * HEAD_DIM
             kmag_g = kmag[:, :, PACK * g : PACK * (g + 1), h]
             nc.vector.tensor_tensor(
-                out=dv_grouped[h // 2][:, BATCH * g : BATCH * (g + 1), first : first + HEAD_DIM, :],
+                out=dv_grouped[pair][:, BATCH * g : BATCH * (g + 1), first : first + HEAD_DIM, :],
                 in0=turned[h, g][:].rearrange("p t (b c) -> p b c t", b=BATCH),
                 in1=kmag_g.unsqueeze(2).to_broadcast([P, BATCH, HEAD_DIM, PACK]),
                 op=ALU.mult,
@@ -336,10 +337,20 @@ def tile_causalwaveletfieldattentionbyte_pa_v_kernel(
         def store(pair, half, copy):
             cols = slice(half * N_TILE, (half + 1) * N_TILE)
             copy(out=result[pair][:, cols], in_=products[pair, half][:])
-            nc.sync.dma_start(out=out[pair * P : (pair + 1) * P, cols], in_=result[pair][:, cols])
+            for k, h in enumerate(pairs[pair]):
+                nc.sync.dma_start(
+                    out=out[h * HEAD_DIM : (h + 1) * HEAD_DIM, cols],
+                    in_=result[pair][k * HEAD_DIM : (k + 1) * HEAD_DIM, cols],
+                )
+
+        mixed = HEADS - BAND_HEADS + 1
+        plain_heads = HEADS - 2 * mixed
+        pairs = [(h, h + 1) for h in range(0, plain_heads, 2)]
+        pairs += [(plain_heads + k, plain_heads + mixed + k) for k in range(mixed)]
+        pair_of = {h: p for p, heads in enumerate(pairs) for h in heads}
 
         def heads_of(pair):
-            return (2 * pair, 2 * pair + 1)
+            return pairs[pair]
 
         PAIRS = HEADS // 2
         parts = {h: [] for h in range(HEADS)}
@@ -352,7 +363,13 @@ def tile_causalwaveletfieldattentionbyte_pa_v_kernel(
         result = {}
         products = {}
         late = [h for h in range(HEADS) if band_classes(h) < STRIDE]
-        background = [(h, tap) for i in range(0, len(late), 2) for tap in band_taps for h in late[i : i + 2]]
+        background = []
+        for i in range(0, len(late), 2):
+            order = sorted((k if h == late[i] else 2 * k + 1, h) for h in late[i : i + 2] for k in range(len(band_taps)))
+            taken = {h: 0 for h in late}
+            for key, h in order:
+                background.append((h, band_taps[taken[h]]))
+                taken[h] += 1
         chunk = -(-len(background) // (PAIRS - 1))
 
         ctx.enter_context(tc.manual_schedule(engines={mybir.EngineType.PE, mybir.EngineType.DVE}))
@@ -370,7 +387,7 @@ def tile_causalwaveletfieldattentionbyte_pa_v_kernel(
                             make_product(h, fine_taps[offset], engine)
                         start_sum(h, "vector")
                         add_to_sum(h)
-                        split_classes(2 + h)
+                        split_classes(heads_of(1)[h])
                 else:
                     for offset in (1, 2, 3, 6):
                         make_product(first, fine_taps[offset], "scalar")
@@ -379,18 +396,19 @@ def tile_causalwaveletfieldattentionbyte_pa_v_kernel(
             if rnd == 0:
                 load_x(2)
                 load_x(3)
-                for h in load_order[4:6]:
-                    load_head(h)
             for h in load_order[6 + 2 * rnd : 8 + 2 * rnd]:
                 load_head(h)
             work = background[chunk * (rnd - 1) : chunk * rnd] if rnd else []
             steps = [work[len(work) * i // 4 : len(work) * (i + 1) // 4] for i in range(4)]
-            turns = [(h, g) for h in heads_of(rnd - 1) for g in range(PASSES_PER_BATCH)]
-            if last:
-                turns = [(h, g) for g in range(PASSES_PER_BATCH) for h in heads_of(rnd - 1)]
-            mx = [[], [(0, 0)], [(0, 2)], [(1, 0)], [(1, 2)]]
-            if last:
-                mx = [[], [(0, 0), (0, 2)], [(1, 0), (1, 2)], [], []]
+            turns = [(h, g) for g in range(PASSES_PER_BATCH) for h in heads_of(rnd - 1)] if turning else []
+            if rnd == 2:
+                mx = {8: [(0, 0), (0, 2), (1, 0), (1, 2)]}
+            elif rnd == 3:
+                mx = {5: [(0, 0)], 6: [(0, 2)], 7: [(1, 0)], 8: [(1, 2)]}
+            elif rnd > plain_heads // 2:
+                mx = {4: [(0, 0)], 6: [(0, 2)], 7: [(1, 0)], 8: [(1, 2)]}
+            else:
+                mx = {3: [(0, 0)], 5: [(0, 2)], 7: [(1, 0)], 8: [(1, 2)]}
 
             def multiply_and_store(steps):
                 for half, first_pass in steps:
@@ -401,26 +419,26 @@ def tile_causalwaveletfieldattentionbyte_pa_v_kernel(
             for i in range(4):
                 if i == 0 and multiplying:
                     quantise_dv(rnd - 2, 0, PASSES)
+                for step in steps[i][:1]:
+                    coarse_tap(*step)
                 if filtering and rnd > 0 and i == 1:
                     add_to_sum(first)
                 if filtering and rnd > 0 and i == 2:
                     add_to_sum(second)
                 if filtering and rnd > 0 and i == 3:
                     merge_three(second)
-                if preparing and i >= 2:
-                    h = 2 * (rnd + 1) + i - 2
-                    if rnd > 0 and h not in by_class:
-                        split_classes(h)
-                for step in steps[i]:
+                if preparing and rnd > 0 and i < 2 and heads_of(rnd + 1)[i] not in by_class:
+                    split_classes(heads_of(rnd + 1)[i])
+                for step in steps[i][1:]:
                     coarse_tap(*step)
                 if rnd == 1:
                     add_bands(*turns[i], 0, False)
                     add_bands(*turns[i], 1, False)
                 elif turning:
-                    turn(*turns[i], 0)
-                    if multiplying:
-                        multiply_and_store(mx[i])
-                    turn(*turns[i], 1)
+                    for half in range(2):
+                        if multiplying:
+                            multiply_and_store(mx.get(2 * i + half, []))
+                        turn(*turns[i], half)
                 if rnd == 0 and i >= 2:
                     for g in range(PASSES_PER_BATCH):
                         turned[i - 2, g] = psum_t.tile([P, PACK, P], F32, name="turned")
@@ -431,11 +449,12 @@ def tile_causalwaveletfieldattentionbyte_pa_v_kernel(
                 if last and i == 1:
                     quantise_dv(PAIRS - 1, 0, 2)
                 if multiplying and i == 3:
-                    multiply_and_store(mx[4])
-                if rnd < 2 and i >= 2:
-                    split_classes(late[2 * rnd + i - 2])
-                if preparing and i >= 2:
-                    transpose_classes(2 * (rnd + 1) + i - 2)
+                    multiply_and_store(mx.get(8, []))
+                if rnd in (0, 2) and i >= 2:
+                    split_classes(late[rnd + i - 2])
+                first_turn = 2 if rnd == 0 else 1
+                if preparing and 0 <= i - first_turn < 2:
+                    transpose_classes(heads_of(rnd + 1)[i - first_turn])
                 if preparing and i == 3:
                     for h in heads_of(rnd + 1):
                         start_sum(h, "scalar")
@@ -443,10 +462,8 @@ def tile_causalwaveletfieldattentionbyte_pa_v_kernel(
                 if rnd == 1 and i < 2:
                     quantise_x(1 - i)
                     regroup_x(3 - i)
-                if rnd == 1 and i == 3:
-                    quantise_x(3)
-                if rnd == 2 and i == 0:
-                    quantise_x(2)
+                if rnd == 2 and 1 <= i <= 2:
+                    quantise_x(4 - i)
         multiply(PAIRS - 1, 0, 0)
         multiply(PAIRS - 1, 1, 0)
         quantise_dv(PAIRS - 1, 2, 4)

from contextlib import ExitStack

import concourse.mybir as mybir
from concourse.masks import make_identity

F32 = mybir.dt.float32
BF16 = mybir.dt.bfloat16
U32 = mybir.dt.uint32
U8 = mybir.dt.uint8
E4M3X4 = mybir.dt.float8_e4m3fn_x4
E5M2X4 = mybir.dt.float8_e5m2_x4
ALU = mybir.AluOpType
ACT = mybir.ActivationFunctionType
AXIS = mybir.AxisListType

P = 128
PACK = 4
K_PASS = P * PACK
BATCH, TOKENS, WIDTH, CHANNELS, HEADS, SCALES = 2, 1024, 1024, 1024, 16, 10
HEAD_DIM = CHANNELS // HEADS
PASSES = BATCH * TOKENS // K_PASS
PASSES_PER_BATCH = TOKENS // K_PASS
N_TILE = 512
STRIDE = 8
CLASS_TOKENS = TOKENS // STRIDE
MX_FLOPS = 2 * CHANNELS * BATCH * TOKENS * WIDTH
BAND_UNITS = MX_FLOPS // 10 // (2 * P * P * P)
BAND_HEADS = -(-BAND_UNITS // STRIDE)
ROW = 2 * P
ZERO_PAD = 32
CLASS_COLS = (TOKENS + ZERO_PAD) // STRIDE
CLASS_PITCH = 136
SHIFTED_COLS = P + 1
TAP0, TAP1, TAP2, TAP3 = 0.4829629131445341, 0.8365163037378079, 0.2241438680420134, -0.1294095225512604

FLOPS = 2 * CHANNELS * BATCH * TOKENS * WIDTH + 2 * 20 * CHANNELS * BATCH * TOKENS
BYTES = 2 * 2 * BATCH * TOKENS * WIDTH + 4 * BATCH * TOKENS * HEADS + 2 * SCALES * HEADS + 4 * CHANNELS * WIDTH


def tile_causalwaveletfieldattentionbyte_pa_v_kernel(
    tc, x, k_w, k_b, v_w, v_b, scale_gain, k_mag, grad_out, out
):
    nc = tc.nc
    with ExitStack() as ctx:
        keep = ctx.enter_context(tc.tile_pool(name="keep", bufs=1))
        stage = ctx.enter_context(tc.tile_pool(name="stage", bufs=2))
        heads_in = ctx.enter_context(tc.tile_pool(name="heads_in", bufs=6))
        by_class_pool = ctx.enter_context(tc.tile_pool(name="by_class", bufs=5))
        class_pool = ctx.enter_context(tc.tile_pool(name="class_pool", bufs=4))
        sums = ctx.enter_context(tc.tile_pool(name="sums", bufs=6))
        terms = ctx.enter_context(tc.tile_pool(name="terms", bufs=12))
        psum_c = ctx.enter_context(tc.psum_pool(name="psum_c", bufs=2))
        psum_t = ctx.enter_context(tc.psum_pool(name="psum_t", bufs=4))
        psum_o = ctx.enter_context(tc.psum_pool(name="psum_o", bufs=2))

        logits = keep.tile([P, SCALES, HEADS], BF16)
        nc.sync.dma_start(
            out=logits[:].rearrange("p j h -> p (j h)"), in_=scale_gain.rearrange("j h -> (j h)").partition_broadcast(P)
        )
        warm = keep.tile([P, 1], F32)
        nc.vector.memset(warm[:], 0.0)
        nc.scalar.activation(out=warm[:], in_=warm[:], func=ACT.Exp)

        grad = {}

        def load_head(h):
            grad[h] = heads_in.tile([P, TOKENS + ZERO_PAD], BF16, name="grad_head")
            nc.gpsimd.memset(grad[h][:, TOKENS:], 0.0)
            for b in range(BATCH):
                nc.sync.dma_start(
                    out=grad[h][b * HEAD_DIM : (b + 1) * HEAD_DIM, 0:TOKENS],
                    in_=grad_out[b, h * HEAD_DIM : (h + 1) * HEAD_DIM, :],
                )

        x_rows = x.rearrange("b (q g t) i -> b g q t i", g=PASSES_PER_BATCH, t=PACK)
        x_raw = {}

        def load_x(s):
            x_raw[s] = stage.tile([P, PACK, WIDTH], BF16, name="x_raw")
            nc.sync.dma_start(out=x_raw[s][:], in_=x_rows[s % BATCH, s // BATCH])

        load_head(0)
        load_head(1)
        load_x(0)
        load_x(1)
        kmag = keep.tile([P, BATCH, STRIDE, HEADS], F32)
        nc.sync.dma_start(
            out=kmag[:].rearrange("p b r h -> p b (r h)"), in_=k_mag.rearrange("b (q r) h -> q b (r h)", r=STRIDE)
        )
        load_order = [2, 3, 4, 5, 12, 13, 6, 7, 14, 15, 8, 9, 10, 11]
        for h in load_order[:6]:
            load_head(h)

        identity = keep.tile([P, P], F32)
        make_identity(nc, identity[:])
        identity_bf = keep.tile([P, P], BF16)
        make_identity(nc, identity_bf[:])

        by_class = {}
        classes = {}

        def band_classes(h):
            return min(max(BAND_UNITS - STRIDE * h, 0), STRIDE)

        def split_classes(h):
            tile = keep.tile([P, STRIDE, CLASS_PITCH], BF16, name=f"late{h}") if band_classes(h) < STRIDE else (
                by_class_pool.tile([P, STRIDE, CLASS_PITCH], BF16, name="by_class")
            )
            by_class[h] = tile
            nc.vector.tensor_copy(
                out=tile[:, :, 0:CLASS_COLS].rearrange("p (a r) (q i) -> p a q r i", a=2, i=4),
                in_=grad[h][:].rearrange("p (q i a r) -> p a q r i", i=4, a=2, r=STRIDE // 2),
            )

        def transpose_classes(h):
            count = band_classes(h)
            if count == 0:
                return
            classes_ps = psum_c.tile([P, STRIDE, P], BF16, name="classes_ps")
            for r in range(count):
                nc.tensor.transpose(classes_ps[:, r, :], by_class[h][:, r, 0:P], identity_bf[:])
            classes[h] = class_pool.tile([P, STRIDE, P], F32, name="classes")
            nc.scalar.copy(out=classes[h][:, 0:count, :], in_=classes_ps[:, 0:count, :])

        for h in (0, 1):
            split_classes(h)
            transpose_classes(h)

        x_codes = keep.tile([P, PASSES, WIDTH], U32, align_bytes=64)
        x_scales = keep.tile([P, PASSES, WIDTH], U8, align_bytes=64)

        x_grouped = {}

        def regroup_x(s):
            x_grouped[s] = stage.tile([P, WIDTH, PACK], BF16, align_bytes=64, name="x_grouped")
            copy, parts_of_x = (nc.scalar.copy, 1) if s in (0, 3) else (nc.vector.tensor_copy, 4)
            for k in range(parts_of_x):
                cols = slice(k * WIDTH // parts_of_x, (k + 1) * WIDTH // parts_of_x)
                copy(
                    out=x_grouped[s][:, cols, :].rearrange("p (c i) t -> p c t i", i=4),
                    in_=x_raw[s][:, :, cols].rearrange("p t (c i) -> p c t i", i=4),
                )

        def quantise_x(s):
            nc.vector.quantize_mx(
                out=x_codes[:, s, :].bitcast(E4M3X4),
                scales=x_scales[:, s, :],
                in_=x_grouped[s][:].rearrange("p c t -> p (c t)"),
            )

        regroup_x(0)
        regroup_x(1)

        top = keep.tile([P, HEADS], F32)
        nc.vector.tensor_reduce(out=top[:], in_=logits[:].rearrange("p j h -> p h j"), axis=AXIS.X, op=ALU.max)
        shifted = keep.tile([P, SCALES, HEADS], F32)
        nc.vector.tensor_tensor(
            out=shifted[:], in0=logits[:], in1=top[:].unsqueeze(1).to_broadcast([P, SCALES, HEADS]), op=ALU.subtract
        )
        grown = keep.tile([P, SCALES, HEADS], F32)
        nc.scalar.activation(out=grown[:], in_=shifted[:], func=ACT.Exp)
        total = keep.tile([P, 1, HEADS], F32)
        nc.vector.tensor_reduce(out=total[:, 0, :], in_=grown[:].rearrange("p j h -> p h j"), axis=AXIS.X, op=ALU.add)
        inverse = keep.tile([P, 1, HEADS], F32)
        nc.vector.reciprocal(out=inverse[:], in_=total[:])
        inverse_of_all = inverse[:].to_broadcast([P, SCALES, HEADS])
        w_tri = keep.tile([P, SCALES, HEADS], F32)
        nc.vector.scalar_tensor_tensor(
            out=w_tri[:], in0=grown[:], scalar=TAP0, in1=inverse_of_all, op0=ALU.mult, op1=ALU.mult
        )
        w_pow = keep.tile([P, SCALES, HEADS], F32)
        nc.vector.tensor_scalar_mul(out=w_pow[:], in0=grown[:], scalar1=TAP2)
        nc.vector.scalar_tensor_tensor(
            out=w_pow[:, 1:, :], in0=grown[:, : SCALES - 1, :], scalar=TAP1, in1=w_pow[:, 1:, :],
            op0=ALU.mult, op1=ALU.add,
        )
        nc.vector.tensor_tensor(out=w_pow[:], in0=w_pow[:], in1=inverse_of_all, op=ALU.mult)
        w_zero = keep.tile([P, 1, HEADS], F32)
        nc.vector.scalar_tensor_tensor(
            out=w_zero[:], in0=total[:], scalar=TAP3, in1=inverse[:], op0=ALU.mult, op1=ALU.mult
        )

        taps = [(0, w_zero, 0)]
        taps += [(2**m, w_pow, m) for m in range(SCALES)]
        taps += [(3 * 2**j, w_tri, j) for j in range(SCALES) if 3 * 2**j < TOKENS]
        taps = sorted(taps, key=lambda tap: tap[0])
        fine_taps = {tap[0]: tap for tap in taps if tap[0] % STRIDE != 0}
        band_taps = [tap for tap in taps if tap[0] % STRIDE == 0]
        sum_taps = [fine_taps[offset] for offset in (4, 12)]


        scratch = out.rearrange("c i -> (c i)")
        band_of = {}
        used = 0
        with tc.tile_pool(name="rows_tiles", bufs=1) as rows_tiles:
            rows = rows_tiles.tile([P, BAND_HEADS + 1, ROW], F32)
            nc.gpsimd.memset(rows[:], 0.0)
            for offset, table, row in band_taps:
                nc.vector.tensor_copy(out=rows[:, 0:BAND_HEADS, P - 1 - offset // STRIDE], in_=table[:, row, 0:BAND_HEADS])
            for group in (slice(0, 2), slice(2, BAND_HEADS)):
                heads = group.stop - group.start
                pitch = (heads + 1) * ROW
                nc.sync.dma_start(
                    out=scratch[used : used + P * pitch].rearrange("(p w) -> p w", w=pitch),
                    in_=rows[:, group.start : group.stop + 1, :].rearrange("p h l -> p (h l)"),
                )
                skewed = scratch[used + P - 1 : used + P - 1 + P * (pitch - 1)].rearrange("(p w) -> p w", w=pitch - 1)
                band = keep.tile([P, heads, P], F32, name=f"band{group.start}")
                nc.sync.dma_start(
                    out=band[:],
                    in_=skewed[:, 0 : heads * ROW].rearrange("p (h l) -> p h l", l=ROW)[:, :, 0:P],
                )
                for h in range(group.start, group.stop):
                    band_of[h] = band[:, h - group.start, :]
                used += P * pitch

        more_terms = ctx.enter_context(tc.tile_pool(name="more_terms", bufs=4))

        def weight(tap, h):
            offset, table, row = tap
            return table[:, row, h : h + 1]

        def product_on(engine, tile, h, tap):
            out, in_ = tile[:, :, 0:SHIFTED_COLS], by_class[h][:, :, 0:SHIFTED_COLS]
            if engine == "vector":
                nc.vector.tensor_scalar_mul(out=out, in0=in_, scalar1=weight(tap, h))
            else:
                nc.scalar.activation(out=out, in_=in_, func=ACT.Copy, scale=weight(tap, h))

        def make_product(h, tap, engine):
            pool = more_terms if h >= 2 and tap[0] == 2 else terms
            product = pool.tile([P, STRIDE, CLASS_PITCH], F32, name="product")
            product_on(engine, product, h, tap)
            parts[h].append((product, tap[0]))

        def start_sum(h, engine):
            acc[h] = sums.tile([P, STRIDE, CLASS_PITCH], F32, name="acc")
            product_on(engine, acc[h], h, sum_taps[0])

        def add_to_sum(h):
            parts[h].append((acc[h], sum_taps[0][0]))
            nc.vector.scalar_tensor_tensor(
                out=acc[h][:, :, 0:SHIFTED_COLS], in0=by_class[h][:, :, 1 : SHIFTED_COLS + 1], scalar=weight(sum_taps[1], h),
                in1=acc[h][:, :, 0:SHIFTED_COLS], op0=ALU.mult, op1=ALU.add,
            )

        def merge_three(h):
            tile = parts[h][0][0]
            for rows, source, q in ((slice(0, 6), slice(2, 8), 0), (slice(6, 8), slice(0, 2), 1)):
                nc.vector.scalar_tensor_tensor(
                    out=tile[:, rows, 0:SHIFTED_COLS], in0=by_class[h][:, source, q : q + SHIFTED_COLS],
                    scalar=weight(fine_taps[3], h), in1=tile[:, rows, 0:SHIFTED_COLS], op0=ALU.mult, op1=ALU.add,
                )

        def coarse_tap(h, tap):
            first = band_classes(h)
            k = tap[0] // STRIDE
            if k == 0:
                coarse[h] = keep.tile([P, STRIDE - first, P], F32, name=f"coarse{h}")
                nc.vector.tensor_scalar_mul(out=coarse[h][:], in0=by_class[h][:, first:STRIDE, 0:P], scalar1=weight(tap, h))
            else:
                nc.vector.scalar_tensor_tensor(
                    out=coarse[h][:, :, 0 : P - k], in0=by_class[h][:, first:STRIDE, k:P], scalar=weight(tap, h),
                    in1=coarse[h][:, :, 0 : P - k], op0=ALU.mult, op1=ALU.add,
                )

        def banded(h, g, half):
            return PACK * g + 2 * half < band_classes(h)

        def add_bands(h, g, half, opens):
            if banded(h, g, half):
                cols = slice(2 * half, 2 * half + 2)
                rows = slice(PACK * g + 2 * half, PACK * g + 2 * half + 2)
                nc.tensor.matmul(
                    out=turned[h, g][:, cols, :].rearrange("p t c -> p (t c)"), lhsT=band_of[h],
                    rhs=classes[h][:, rows, :].rearrange("p t c -> p (t c)"), start=opens, stop=not opens and half == 1,
                )

        def add_transposes(h, g, half, opens, closes):
            for t in (2 * half, 2 * half + 1):
                r = PACK * g + t
                tiles = [(part, (r + offset) % STRIDE, (r + offset) // STRIDE) for part, offset in parts[h]]
                if not banded(h, g, half):
                    tiles.append((coarse[h], r - band_classes(h), 0))
                for i, (part, row, q) in enumerate(tiles):
                    nc.tensor.matmul(
                        out=turned[h, g][:, t, :], lhsT=part[:, row, q : q + P], rhs=identity[:], is_transpose=True,
                        start=opens and i == 0 and t % 2 == 0, stop=closes and i == len(tiles) - 1 and t % 2 == 1,
                    )

        def turn(h, g, half):
            if half == 0:
                turned[h, g] = psum_t.tile([P, PACK, P], F32, name="turned")
            add_bands(h, g, half, True)
            add_transposes(h, g, half, not banded(h, g, half), True)

        def scale(h, g):
            pair = pair_of[h]
            if pair not in dv_grouped:
                dv_grouped[pair] = stage.tile([P, PASSES, P, PACK], BF16, align_bytes=64, name="dv_grouped")
            first = pairs[pair].index(h) * HEAD_DIM
            kmag_g = kmag[:, :, PACK * g : PACK * (g + 1), h]
            nc.vector.tensor_tensor(
                out=dv_grouped[pair][:, BATCH * g : BATCH * (g + 1), first : first + HEAD_DIM, :],
                in0=turned[h, g][:].rearrange("p t (b c) -> p b c t", b=BATCH),
                in1=kmag_g.unsqueeze(2).to_broadcast([P, BATCH, HEAD_DIM, PACK]),
                op=ALU.mult,
            )

        def quantise_dv(pair, first, last):
            if first == 0:
                dv_codes[pair] = stage.tile([P, PASSES * P], U32, align_bytes=64, name="dv_codes")
                dv_scales[pair] = stage.tile([P, PASSES * P], U8, align_bytes=64, name="dv_scales")
            cols = slice(first * P, last * P)
            nc.vector.quantize_mx(
                out=dv_codes[pair][:, cols].bitcast(E5M2X4), scales=dv_scales[pair][:, cols],
                in_=dv_grouped[pair][:, first:last, :, :].rearrange("p s c t -> p (s c t)"),
            )

        def multiply(pair, half, first):
            if first == 0 and half == 0:
                result[pair] = stage.tile([P, WIDTH], F32, name="result")
            if first == 0:
                products[pair, half] = psum_o.tile([P, N_TILE], F32, name="product")
            cols = slice(half * N_TILE, (half + 1) * N_TILE)
            for s in (first, first + 1):
                nc.tensor.matmul_mx(
                    out=products[pair, half][:],
                    lhsT=dv_codes[pair][:, s * P : (s + 1) * P].bitcast(E5M2X4),
                    lhsT_scale=dv_scales[pair][:, s * P : (s + 1) * P],
                    rhs=x_codes[:, s, cols].bitcast(E4M3X4),
                    rhs_scale=x_scales[:, s, cols],
                    start=(s == 0),
                    stop=(s == PASSES - 1),
                )

        def store(pair, half, copy):
            cols = slice(half * N_TILE, (half + 1) * N_TILE)
            copy(out=result[pair][:, cols], in_=products[pair, half][:])
            for k, h in enumerate(pairs[pair]):
                nc.sync.dma_start(
                    out=out[h * HEAD_DIM : (h + 1) * HEAD_DIM, cols],
                    in_=result[pair][k * HEAD_DIM : (k + 1) * HEAD_DIM, cols],
                )

        mixed = HEADS - BAND_HEADS + 1
        plain_heads = HEADS - 2 * mixed
        pairs = [(h, h + 1) for h in range(0, plain_heads, 2)]
        pairs += [(plain_heads + k, plain_heads + mixed + k) for k in range(mixed)]
        pair_of = {h: p for p, heads in enumerate(pairs) for h in heads}

        def heads_of(pair):
            return pairs[pair]

        PAIRS = HEADS // 2
        parts = {h: [] for h in range(HEADS)}
        acc = {}
        coarse = {}
        turned = {}
        dv_grouped = {}
        dv_codes = {}
        dv_scales = {}
        result = {}
        products = {}
        late = [h for h in range(HEADS) if band_classes(h) < STRIDE]
        background = []
        for i in range(0, len(late), 2):
            order = sorted((k if h == late[i] else 2 * k + 1, h) for h in late[i : i + 2] for k in range(len(band_taps)))
            taken = {h: 0 for h in late}
            for key, h in order:
                background.append((h, band_taps[taken[h]]))
                taken[h] += 1
        chunk = -(-len(background) // (PAIRS - 1))

        ctx.enter_context(tc.manual_schedule(engines={mybir.EngineType.PE, mybir.EngineType.DVE}))
        for rnd in range(PAIRS + 1):
            filtering = rnd < PAIRS
            preparing = rnd + 1 < PAIRS
            turning = rnd >= 1
            last = rnd == PAIRS
            multiplying = rnd >= 2
            if filtering:
                first, second = heads_of(rnd)
                if rnd == 0:
                    for h in (first, second):
                        for offset, engine in ((3, "vector"), (6, "vector"), (1, "scalar"), (2, "scalar")):
                            make_product(h, fine_taps[offset], engine)
                        start_sum(h, "vector")
                        add_to_sum(h)
                        split_classes(heads_of(1)[h])
                else:
                    for offset in (1, 2, 3, 6):
                        make_product(first, fine_taps[offset], "scalar")
                    for offset in (2, 6):
                        make_product(second, fine_taps[offset], "scalar")
            if rnd == 0:
                load_x(2)
                load_x(3)
            for h in load_order[6 + 2 * rnd : 8 + 2 * rnd]:
                load_head(h)
            work = background[chunk * (rnd - 1) : chunk * rnd] if rnd else []
            steps = [work[len(work) * i // 4 : len(work) * (i + 1) // 4] for i in range(4)]
            turns = [(h, g) for g in range(PASSES_PER_BATCH) for h in heads_of(rnd - 1)] if turning else []
            if rnd == 2:
                mx = {8: [(0, 0), (0, 2), (1, 0), (1, 2)]}
            elif rnd == 3:
                mx = {5: [(0, 0)], 6: [(0, 2)], 7: [(1, 0)], 8: [(1, 2)]}
            elif rnd > plain_heads // 2:
                mx = {4: [(0, 0)], 6: [(0, 2)], 7: [(1, 0)], 8: [(1, 2)]}
            else:
                mx = {3: [(0, 0)], 5: [(0, 2)], 7: [(1, 0)], 8: [(1, 2)]}

            def multiply_and_store(steps):
                for half, first_pass in steps:
                    multiply(rnd - 2, half, first_pass)
                    if first_pass == 2:
                        store(rnd - 2, half, nc.scalar.copy)

            for i in range(4):
                if i == 0 and multiplying:
                    quantise_dv(rnd - 2, 0, PASSES)
                for step in steps[i][:1]:
                    coarse_tap(*step)
                if filtering and rnd > 0 and i == 1:
                    add_to_sum(first)
                if filtering and rnd > 0 and i == 2:
                    add_to_sum(second)
                if filtering and rnd > 0 and i == 3:
                    merge_three(second)
                if preparing and rnd > 0 and i < 2 and heads_of(rnd + 1)[i] not in by_class:
                    split_classes(heads_of(rnd + 1)[i])
                for step in steps[i][1:]:
                    coarse_tap(*step)
                if rnd == 1:
                    add_bands(*turns[i], 0, False)
                    add_bands(*turns[i], 1, False)
                elif turning:
                    for half in range(2):
                        if multiplying:
                            multiply_and_store(mx.get(2 * i + half, []))
                        turn(*turns[i], half)
                if rnd == 0 and i >= 2:
                    for g in range(PASSES_PER_BATCH):
                        turned[i - 2, g] = psum_t.tile([P, PACK, P], F32, name="turned")
                        add_transposes(i - 2, g, 0, True, False)
                        add_transposes(i - 2, g, 1, False, False)
                for ready in ([], [], turns[0:2], turns[2:4])[i] if rnd == 1 else turns[i : i + 1] if turning else []:
                    scale(*ready)
                if last and i == 1:
                    quantise_dv(PAIRS - 1, 0, 2)
                if multiplying and i == 3:
                    multiply_and_store(mx.get(8, []))
                if rnd in (0, 2) and i >= 2:
                    split_classes(late[rnd + i - 2])
                first_turn = 2 if rnd == 0 else 1
                if preparing and 0 <= i - first_turn < 2:
                    transpose_classes(heads_of(rnd + 1)[i - first_turn])
                if preparing and i == 3:
                    for h in heads_of(rnd + 1):
                        start_sum(h, "scalar")
                    make_product(heads_of(rnd + 1)[1], fine_taps[1], "scalar")
                if rnd == 1 and i < 2:
                    quantise_x(1 - i)
                    regroup_x(3 - i)
                if rnd == 2 and 1 <= i <= 2:
                    quantise_x(4 - i)
        multiply(PAIRS - 1, 0, 0)
        multiply(PAIRS - 1, 1, 0)
        quantise_dv(PAIRS - 1, 2, 4)
        multiply(PAIRS - 1, 0, 2)
        store(PAIRS - 1, 0, nc.scalar.copy)
        multiply(PAIRS - 1, 1, 2)
        store(PAIRS - 1, 1, nc.vector.tensor_copy)
